import numpy as np
import ml_dtypes


def mxq(x, axis, fmt="e4m3"):
    dtype, down = {"e4m3": (ml_dtypes.float8_e4m3fn, 7), "e5m2": (ml_dtypes.float8_e5m2, 14)}[fmt]
    v = np.moveaxis(np.asarray(x, np.float32).astype(ml_dtypes.bfloat16).astype(np.float64), axis, -1)
    blocks = v.reshape(v.shape[:-1] + (-1, 32))
    amax = np.abs(blocks).max(-1, keepdims=True)
    byte = np.maximum(np.where(amax > 0, np.frexp(amax)[1] - 1 + 127, 0) - down, 1)
    scale = np.exp2(byte - 127.0)
    codes = (blocks / scale).astype(np.float32).astype(dtype).astype(np.float64)
    return np.moveaxis((codes * scale).reshape(v.shape), -1, axis)


WIDE = False


def mx_kscale(k):
    if not WIDE:
        return np.ones(k)
    levels = np.array([10, -10, 5, -5, 0])
    a = np.random.permutation(np.resize(levels, k // 512 * 4)).reshape(k // 512, 4)
    idx = np.arange(k)
    return np.exp2(a[idx // 512, idx % 128 // 32])


BF16 = ml_dtypes.bfloat16


def bf(x):
    return np.asarray(x, np.float32).astype(BF16)


def f64(x):
    return np.asarray(x).astype(np.float64)


B, S, D, DV, DK = 8, 512, 512, 1024, 128
DROPOUT_P = 0.1
KEEP = 1.0 - DROPOUT_P


def setup_inputs():
    s = mx_kscale(D)
    return {
        "q": bf(np.random.standard_normal((B, S, DK)) * 2.0 / DK ** 0.25),
        "k": bf(np.random.standard_normal((B, S, DK)) * 2.0 / DK ** 0.25),
        "x3": bf(np.random.standard_normal((B, S, D)) * s),
        "Wv": bf(np.random.standard_normal((DV, D)) / np.sqrt(D) / s),
        "bv": bf(np.random.standard_normal(DV) * 0.1),
        "inv_scale": bf(np.random.uniform(size=(S, S)) + 1.0),
        "dropout_mask": bf((np.random.uniform(size=(B, S, S)) < KEEP) / KEEP),
    }


def reference(q, k, x3, Wv, bv, inv_scale, dropout_mask):
    v = (mxq(f64(x3), 2, "e4m3") @ mxq(f64(Wv), 1, "e4m3").T) + f64(bv)
    attn = f64(q) @ f64(k).transpose(0, 2, 1)
    scaled = attn / f64(inv_scale)
    e = np.exp(scaled - scaled.max(-1, keepdims=True))
    pe = e * f64(dropout_mask)
    return (mxq(pe, 2, "e4m3") @ mxq(v, 1, "e4m3")) / e.sum(-1, keepdims=True)

@@ -1,0 +1,236 @@
+from contextlib import ExitStack
+
+import concourse.mybir as mybir
+from concourse.masks import make_identity
+
+F32 = mybir.dt.float32
+BF16 = mybir.dt.bfloat16
+U32 = mybir.dt.uint32
+U8 = mybir.dt.uint8
+FP8X4 = mybir.dt.float8_e4m3fn_x4
+ALU = mybir.AluOpType
+ACT = mybir.ActivationFunctionType
+AX = mybir.AxisListType
+
+B, S, D, DV, DK = 8, 512, 512, 1024, 128
+P = 128
+FLOPS = 2 * B * (S * D * DV + S * S * DK + S * S * DV)
+
+
+def tile_model_pa_t_kernel(tc, q, k, x3, Wv, bv, inv_scale, dropout_mask, out):
+    nc = tc.nc
+    with ExitStack() as ctx:
+        const = ctx.enter_context(tc.tile_pool(name="const", bufs=1))
+        big = ctx.enter_context(tc.tile_pool(name="big", bufs=2))
+        work2 = ctx.enter_context(tc.tile_pool(name="work2", bufs=2))
+        work3 = ctx.enter_context(tc.tile_pool(name="work3", bufs=3))
+        work4 = ctx.enter_context(tc.tile_pool(name="work4", bufs=4))
+        work8 = ctx.enter_context(tc.tile_pool(name="work8", bufs=8))
+        ps_t = ctx.enter_context(tc.psum_pool(name="ps_t", bufs=2))
+        ps_v = ctx.enter_context(tc.psum_pool(name="ps_v", bufs=2))
+        ps_s = ctx.enter_context(tc.psum_pool(name="ps_s", bufs=2))
+        ps_o = ctx.enter_context(tc.psum_pool(name="ps_o", bufs=2))
+
+        inv_raw = const.tile([P, 4, S], BF16, name="inv_raw")
+        nc.sync.dma_start(out=inv_raw[:], in_=inv_scale.rearrange("(p i) k -> p i k", i=4))
+        x_raw = []
+        k_raw = []
+        q_raw = []
+        m_raw = []
+        for b in range(B):
+            x_raw.append(const.tile([P, 4, D], BF16, name="x_raw%d" % b))
+            k_raw.append(const.tile([P, 4, DK], BF16, name="k_raw%d" % b))
+            q_raw.append(const.tile([P, 4, DK], BF16, name="q_raw%d" % b))
+            m_raw.append(const.tile([P, 4, S], BF16, name="m_raw%d" % b))
+        w_raw = big.tile([P, 8, D], BF16, name="w_raw", tag="big", align_bytes=64)
+        brow = const.tile([P, DV], BF16, name="brow")
+        nc.vector.memset(brow[:], 0.0)
+
+        def load(b):
+            nc.sync.dma_start(out=x_raw[b][:], in_=x3[b].rearrange("(t p) d -> p t d", p=P))
+            if b == 0:
+                nc.sync.dma_start(out=w_raw[:], in_=Wv.rearrange("(j p) d -> p j d", p=P))
+            nc.sync.dma_start(out=k_raw[b][:], in_=k[b].rearrange("(t p) d -> p t d", p=P))
+            nc.sync.dma_start(out=q_raw[b][:], in_=q[b].rearrange("(p i) d -> p i d", i=4))
+            if b == 0:
+                nc.sync.dma_start(out=brow[0:1, :], in_=bv.rearrange("(o n) -> o n", o=1))
+            nc.sync.dma_start(out=m_raw[b][:], in_=dropout_mask[b].rearrange("(p i) k -> p i k", i=4))
+
+        for b in range(B):
+            load(b)
+
+        id_f = const.tile([P, P], F32, name="id_f")
+        make_identity(nc, id_f[:])
+        id_b = const.tile([P, P], BF16, name="id_b")
+        make_identity(nc, id_b[:])
+        ones = const.tile([P, P], BF16, name="ones")
+        nc.vector.memset(ones[:], 1.0)
+
+        rinv = const.tile([P, 4, S], F32, name="rinv")
+        bias = const.tile([P, DV], F32, name="bias")
+        wc = const.tile([P, DV], U32, name="wc", align_bytes=64)
+        ws = const.tile([P, DV], U8, name="ws", align_bytes=64)
+
+        xc = {}
+        xs = {}
+        qkT = {}
+        vc = {}
+        vs = {}
+        pe = {}
+        pc = {}
+        psc = {}
+        rr = {}
+
+        def words_to_psum(src, n):
+            banks = []
+            for h in range(n // 2):
+                xt = ps_t.tile([P, 2, 2, P], F32, name="xt", tag="tr")
+                for t in range(2):
+                    for u in range(2):
+                        nc.tensor.transpose(
+                            xt[:, t, u, :],
+                            src[:, 2 * h + t, :].bitcast(F32)[:, P * u : P * u + P],
+                            id_f[:],
+                        )
+                banks.append(xt)
+            return banks
+
+        def t1(b):
+            xg = work2.tile([P, 4 * S], BF16, name="xg", align_bytes=64)
+            xgw = xg[:].bitcast(F32).rearrange("p (h t r u) -> p h t r u", h=2, t=2, u=2)
+            for h, xt in enumerate(words_to_psum(x_raw[b], 4)):
+                nc.scalar.copy(out=xgw[:, h], in_=xt[:].rearrange("p t u r -> p t r u"))
+            qk_ps = ps_t.tile([P, 8, P], BF16, name="qk_ps", tag="tr")
+            for i in range(4):
+                nc.tensor.transpose(qk_ps[:, i, :], q_raw[b][:, i, :], id_b[:])
+            for t in range(4):
+                nc.tensor.transpose(qk_ps[:, 4 + t, :], k_raw[b][:, t, :], id_b[:])
+            qkT[b] = work3.tile([P, 8, P], BF16, name="qkT")
+            nc.scalar.copy(out=qkT[b][:], in_=qk_ps[:])
+            xc[b] = work3.tile([P, S], U32, name="xc", align_bytes=64)
+            xs[b] = work3.tile([P, S], U8, name="xs", align_bytes=64)
+            nc.vector.quantize_mx(out=xc[b][:].bitcast(FP8X4), scales=xs[b][:], in_=xg[:])
+
+        def m1(b):
+            vg = work2.tile([P, DV, 4], BF16, name="vg", align_bytes=64)
+            for c in range(8):
+                cols = slice(P * c, P * c + P)
+                vp = ps_v.tile([P, 4, P], F32, name="vp")
+                for t in range(4):
+                    keys = slice(P * t, P * t + P)
+                    nc.tensor.matmul_mx(
+                        out=vp[:, t, :],
+                        lhsT=xc[b][:, keys].bitcast(FP8X4),
+                        lhsT_scale=xs[b][:, keys],
+                        rhs=wc[:, cols].bitcast(FP8X4),
+                        rhs_scale=ws[:, cols],
+                        start=True,
+                        stop=True,
+                    )
+                nc.vector.tensor_tensor(
+                    out=vg[:, cols, :],
+                    in0=vp[:].rearrange("p t c -> p c t"),
+                    in1=bias[:, cols].unsqueeze(2).to_broadcast([P, P, 4]),
+                    op=ALU.add,
+                )
+            vc[b] = work2.tile([P, DV], U32, name="vc", align_bytes=64)
+            vs[b] = work2.tile([P, DV], U8, name="vs", align_bytes=64)
+            for h in range(2):
+                cols = slice(512 * h, 512 * h + 512)
+                nc.vector.quantize_mx(
+                    out=vc[b][:, cols].bitcast(FP8X4),
+                    scales=vs[b][:, cols],
+                    in_=vg[:, cols, :].rearrange("p c t -> p (c t)"),
+                )
+
+        def qk(b):
+            rs = work3.tile([P, 4], F32, name="rs")
+            pe[b] = []
+            for i in range(4):
+                sp = ps_s.tile([P, S], F32, name="sp")
+                nc.tensor.matmul(
+                    out=sp[:],
+                    lhsT=qkT[b][:, i, :],
+                    rhs=qkT[b][:, 4:8, :].rearrange("p t c -> p (t c)"),
+                    start=True,
+                    stop=True,
+                )
+                z = work4.tile([P, S], F32, name="z")
+                nc.vector.tensor_tensor(out=z[:], in0=sp[:], in1=rinv[:, i, :], op=ALU.mult)
+                nm = work8.tile([P, 1], F32, name="nm")
+                nc.vector.tensor_reduce(out=nm[:], in_=z[:], axis=AX.X, op=ALU.max, negate=True)
+                e = work4.tile([P, S], F32, name="e")
+                nc.scalar.activation(
+                    out=e[:], in_=z[:], func=ACT.Exp, bias=nm[:], scale=1.0, accum_out=rs[:, i : i + 1]
+                )
+                pei = work8.tile([P, S], BF16, name="pei")
+                nc.gpsimd.tensor_tensor(out=pei[:], in0=e[:], in1=m_raw[b][:, i, :], op=ALU.mult)
+                pe[b].append(pei)
+            rr[b] = work3.tile([P, 4], F32, name="rr")
+            nc.vector.reciprocal(out=rr[b][:], in_=rs[:])
+
+        def t2(b):
+            pg = work2.tile([P, 2, 2, P, 4], BF16, name="pg", align_bytes=64)
+            for h in range(2):
+                pt = ps_t.tile([P, 2, 4, P], BF16, name="pt", tag="tr")
+                for ii in range(2):
+                    for t in range(4):
+                        nc.tensor.transpose(
+                            pt[:, ii, t, :], pe[b][2 * h + ii][:, P * t : P * t + P], id_b[:]
+                        )
+                nc.scalar.copy(out=pg[:, h], in_=pt[:].rearrange("p i t r -> p i r t"))
+            pc[b] = work2.tile([P, S], U32, name="pc", align_bytes=64)
+            psc[b] = work2.tile([P, S], U8, name="psc", align_bytes=64)
+            nc.vector.quantize_mx(
+                out=pc[b][:].bitcast(FP8X4),
+                scales=psc[b][:],
+                in_=pg[:].rearrange("p h i r t -> p (h i r t)"),
+            )
+
+        def m2(b):
+            o = big.tile([P, 4, DV], F32, name="o", tag="big", align_bytes=64)
+            for i in range(4):
+                rows = slice(P * i, P * i + P)
+                for h in range(2):
+                    cols = slice(512 * h, 512 * h + 512)
+                    op = ps_o.tile([P, 512], F32, name="op")
+                    nc.tensor.matmul_mx(
+                        out=op[:],
+                        lhsT=pc[b][:, rows].bitcast(FP8X4),
+                        lhsT_scale=psc[b][:, rows],
+                        rhs=vc[b][:, cols].bitcast(FP8X4),
+                        rhs_scale=vs[b][:, cols],
+                        start=True,
+                        stop=True,
+                    )
+                    nc.scalar.activation(
+                        out=o[:, i, cols], in_=op[:], func=ACT.Copy, scale=rr[b][:, i : i + 1]
+                    )
+            nc.sync.dma_start(out=out[b].rearrange("(p i) n -> p i n", i=4), in_=o[:])
+
+        t1(0)
+        wg = big.tile([P, 4 * DV], BF16, name="wg", tag="big", align_bytes=64)
+        wgw = wg[:].bitcast(F32).rearrange("p (h t r u) -> p h t r u", h=4, t=2, u=2)
+        for h, xt in enumerate(words_to_psum(w_raw, 8)):
+            if h % 2 == 0:
+                nc.vector.tensor_copy(out=wgw[:, h], in_=xt[:].rearrange("p t u r -> p t r u"))
+            else:
+                nc.scalar.copy(out=wgw[:, h], in_=xt[:].rearrange("p t u r -> p t r u"))
+        nc.vector.quantize_mx(out=wc[:].bitcast(FP8X4), scales=ws[:], in_=wg[:])
+        for h in range(2):
+            bp = ps_o.tile([P, 512], F32, name="bp", tag="op")
+            nc.tensor.matmul(out=bp[:], lhsT=ones[:], rhs=brow[:, 512 * h : 512 * h + 512], start=True, stop=True)
+            nc.scalar.copy(out=bias[:, 512 * h : 512 * h + 512], in_=bp[:])
+        for i in range(4):
+            nc.vector.reciprocal(out=rinv[:, i, :], in_=inv_raw[:, i, :])
+        t1(1)
+        qk(0)
+        m1(0)
+        for b in range(B):
+            t2(b)
+            if b + 2 < B:
+                t1(b + 2)
+            if b + 1 < B:
+                qk(b + 1)
+                m1(b + 1)
+            m2(b)

@@ -15,222 +15,320 @@ AX = mybir.AxisListType
 B, S, D, DV, DK = 8, 512, 512, 1024, 128
 P = 128
 FLOPS = 2 * B * (S * D * DV + S * S * DK + S * S * DV)
+PINNED = False
+NEWTON = True
 
 
 def tile_model_pa_t_kernel(tc, q, k, x3, Wv, bv, inv_scale, dropout_mask, out):
     nc = tc.nc
     with ExitStack() as ctx:
+        if PINNED:
+            ctx.enter_context(tc.manual_schedule())
         const = ctx.enter_context(tc.tile_pool(name="const", bufs=1))
         big = ctx.enter_context(tc.tile_pool(name="big", bufs=2))
         work2 = ctx.enter_context(tc.tile_pool(name="work2", bufs=2))
         work3 = ctx.enter_context(tc.tile_pool(name="work3", bufs=3))
         work4 = ctx.enter_context(tc.tile_pool(name="work4", bufs=4))
         work8 = ctx.enter_context(tc.tile_pool(name="work8", bufs=8))
-        ps_t = ctx.enter_context(tc.psum_pool(name="ps_t", bufs=2))
-        ps_v = ctx.enter_context(tc.psum_pool(name="ps_v", bufs=2))
-        ps_s = ctx.enter_context(tc.psum_pool(name="ps_s", bufs=2))
-        ps_o = ctx.enter_context(tc.psum_pool(name="ps_o", bufs=2))
+        ring_v = ctx.enter_context(tc.psum_pool(name="ring_v", bufs=4))
+        ring_s = ctx.enter_context(tc.psum_pool(name="ring_s", bufs=4))
 
-        inv_raw = const.tile([P, 4, S], BF16, name="inv_raw")
-        nc.sync.dma_start(out=inv_raw[:], in_=inv_scale.rearrange("(p i) k -> p i k", i=4))
         x_raw = []
-        k_raw = []
-        q_raw = []
         m_raw = []
         for b in range(B):
             x_raw.append(const.tile([P, 4, D], BF16, name="x_raw%d" % b))
-            k_raw.append(const.tile([P, 4, DK], BF16, name="k_raw%d" % b))
-            q_raw.append(const.tile([P, 4, DK], BF16, name="q_raw%d" % b))
             m_raw.append(const.tile([P, 4, S], BF16, name="m_raw%d" % b))
+        k_raw = const.tile([P, B, 4, DK], BF16, name="k_raw")
+        q_raw = const.tile([P, B, 4, DK], BF16, name="q_raw")
+        inv_raw = const.tile([P, 4, S], BF16, name="inv_raw")
         w_raw = big.tile([P, 8, D], BF16, name="w_raw", tag="big", align_bytes=64)
         brow = const.tile([P, DV], BF16, name="brow")
         nc.vector.memset(brow[:], 0.0)
+        ones = const.tile([P, P], BF16, name="ones")
+        nc.vector.memset(ones[:], 1.0)
 
-        def load(b):
+        def load_x(b):
             nc.sync.dma_start(out=x_raw[b][:], in_=x3[b].rearrange("(t p) d -> p t d", p=P))
-            if b == 0:
-                nc.sync.dma_start(out=w_raw[:], in_=Wv.rearrange("(j p) d -> p j d", p=P))
-            nc.sync.dma_start(out=k_raw[b][:], in_=k[b].rearrange("(t p) d -> p t d", p=P))
-            nc.sync.dma_start(out=q_raw[b][:], in_=q[b].rearrange("(p i) d -> p i d", i=4))
-            if b == 0:
-                nc.sync.dma_start(out=brow[0:1, :], in_=bv.rearrange("(o n) -> o n", o=1))
+
+        def load_m(b):
             nc.sync.dma_start(out=m_raw[b][:], in_=dropout_mask[b].rearrange("(p i) k -> p i k", i=4))
 
-        for b in range(B):
-            load(b)
+        nc.sync.dma_start(out=inv_raw[:], in_=inv_scale.rearrange("(p i) k -> p i k", i=4))
+        nc.sync.dma_start(out=brow[0:1, :], in_=bv.rearrange("(o n) -> o n", o=1))
+        w_view = Wv.rearrange("(j p) d -> p j d", p=P)
+        nc.sync.dma_start(out=w_raw[:, 0:4], in_=w_view[:, 0:4])
+        nc.sync.dma_start(out=w_raw[:, 4:8], in_=w_view[:, 4:8])
+        load_x(0)
+        nc.sync.dma_start(out=k_raw[:, 0], in_=k[0].rearrange("(t p) d -> p t d", p=P))
+        nc.sync.dma_start(out=q_raw[:, 0], in_=q[0].rearrange("(p i) d -> p i d", i=4))
+        load_m(0)
+        load_x(1)
+        nc.sync.dma_start(out=k_raw[:, 1:B], in_=k[1:B].rearrange("b (t p) d -> p b t d", p=P))
+        nc.sync.dma_start(out=q_raw[:, 1:B], in_=q[1:B].rearrange("b (p i) d -> p b i d", i=4))
+        load_m(1)
+        for b in range(2, B):
+            load_x(b)
+            load_m(b)
 
         id_f = const.tile([P, P], F32, name="id_f")
         make_identity(nc, id_f[:])
         id_b = const.tile([P, P], BF16, name="id_b")
         make_identity(nc, id_b[:])
-        ones = const.tile([P, P], BF16, name="ones")
-        nc.vector.memset(ones[:], 1.0)
-
         rinv = const.tile([P, 4, S], F32, name="rinv")
         bias = const.tile([P, DV], F32, name="bias")
         wc = const.tile([P, DV], U32, name="wc", align_bytes=64)
         ws = const.tile([P, DV], U8, name="ws", align_bytes=64)
 
-        xc = {}
-        xs = {}
-        qkT = {}
-        vc = {}
-        vs = {}
-        pe = {}
-        pc = {}
-        psc = {}
-        rr = {}
+        live = {}
 
-        def words_to_psum(src, n):
-            banks = []
-            for h in range(n // 2):
-                xt = ps_t.tile([P, 2, 2, P], F32, name="xt", tag="tr")
-                for t in range(2):
-                    for u in range(2):
-                        nc.tensor.transpose(
-                            xt[:, t, u, :],
-                            src[:, 2 * h + t, :].bitcast(F32)[:, P * u : P * u + P],
-                            id_f[:],
-                        )
-                banks.append(xt)
-            return banks
+        def there(b):
+            return 0 <= b < B
 
-        def t1(b):
-            xg = work2.tile([P, 4 * S], BF16, name="xg", align_bytes=64)
-            xgw = xg[:].bitcast(F32).rearrange("p (h t r u) -> p h t r u", h=2, t=2, u=2)
-            for h, xt in enumerate(words_to_psum(x_raw[b], 4)):
-                nc.scalar.copy(out=xgw[:, h], in_=xt[:].rearrange("p t u r -> p t r u"))
-            qk_ps = ps_t.tile([P, 8, P], BF16, name="qk_ps", tag="tr")
-            for i in range(4):
-                nc.tensor.transpose(qk_ps[:, i, :], q_raw[b][:, i, :], id_b[:])
-            for t in range(4):
-                nc.tensor.transpose(qk_ps[:, 4 + t, :], k_raw[b][:, t, :], id_b[:])
-            qkT[b] = work3.tile([P, 8, P], BF16, name="qkT")
-            nc.scalar.copy(out=qkT[b][:], in_=qk_ps[:])
-            xc[b] = work3.tile([P, S], U32, name="xc", align_bytes=64)
-            xs[b] = work3.tile([P, S], U8, name="xs", align_bytes=64)
-            nc.vector.quantize_mx(out=xc[b][:].bitcast(FP8X4), scales=xs[b][:], in_=xg[:])
+        def copy_on(engine_is_vector, dst, src):
+            if engine_is_vector:
+                nc.vector.tensor_copy(out=dst, in_=src)
+            else:
+                nc.scalar.copy(out=dst, in_=src)
 
-        def m1(b):
-            vg = work2.tile([P, DV, 4], BF16, name="vg", align_bytes=64)
-            for c in range(8):
+        def word_transposes(src, h):
+            xt = ring_s.tile([P, 2, 2, P], F32, name="xt", tag="rs")
+            for t in range(2):
+                for u in range(2):
+                    nc.tensor.transpose(
+                        xt[:, t, u, :], src[:, 2 * h + t, :].bitcast(F32)[:, P * u : P * u + P], id_f[:]
+                    )
+            return xt
+
+        def x_transpose(b, h):
+            if there(b):
+                live["xt", b, h] = word_transposes(x_raw[b], h)
+
+        def x_drain(b, h):
+            if there(b):
+                if h == 0:
+                    live["xg", b] = work2.tile([P, 4 * S], BF16, name="xg", align_bytes=64)
+                xgw = live["xg", b][:].bitcast(F32).rearrange("p (h t r u) -> p h t r u", h=2, t=2, u=2)
+                copy_on(b == 0, xgw[:, h], live["xt", b, h][:].rearrange("p t u r -> p t r u"))
+
+        def qk_transpose(b):
+            if there(b):
+                qk_ps = ring_s.tile([P, 8, P], BF16, name="qk_ps", tag="rs")
+                for i in range(4):
+                    nc.tensor.transpose(qk_ps[:, i, :], q_raw[:, b, i, :], id_b[:])
+                for t in range(4):
+                    nc.tensor.transpose(qk_ps[:, 4 + t, :], k_raw[:, b, t, :], id_b[:])
+                live["qk_ps", b] = qk_ps
+
+        def qk_drain(b):
+            if there(b):
+                live["qkT", b] = work3.tile([P, 8, P], BF16, name="qkT")
+                copy_on(b == 0, live["qkT", b][:], live["qk_ps", b][:])
+
+        def quant_x(b):
+            if there(b):
+                live["xc", b] = work3.tile([P, S], U32, name="xc", align_bytes=64)
+                live["xs", b] = work3.tile([P, S], U8, name="xs", align_bytes=64)
+                nc.vector.quantize_mx(
+                    out=live["xc", b][:].bitcast(FP8X4), scales=live["xs", b][:], in_=live["xg", b][:]
+                )
+
+        def v_pass(b, c):
+            if there(b):
                 cols = slice(P * c, P * c + P)
-                vp = ps_v.tile([P, 4, P], F32, name="vp")
+                vp = ring_v.tile([P, 4, P], F32, name="vp", tag="rv")
                 for t in range(4):
                     keys = slice(P * t, P * t + P)
                     nc.tensor.matmul_mx(
                         out=vp[:, t, :],
-                        lhsT=xc[b][:, keys].bitcast(FP8X4),
-                        lhsT_scale=xs[b][:, keys],
+                        lhsT=live["xc", b][:, keys].bitcast(FP8X4),
+                        lhsT_scale=live["xs", b][:, keys],
                         rhs=wc[:, cols].bitcast(FP8X4),
                         rhs_scale=ws[:, cols],
                         start=True,
                         stop=True,
                     )
+                live["vp", b, c] = vp
+
+        def v_drain(b, c):
+            if there(b):
+                if c == 0:
+                    live["vg", b] = work2.tile([P, DV, 4], BF16, name="vg", align_bytes=64)
+                cols = slice(P * c, P * c + P)
                 nc.vector.tensor_tensor(
-                    out=vg[:, cols, :],
-                    in0=vp[:].rearrange("p t c -> p c t"),
+                    out=live["vg", b][:, cols, :],
+                    in0=live["vp", b, c][:].rearrange("p t c -> p c t"),
                     in1=bias[:, cols].unsqueeze(2).to_broadcast([P, P, 4]),
                     op=ALU.add,
                 )
-            vc[b] = work2.tile([P, DV], U32, name="vc", align_bytes=64)
-            vs[b] = work2.tile([P, DV], U8, name="vs", align_bytes=64)
-            for h in range(2):
-                cols = slice(512 * h, 512 * h + 512)
+
+        def quant_v(b):
+            if there(b):
+                live["vc", b] = work2.tile([P, DV], U32, name="vc", align_bytes=64)
+                live["vs", b] = work2.tile([P, DV], U8, name="vs", align_bytes=64)
                 nc.vector.quantize_mx(
-                    out=vc[b][:, cols].bitcast(FP8X4),
-                    scales=vs[b][:, cols],
-                    in_=vg[:, cols, :].rearrange("p c t -> p (c t)"),
+                    out=live["vc", b][:].bitcast(FP8X4),
+                    scales=live["vs", b][:],
+                    in_=live["vg", b][:].rearrange("p c t -> p (c t)"),
                 )
 
-        def qk(b):
-            rs = work3.tile([P, 4], F32, name="rs")
-            pe[b] = []
-            for i in range(4):
-                sp = ps_s.tile([P, S], F32, name="sp")
+        def score_pass(b, i):
+            if there(b):
+                sp = ring_v.tile([P, S], F32, name="sp", tag="rv")
                 nc.tensor.matmul(
                     out=sp[:],
-                    lhsT=qkT[b][:, i, :],
-                    rhs=qkT[b][:, 4:8, :].rearrange("p t c -> p (t c)"),
+                    lhsT=live["qkT", b][:, i, :],
+                    rhs=live["qkT", b][:, 4:8, :].rearrange("p t c -> p (t c)"),
                     start=True,
                     stop=True,
                 )
+                live["sp", b, i] = sp
+
+        def score_scale_max(b, i):
+            if there(b):
                 z = work4.tile([P, S], F32, name="z")
-                nc.vector.tensor_tensor(out=z[:], in0=sp[:], in1=rinv[:, i, :], op=ALU.mult)
+                nc.vector.tensor_tensor(out=z[:], in0=live["sp", b, i][:], in1=rinv[:, i, :], op=ALU.mult)
                 nm = work8.tile([P, 1], F32, name="nm")
                 nc.vector.tensor_reduce(out=nm[:], in_=z[:], axis=AX.X, op=ALU.max, negate=True)
+                live["z", b, i] = z
+                live["nm", b, i] = nm
+
+        def score_exp(b, i):
+            if there(b):
+                if i == 0:
+                    live["rs", b] = work4.tile([P, 4], F32, name="rs")
                 e = work4.tile([P, S], F32, name="e")
                 nc.scalar.activation(
-                    out=e[:], in_=z[:], func=ACT.Exp, bias=nm[:], scale=1.0, accum_out=rs[:, i : i + 1]
+                    out=e[:],
+                    in_=live["z", b, i][:],
+                    func=ACT.Exp,
+                    bias=live["nm", b, i][:],
+                    scale=1.0,
+                    accum_out=live["rs", b][:, i : i + 1],
                 )
-                pei = work8.tile([P, S], BF16, name="pei")
-                nc.gpsimd.tensor_tensor(out=pei[:], in0=e[:], in1=m_raw[b][:, i, :], op=ALU.mult)
-                pe[b].append(pei)
-            rr[b] = work3.tile([P, 4], F32, name="rr")
-            nc.vector.reciprocal(out=rr[b][:], in_=rs[:])
+                live["e", b, i] = e
 
-        def t2(b):
-            pg = work2.tile([P, 2, 2, P, 4], BF16, name="pg", align_bytes=64)
-            for h in range(2):
-                pt = ps_t.tile([P, 2, 4, P], BF16, name="pt", tag="tr")
+        def score_mask(b, i):
+            if there(b):
+                pei = work8.tile([P, S], BF16, name="pei")
+                nc.gpsimd.tensor_tensor(out=pei[:], in0=live["e", b, i][:], in1=m_raw[b][:, i, :], op=ALU.mult)
+                live["pe", b, i] = pei
+
+        def recip_rowsum(b):
+            if there(b):
+                live["rr", b] = work4.tile([P, 4], F32, name="rr")
+                nc.vector.reciprocal(out=live["rr", b][:], in_=live["rs", b][:])
+
+        def p_transpose(b, h):
+            if there(b):
+                pt = ring_s.tile([P, 2, 4, P], BF16, name="pt", tag="rs")
                 for ii in range(2):
                     for t in range(4):
                         nc.tensor.transpose(
-                            pt[:, ii, t, :], pe[b][2 * h + ii][:, P * t : P * t + P], id_b[:]
+                            pt[:, ii, t, :], live["pe", b, 2 * h + ii][:, P * t : P * t + P], id_b[:]
                         )
-                nc.scalar.copy(out=pg[:, h], in_=pt[:].rearrange("p i t r -> p i r t"))
-            pc[b] = work2.tile([P, S], U32, name="pc", align_bytes=64)
-            psc[b] = work2.tile([P, S], U8, name="psc", align_bytes=64)
-            nc.vector.quantize_mx(
-                out=pc[b][:].bitcast(FP8X4),
-                scales=psc[b][:],
-                in_=pg[:].rearrange("p h i r t -> p (h i r t)"),
-            )
+                live["pt", b, h] = pt
 
-        def m2(b):
-            o = big.tile([P, 4, DV], F32, name="o", tag="big", align_bytes=64)
-            for i in range(4):
+        def p_drain(b, h):
+            if there(b):
+                if h == 0:
+                    live["pg", b] = work2.tile([P, 2, 2, P, 4], BF16, name="pg", align_bytes=64)
+                nc.scalar.copy(out=live["pg", b][:, h], in_=live["pt", b, h][:].rearrange("p i t r -> p i r t"))
+
+        def quant_p(b):
+            if there(b):
+                live["pc", b] = work2.tile([P, S], U32, name="pc", align_bytes=64)
+                live["ps", b] = work2.tile([P, S], U8, name="psc", align_bytes=64)
+                nc.vector.quantize_mx(
+                    out=live["pc", b][:].bitcast(FP8X4),
+                    scales=live["ps", b][:],
+                    in_=live["pg", b][:].rearrange("p h i r t -> p (h i r t)"),
+                )
+
+        def out_pass(b, j):
+            if there(b):
+                i, h = divmod(j, 2)
                 rows = slice(P * i, P * i + P)
-                for h in range(2):
-                    cols = slice(512 * h, 512 * h + 512)
-                    op = ps_o.tile([P, 512], F32, name="op")
-                    nc.tensor.matmul_mx(
-                        out=op[:],
-                        lhsT=pc[b][:, rows].bitcast(FP8X4),
-                        lhsT_scale=psc[b][:, rows],
-                        rhs=vc[b][:, cols].bitcast(FP8X4),
-                        rhs_scale=vs[b][:, cols],
-                        start=True,
-                        stop=True,
-                    )
-                    nc.scalar.activation(
-                        out=o[:, i, cols], in_=op[:], func=ACT.Copy, scale=rr[b][:, i : i + 1]
-                    )
-            nc.sync.dma_start(out=out[b].rearrange("(p i) n -> p i n", i=4), in_=o[:])
+                cols = slice(512 * h, 512 * h + 512)
+                op = ring_s.tile([P, 512], F32, name="op", tag="rs")
+                nc.tensor.matmul_mx(
+                    out=op[:],
+                    lhsT=live["pc", b][:, rows].bitcast(FP8X4),
+                    lhsT_scale=live["ps", b][:, rows],
+                    rhs=live["vc", b][:, cols].bitcast(FP8X4),
+                    rhs_scale=live["vs", b][:, cols],
+                    start=True,
+                    stop=True,
+                )
+                live["op", b, j] = op
 
-        t1(0)
+        def out_drain(b, j):
+            if there(b):
+                i, h = divmod(j, 2)
+                if j == 0:
+                    live["o", b] = big.tile([P, 4, DV], F32, name="o", tag="big", align_bytes=64)
+                dst = live["o", b][:, i, 512 * h : 512 * h + 512]
+                scale = live["rr", b][:, i : i + 1]
+                if b + 2 >= B and h == 1:
+                    nc.vector.tensor_scalar_mul(out=dst, in0=live["op", b, j][:], scalar1=scale)
+                else:
+                    nc.scalar.activation(out=dst, in_=live["op", b, j][:], func=ACT.Copy, scale=scale)
+                rows_of = out[b].rearrange("(p i) n -> p i n", i=4)
+                if b == B - 1:
+                    if h == 1:
+                        nc.sync.dma_start(out=rows_of[:, i, :], in_=live["o", b][:, i, :])
+                elif j == 7:
+                    nc.sync.dma_start(out=rows_of, in_=live["o", b][:])
+
+        def period(n):
+            x_drain(n + 4, 0)
+            x_drain(n + 4, 1)
+            qk_drain(n + 4)
+            p_transpose(n + 1, 0)
+            p_transpose(n + 1, 1)
+            p_drain(n + 1, 0)
+            p_drain(n + 1, 1)
+            quant_v(n + 1)
+            quant_x(n + 3)
+            quant_p(n)
+            recip_rowsum(n)
+            for j in range(8):
+                out_pass(n, j)
+                if j < 4:
+                    score_scale_max(n + 2, j)
+                    score_exp(n + 2, j)
+                    score_mask(n + 2, j)
+                else:
+                    v_drain(n + 2, j - 4)
+                v_pass(n + 2, j)
+                out_drain(n, j)
+            for c in range(4, 8):
+                v_drain(n + 2, c)
+                score_pass(n + 3, c - 4)
+                if c < 6:
+                    x_transpose(n + 5, c - 4)
+                elif c == 6:
+                    qk_transpose(n + 5)
+
         wg = big.tile([P, 4 * DV], BF16, name="wg", tag="big", align_bytes=64)
         wgw = wg[:].bitcast(F32).rearrange("p (h t r u) -> p h t r u", h=4, t=2, u=2)
-        for h, xt in enumerate(words_to_psum(w_raw, 8)):
-            if h % 2 == 0:
-                nc.vector.tensor_copy(out=wgw[:, h], in_=xt[:].rearrange("p t u r -> p t r u"))
-            else:
-                nc.scalar.copy(out=wgw[:, h], in_=xt[:].rearrange("p t u r -> p t r u"))
+        for h in range(4):
+            wt = word_transposes(w_raw, h)
+            nc.vector.tensor_copy(out=wgw[:, h], in_=wt[:].rearrange("p t u r -> p t r u"))
         nc.vector.quantize_mx(out=wc[:].bitcast(FP8X4), scales=ws[:], in_=wg[:])
+        for i in range(4):
+            x = inv_raw[:, i, :]
+            y = work4.tile([P, S], F32, name="y", tag="z")
+            nc.scalar.activation(out=y[:], in_=x, func=ACT.Abs_reciprocal_sqrt)
+            nc.scalar.activation(out=y[:], in_=y[:], func=ACT.Square)
+            nc.scalar.activation(out=y[:], in_=y[:], func=ACT.Square)
+            r0 = work4.tile([P, S], F32, name="r0", tag="e")
+            nc.gpsimd.tensor_tensor(out=r0[:], in0=y[:], in1=x, op=ALU.mult)
+            nc.gpsimd.tensor_tensor(out=y[:], in0=r0[:], in1=x, op=ALU.mult)
+            nc.gpsimd.tensor_scalar(out=y[:], in0=y[:], scalar1=-1.0, scalar2=2.0, op0=ALU.mult, op1=ALU.add)
+            nc.gpsimd.tensor_tensor(out=rinv[:, i, :], in0=r0[:], in1=y[:], op=ALU.mult)
         for h in range(2):
-            bp = ps_o.tile([P, 512], F32, name="bp", tag="op")
+            bp = ring_s.tile([P, 512], F32, name="bp", tag="rs")
             nc.tensor.matmul(out=bp[:], lhsT=ones[:], rhs=brow[:, 512 * h : 512 * h + 512], start=True, stop=True)
             nc.scalar.copy(out=bias[:, 512 * h : 512 * h + 512], in_=bp[:])
-        for i in range(4):
-            nc.vector.reciprocal(out=rinv[:, i, :], in_=inv_raw[:, i, :])
-        t1(1)
-        qk(0)
-        m1(0)
-        for b in range(B):
-            t2(b)
-            if b + 2 < B:
-                t1(b + 2)
-            if b + 1 < B:
-                qk(b + 1)
-                m1(b + 1)
-            m2(b)
+        for n in range(-5, B):
+            period(n)

@@ -17,6 +17,7 @@ P = 128
 FLOPS = 2 * B * (S * D * DV + S * S * DK + S * S * DV)
 PINNED = False
 NEWTON = True
+DETOUR = (0,)
 
 
 def tile_model_pa_t_kernel(tc, q, k, x3, Wv, bv, inv_scale, dropout_mask, out):
@@ -30,8 +31,9 @@ def tile_model_pa_t_kernel(tc, q, k, x3, Wv, bv, inv_scale, dropout_mask, out):
         work3 = ctx.enter_context(tc.tile_pool(name="work3", bufs=3))
         work4 = ctx.enter_context(tc.tile_pool(name="work4", bufs=4))
         work8 = ctx.enter_context(tc.tile_pool(name="work8", bufs=8))
-        ring_v = ctx.enter_context(tc.psum_pool(name="ring_v", bufs=4))
-        ring_s = ctx.enter_context(tc.psum_pool(name="ring_s", bufs=4))
+        ring_v = ctx.enter_context(tc.psum_pool(name="ring_v", bufs=3))
+        ring_a = ctx.enter_context(tc.psum_pool(name="ring_a", bufs=2))
+        ring_s = ctx.enter_context(tc.psum_pool(name="ring_s", bufs=3))
 
         x_raw = []
         m_raw = []
@@ -53,14 +55,14 @@ def tile_model_pa_t_kernel(tc, q, k, x3, Wv, bv, inv_scale, dropout_mask, out):
         def load_m(b):
             nc.sync.dma_start(out=m_raw[b][:], in_=dropout_mask[b].rearrange("(p i) k -> p i k", i=4))
 
-        nc.sync.dma_start(out=inv_raw[:], in_=inv_scale.rearrange("(p i) k -> p i k", i=4))
         nc.sync.dma_start(out=brow[0:1, :], in_=bv.rearrange("(o n) -> o n", o=1))
+        load_x(0)
         w_view = Wv.rearrange("(j p) d -> p j d", p=P)
         nc.sync.dma_start(out=w_raw[:, 0:4], in_=w_view[:, 0:4])
-        nc.sync.dma_start(out=w_raw[:, 4:8], in_=w_view[:, 4:8])
-        load_x(0)
+        nc.sync.dma_start(out=inv_raw[:], in_=inv_scale.rearrange("(p i) k -> p i k", i=4))
         nc.sync.dma_start(out=k_raw[:, 0], in_=k[0].rearrange("(t p) d -> p t d", p=P))
         nc.sync.dma_start(out=q_raw[:, 0], in_=q[0].rearrange("(p i) d -> p i d", i=4))
+        nc.sync.dma_start(out=w_raw[:, 4:8], in_=w_view[:, 4:8])
         load_m(0)
         load_x(1)
         nc.sync.dma_start(out=k_raw[:, 1:B], in_=k[1:B].rearrange("b (t p) d -> p b t d", p=P))
@@ -154,12 +156,22 @@ def tile_model_pa_t_kernel(tc, q, k, x3, Wv, bv, inv_scale, dropout_mask, out):
                 if c == 0:
                     live["vg", b] = work2.tile([P, DV, 4], BF16, name="vg", align_bytes=64)
                 cols = slice(P * c, P * c + P)
-                nc.vector.tensor_tensor(
-                    out=live["vg", b][:, cols, :],
-                    in0=live["vp", b, c][:].rearrange("p t c -> p c t"),
-                    in1=bias[:, cols].unsqueeze(2).to_broadcast([P, P, 4]),
-                    op=ALU.add,
-                )
+                if c in DETOUR:
+                    vf = work3.tile([P, 4, P], F32, name="vf")
+                    nc.scalar.copy(out=vf[:], in_=live["vp", b, c][:])
+                    nc.gpsimd.tensor_tensor(
+                        out=live["vg", b][:, cols, :],
+                        in0=vf[:].rearrange("p t c -> p c t"),
+                        in1=bias[:, cols].unsqueeze(2).to_broadcast([P, P, 4]),
+                        op=ALU.add,
+                    )
+                else:
+                    nc.vector.tensor_tensor(
+                        out=live["vg", b][:, cols, :],
+                        in0=live["vp", b, c][:].rearrange("p t c -> p c t"),
+                        in1=bias[:, cols].unsqueeze(2).to_broadcast([P, P, 4]),
+                        op=ALU.add,
+                    )
 
         def quant_v(b):
             if there(b):
@@ -173,7 +185,7 @@ def tile_model_pa_t_kernel(tc, q, k, x3, Wv, bv, inv_scale, dropout_mask, out):
 
         def score_pass(b, i):
             if there(b):
-                sp = ring_v.tile([P, S], F32, name="sp", tag="rv")
+                sp = ring_a.tile([P, S], F32, name="sp", tag="ra")
                 nc.tensor.matmul(
                     out=sp[:],
                     lhsT=live["qkT", b][:, i, :],
@@ -273,11 +285,8 @@ def tile_model_pa_t_kernel(tc, q, k, x3, Wv, bv, inv_scale, dropout_mask, out):
                 else:
                     nc.scalar.activation(out=dst, in_=live["op", b, j][:], func=ACT.Copy, scale=scale)
                 rows_of = out[b].rearrange("(p i) n -> p i n", i=4)
-                if b == B - 1:
-                    if h == 1:
-                        nc.sync.dma_start(out=rows_of[:, i, :], in_=live["o", b][:, i, :])
-                elif j == 7:
-                    nc.sync.dma_start(out=rows_of, in_=live["o", b][:])
+                if h == 1:
+                    nc.sync.dma_start(out=rows_of[:, i, :], in_=live["o", b][:, i, :])
 
         def period(n):
             x_drain(n + 4, 0)
@@ -314,7 +323,13 @@ def tile_model_pa_t_kernel(tc, q, k, x3, Wv, bv, inv_scale, dropout_mask, out):
         for h in range(4):
             wt = word_transposes(w_raw, h)
             nc.vector.tensor_copy(out=wgw[:, h], in_=wt[:].rearrange("p t u r -> p t r u"))
-        nc.vector.quantize_mx(out=wc[:].bitcast(FP8X4), scales=ws[:], in_=wg[:])
+            if h % 2 == 1:
+                half = slice(512 * (h // 2), 512 * (h // 2) + 512)
+                nc.vector.quantize_mx(
+                    out=wc[:, half].bitcast(FP8X4),
+                    scales=ws[:, half],
+                    in_=wg[:, 2048 * (h // 2) : 2048 * (h // 2) + 2048],
+                )
         for i in range(4):
             x = inv_raw[:, i, :]
             y = work4.tile([P, S], F32, name="y", tag="z")
@@ -324,8 +339,8 @@ def tile_model_pa_t_kernel(tc, q, k, x3, Wv, bv, inv_scale, dropout_mask, out):
             r0 = work4.tile([P, S], F32, name="r0", tag="e")
             nc.gpsimd.tensor_tensor(out=r0[:], in0=y[:], in1=x, op=ALU.mult)
             nc.gpsimd.tensor_tensor(out=y[:], in0=r0[:], in1=x, op=ALU.mult)
-            nc.gpsimd.tensor_scalar(out=y[:], in0=y[:], scalar1=-1.0, scalar2=2.0, op0=ALU.mult, op1=ALU.add)
-            nc.gpsimd.tensor_tensor(out=rinv[:, i, :], in0=r0[:], in1=y[:], op=ALU.mult)
+            nc.scalar.activation(out=y[:], in_=y[:], func=ACT.Identity, bias=2.0, scale=-1.0)
+            nc.vector.tensor_tensor(out=rinv[:, i, :], in0=r0[:], in1=y[:], op=ALU.mult)
         for h in range(2):
             bp = ring_s.tile([P, 512], F32, name="bp", tag="rs")
             nc.tensor.matmul(out=bp[:], lhsT=ones[:], rhs=brow[:, 512 * h : 512 * h + 512], start=True, stop=True)

@@ -15,9 +15,8 @@ AX = mybir.AxisListType
 B, S, D, DV, DK = 8, 512, 512, 1024, 128
 P = 128
 FLOPS = 2 * B * (S * D * DV + S * S * DK + S * S * DV)
-PINNED = False
+PINNED = True
 NEWTON = True
-DETOUR = (0,)
 
 
 def tile_model_pa_t_kernel(tc, q, k, x3, Wv, bv, inv_scale, dropout_mask, out):
@@ -31,9 +30,8 @@ def tile_model_pa_t_kernel(tc, q, k, x3, Wv, bv, inv_scale, dropout_mask, out):
         work3 = ctx.enter_context(tc.tile_pool(name="work3", bufs=3))
         work4 = ctx.enter_context(tc.tile_pool(name="work4", bufs=4))
         work8 = ctx.enter_context(tc.tile_pool(name="work8", bufs=8))
-        ring_v = ctx.enter_context(tc.psum_pool(name="ring_v", bufs=3))
-        ring_a = ctx.enter_context(tc.psum_pool(name="ring_a", bufs=2))
-        ring_s = ctx.enter_context(tc.psum_pool(name="ring_s", bufs=3))
+        ring_v = ctx.enter_context(tc.psum_pool(name="ring_v", bufs=4))
+        ring_s = ctx.enter_context(tc.psum_pool(name="ring_s", bufs=4))
 
         x_raw = []
         m_raw = []
@@ -55,14 +53,14 @@ def tile_model_pa_t_kernel(tc, q, k, x3, Wv, bv, inv_scale, dropout_mask, out):
         def load_m(b):
             nc.sync.dma_start(out=m_raw[b][:], in_=dropout_mask[b].rearrange("(p i) k -> p i k", i=4))
 
+        nc.sync.dma_start(out=inv_raw[:], in_=inv_scale.rearrange("(p i) k -> p i k", i=4))
         nc.sync.dma_start(out=brow[0:1, :], in_=bv.rearrange("(o n) -> o n", o=1))
-        load_x(0)
         w_view = Wv.rearrange("(j p) d -> p j d", p=P)
         nc.sync.dma_start(out=w_raw[:, 0:4], in_=w_view[:, 0:4])
-        nc.sync.dma_start(out=inv_raw[:], in_=inv_scale.rearrange("(p i) k -> p i k", i=4))
+        nc.sync.dma_start(out=w_raw[:, 4:8], in_=w_view[:, 4:8])
+        load_x(0)
         nc.sync.dma_start(out=k_raw[:, 0], in_=k[0].rearrange("(t p) d -> p t d", p=P))
         nc.sync.dma_start(out=q_raw[:, 0], in_=q[0].rearrange("(p i) d -> p i d", i=4))
-        nc.sync.dma_start(out=w_raw[:, 4:8], in_=w_view[:, 4:8])
         load_m(0)
         load_x(1)
         nc.sync.dma_start(out=k_raw[:, 1:B], in_=k[1:B].rearrange("b (t p) d -> p b t d", p=P))
@@ -156,22 +154,12 @@ def tile_model_pa_t_kernel(tc, q, k, x3, Wv, bv, inv_scale, dropout_mask, out):
                 if c == 0:
                     live["vg", b] = work2.tile([P, DV, 4], BF16, name="vg", align_bytes=64)
                 cols = slice(P * c, P * c + P)
-                if c in DETOUR:
-                    vf = work3.tile([P, 4, P], F32, name="vf")
-                    nc.scalar.copy(out=vf[:], in_=live["vp", b, c][:])
-                    nc.gpsimd.tensor_tensor(
-                        out=live["vg", b][:, cols, :],
-                        in0=vf[:].rearrange("p t c -> p c t"),
-                        in1=bias[:, cols].unsqueeze(2).to_broadcast([P, P, 4]),
-                        op=ALU.add,
-                    )
-                else:
-                    nc.vector.tensor_tensor(
-                        out=live["vg", b][:, cols, :],
-                        in0=live["vp", b, c][:].rearrange("p t c -> p c t"),
-                        in1=bias[:, cols].unsqueeze(2).to_broadcast([P, P, 4]),
-                        op=ALU.add,
-                    )
+                nc.vector.tensor_tensor(
+                    out=live["vg", b][:, cols, :],
+                    in0=live["vp", b, c][:].rearrange("p t c -> p c t"),
+                    in1=bias[:, cols].unsqueeze(2).to_broadcast([P, P, 4]),
+                    op=ALU.add,
+                )
 
         def quant_v(b):
             if there(b):
@@ -185,7 +173,7 @@ def tile_model_pa_t_kernel(tc, q, k, x3, Wv, bv, inv_scale, dropout_mask, out):
 
         def score_pass(b, i):
             if there(b):
-                sp = ring_a.tile([P, S], F32, name="sp", tag="ra")
+                sp = ring_v.tile([P, S], F32, name="sp", tag="rv")
                 nc.tensor.matmul(
                     out=sp[:],
                     lhsT=live["qkT", b][:, i, :],
@@ -285,8 +273,11 @@ def tile_model_pa_t_kernel(tc, q, k, x3, Wv, bv, inv_scale, dropout_mask, out):
                 else:
                     nc.scalar.activation(out=dst, in_=live["op", b, j][:], func=ACT.Copy, scale=scale)
                 rows_of = out[b].rearrange("(p i) n -> p i n", i=4)
-                if h == 1:
-                    nc.sync.dma_start(out=rows_of[:, i, :], in_=live["o", b][:, i, :])
+                if b == B - 1:
+                    if h == 1:
+                        nc.sync.dma_start(out=rows_of[:, i, :], in_=live["o", b][:, i, :])
+                elif j == 7:
+                    nc.sync.dma_start(out=rows_of, in_=live["o", b][:])
 
         def period(n):
             x_drain(n + 4, 0)
@@ -323,13 +314,7 @@ def tile_model_pa_t_kernel(tc, q, k, x3, Wv, bv, inv_scale, dropout_mask, out):
         for h in range(4):
             wt = word_transposes(w_raw, h)
             nc.vector.tensor_copy(out=wgw[:, h], in_=wt[:].rearrange("p t u r -> p t r u"))
-            if h % 2 == 1:
-                half = slice(512 * (h // 2), 512 * (h // 2) + 512)
-                nc.vector.quantize_mx(
-                    out=wc[:, half].bitcast(FP8X4),
-                    scales=ws[:, half],
-                    in_=wg[:, 2048 * (h // 2) : 2048 * (h // 2) + 2048],
-                )
+        nc.vector.quantize_mx(out=wc[:].bitcast(FP8X4), scales=ws[:], in_=wg[:])
         for i in range(4):
             x = inv_raw[:, i, :]
             y = work4.tile([P, S], F32, name="y", tag="z")
@@ -338,8 +323,8 @@ def tile_model_pa_t_kernel(tc, q, k, x3, Wv, bv, inv_scale, dropout_mask, out):
             nc.scalar.activation(out=y[:], in_=y[:], func=ACT.Square)
             r0 = work4.tile([P, S], F32, name="r0", tag="e")
             nc.gpsimd.tensor_tensor(out=r0[:], in0=y[:], in1=x, op=ALU.mult)
-            nc.gpsimd.tensor_tensor(out=y[:], in0=r0[:], in1=x, op=ALU.mult)
-            nc.scalar.activation(out=y[:], in_=y[:], func=ACT.Identity, bias=2.0, scale=-1.0)
+            nc.vector.tensor_tensor(out=y[:], in0=r0[:], in1=x, op=ALU.mult)
+            nc.vector.tensor_scalar(out=y[:], in0=y[:], scalar1=-1.0, scalar2=2.0, op0=ALU.mult, op1=ALU.add)
             nc.vector.tensor_tensor(out=rinv[:, i, :], in0=r0[:], in1=y[:], op=ALU.mult)
         for h in range(2):
             bp = ring_s.tile([P, 512], F32, name="bp", tag="rs")

@@ -15,7 +15,7 @@ AX = mybir.AxisListType
 B, S, D, DV, DK = 8, 512, 512, 1024, 128
 P = 128
 FLOPS = 2 * B * (S * D * DV + S * S * DK + S * S * DV)
-PINNED = True
+PINNED = False
 NEWTON = True
 
 
@@ -30,8 +30,8 @@ def tile_model_pa_t_kernel(tc, q, k, x3, Wv, bv, inv_scale, dropout_mask, out):
         work3 = ctx.enter_context(tc.tile_pool(name="work3", bufs=3))
         work4 = ctx.enter_context(tc.tile_pool(name="work4", bufs=4))
         work8 = ctx.enter_context(tc.tile_pool(name="work8", bufs=8))
-        ring_v = ctx.enter_context(tc.psum_pool(name="ring_v", bufs=4))
-        ring_s = ctx.enter_context(tc.psum_pool(name="ring_s", bufs=4))
+        ring_v = ctx.enter_context(tc.psum_pool(name="ring_v", bufs=5))
+        ring_s = ctx.enter_context(tc.psum_pool(name="ring_s", bufs=3))
 
         x_raw = []
         m_raw = []
@@ -273,11 +273,8 @@ def tile_model_pa_t_kernel(tc, q, k, x3, Wv, bv, inv_scale, dropout_mask, out):
                 else:
                     nc.scalar.activation(out=dst, in_=live["op", b, j][:], func=ACT.Copy, scale=scale)
                 rows_of = out[b].rearrange("(p i) n -> p i n", i=4)
-                if b == B - 1:
-                    if h == 1:
-                        nc.sync.dma_start(out=rows_of[:, i, :], in_=live["o", b][:, i, :])
-                elif j == 7:
-                    nc.sync.dma_start(out=rows_of, in_=live["o", b][:])
+                if h == 1:
+                    nc.sync.dma_start(out=rows_of[:, i, :], in_=live["o", b][:, i, :])
 
         def period(n):
             x_drain(n + 4, 0)
@@ -323,9 +320,9 @@ def tile_model_pa_t_kernel(tc, q, k, x3, Wv, bv, inv_scale, dropout_mask, out):
             nc.scalar.activation(out=y[:], in_=y[:], func=ACT.Square)
             r0 = work4.tile([P, S], F32, name="r0", tag="e")
             nc.gpsimd.tensor_tensor(out=r0[:], in0=y[:], in1=x, op=ALU.mult)
-            nc.vector.tensor_tensor(out=y[:], in0=r0[:], in1=x, op=ALU.mult)
-            nc.vector.tensor_scalar(out=y[:], in0=y[:], scalar1=-1.0, scalar2=2.0, op0=ALU.mult, op1=ALU.add)
-            nc.vector.tensor_tensor(out=rinv[:, i, :], in0=r0[:], in1=y[:], op=ALU.mult)
+            nc.gpsimd.tensor_tensor(out=y[:], in0=r0[:], in1=x, op=ALU.mult)
+            nc.gpsimd.tensor_scalar(out=y[:], in0=y[:], scalar1=-1.0, scalar2=2.0, op0=ALU.mult, op1=ALU.add)
+            nc.gpsimd.tensor_tensor(out=rinv[:, i, :], in0=r0[:], in1=y[:], op=ALU.mult)
         for h in range(2):
             bp = ring_s.tile([P, 512], F32, name="bp", tag="rs")
             nc.tensor.matmul(out=bp[:], lhsT=ones[:], rhs=brow[:, 512 * h : 512 * h + 512], start=True, stop=True)

@@ -15,15 +15,11 @@ AX = mybir.AxisListType
 B, S, D, DV, DK = 8, 512, 512, 1024, 128
 P = 128
 FLOPS = 2 * B * (S * D * DV + S * S * DK + S * S * DV)
-PINNED = False
-NEWTON = True
 
 
 def tile_model_pa_t_kernel(tc, q, k, x3, Wv, bv, inv_scale, dropout_mask, out):
     nc = tc.nc
     with ExitStack() as ctx:
-        if PINNED:
-            ctx.enter_context(tc.manual_schedule())
         const = ctx.enter_context(tc.tile_pool(name="const", bufs=1))
         big = ctx.enter_context(tc.tile_pool(name="big", bufs=2))
         work2 = ctx.enter_context(tc.tile_pool(name="work2", bufs=2))
@@ -188,7 +184,7 @@ def tile_model_pa_t_kernel(tc, q, k, x3, Wv, bv, inv_scale, dropout_mask, out):
                 z = work4.tile([P, S], F32, name="z")
                 nc.vector.tensor_tensor(out=z[:], in0=live["sp", b, i][:], in1=rinv[:, i, :], op=ALU.mult)
                 nm = work8.tile([P, 1], F32, name="nm")
-                nc.vector.tensor_reduce(out=nm[:], in_=z[:], axis=AX.X, op=ALU.max, negate=True)
+                nc.vector.tensor_reduce(out=nm[:], in_=z[:], axis=AX.X, op=ALU.min)
                 live["z", b, i] = z
                 live["nm", b, i] = nm
 
@@ -202,7 +198,7 @@ def tile_model_pa_t_kernel(tc, q, k, x3, Wv, bv, inv_scale, dropout_mask, out):
                     in_=live["z", b, i][:],
                     func=ACT.Exp,
                     bias=live["nm", b, i][:],
-                    scale=1.0,
+                    scale=-1.0,
                     accum_out=live["rs", b][:, i : i + 1],
                 )
                 live["e", b, i] = e
@@ -314,15 +310,14 @@ def tile_model_pa_t_kernel(tc, q, k, x3, Wv, bv, inv_scale, dropout_mask, out):
         nc.vector.quantize_mx(out=wc[:].bitcast(FP8X4), scales=ws[:], in_=wg[:])
         for i in range(4):
             x = inv_raw[:, i, :]
-            y = work4.tile([P, S], F32, name="y", tag="z")
-            nc.scalar.activation(out=y[:], in_=x, func=ACT.Abs_reciprocal_sqrt)
-            nc.scalar.activation(out=y[:], in_=y[:], func=ACT.Square)
-            nc.scalar.activation(out=y[:], in_=y[:], func=ACT.Square)
             r0 = work4.tile([P, S], F32, name="r0", tag="e")
-            nc.gpsimd.tensor_tensor(out=r0[:], in0=y[:], in1=x, op=ALU.mult)
-            nc.gpsimd.tensor_tensor(out=y[:], in0=r0[:], in1=x, op=ALU.mult)
-            nc.gpsimd.tensor_scalar(out=y[:], in0=y[:], scalar1=-1.0, scalar2=2.0, op0=ALU.mult, op1=ALU.add)
-            nc.gpsimd.tensor_tensor(out=rinv[:, i, :], in0=r0[:], in1=y[:], op=ALU.mult)
+            nc.scalar.activation(out=r0[:], in_=x, func=ACT.Abs_reciprocal_sqrt)
+            nc.scalar.activation(out=r0[:], in_=r0[:], func=ACT.Square)
+            t0 = work4.tile([P, S], F32, name="t0", tag="z")
+            nc.gpsimd.tensor_tensor(out=t0[:], in0=r0[:], in1=x, op=ALU.mult)
+            nc.vector.scalar_tensor_tensor(
+                out=rinv[:, i, :], in0=t0[:], scalar=2.0, in1=r0[:], op0=ALU.subtract, op1=ALU.mult
+            )
         for h in range(2):
             bp = ring_s.tile([P, 512], F32, name="bp", tag="rs")
             nc.tensor.matmul(out=bp[:], lhsT=ones[:], rhs=brow[:, 512 * h : 512 * h + 512], start=True, stop=True)

@@ -20,6 +20,7 @@ FLOPS = 2 * B * (S * D * DV + S * S * DK + S * S * DV)
 def tile_model_pa_t_kernel(tc, q, k, x3, Wv, bv, inv_scale, dropout_mask, out):
     nc = tc.nc
     with ExitStack() as ctx:
+        ctx.enter_context(tc.manual_schedule())
         const = ctx.enter_context(tc.tile_pool(name="const", bufs=1))
         big = ctx.enter_context(tc.tile_pool(name="big", bufs=2))
         work2 = ctx.enter_context(tc.tile_pool(name="work2", bufs=2))
@@ -49,27 +50,30 @@ def tile_model_pa_t_kernel(tc, q, k, x3, Wv, bv, inv_scale, dropout_mask, out):
         def load_m(b):
             nc.sync.dma_start(out=m_raw[b][:], in_=dropout_mask[b].rearrange("(p i) k -> p i k", i=4))
 
+        def load_qk(b):
+            nc.sync.dma_start(out=q_raw[:, b], in_=q[b].rearrange("(p i) d -> p i d", i=4))
+            nc.sync.dma_start(out=k_raw[:, b], in_=k[b].rearrange("(t p) d -> p t d", p=P))
+
         nc.sync.dma_start(out=inv_raw[:], in_=inv_scale.rearrange("(p i) k -> p i k", i=4))
-        nc.sync.dma_start(out=brow[0:1, :], in_=bv.rearrange("(o n) -> o n", o=1))
+        load_qk(0)
         w_view = Wv.rearrange("(j p) d -> p j d", p=P)
         nc.sync.dma_start(out=w_raw[:, 0:4], in_=w_view[:, 0:4])
         nc.sync.dma_start(out=w_raw[:, 4:8], in_=w_view[:, 4:8])
+        nc.sync.dma_start(out=brow[0:1, :], in_=bv.rearrange("(o n) -> o n", o=1))
         load_x(0)
-        nc.sync.dma_start(out=k_raw[:, 0], in_=k[0].rearrange("(t p) d -> p t d", p=P))
-        nc.sync.dma_start(out=q_raw[:, 0], in_=q[0].rearrange("(p i) d -> p i d", i=4))
         load_m(0)
+        load_qk(1)
         load_x(1)
-        nc.sync.dma_start(out=k_raw[:, 1:B], in_=k[1:B].rearrange("b (t p) d -> p b t d", p=P))
-        nc.sync.dma_start(out=q_raw[:, 1:B], in_=q[1:B].rearrange("b (p i) d -> p b i d", i=4))
         load_m(1)
         for b in range(2, B):
+            load_qk(b)
             load_x(b)
             load_m(b)
 
-        id_f = const.tile([P, P], F32, name="id_f")
-        make_identity(nc, id_f[:])
         id_b = const.tile([P, P], BF16, name="id_b")
         make_identity(nc, id_b[:])
+        id_f = const.tile([P, P], F32, name="id_f")
+        make_identity(nc, id_f[:])
         rinv = const.tile([P, 4, S], F32, name="rinv")
         bias = const.tile([P, DV], F32, name="bias")
         wc = const.tile([P, DV], U32, name="wc", align_bytes=64)
@@ -79,12 +83,6 @@ def tile_model_pa_t_kernel(tc, q, k, x3, Wv, bv, inv_scale, dropout_mask, out):
 
         def there(b):
             return 0 <= b < B
-
-        def copy_on(engine_is_vector, dst, src):
-            if engine_is_vector:
-                nc.vector.tensor_copy(out=dst, in_=src)
-            else:
-                nc.scalar.copy(out=dst, in_=src)
 
         def word_transposes(src, h):
             xt = ring_s.tile([P, 2, 2, P], F32, name="xt", tag="rs")
@@ -104,7 +102,7 @@ def tile_model_pa_t_kernel(tc, q, k, x3, Wv, bv, inv_scale, dropout_mask, out):
                 if h == 0:
                     live["xg", b] = work2.tile([P, 4 * S], BF16, name="xg", align_bytes=64)
                 xgw = live["xg", b][:].bitcast(F32).rearrange("p (h t r u) -> p h t r u", h=2, t=2, u=2)
-                copy_on(b == 0, xgw[:, h], live["xt", b, h][:].rearrange("p t u r -> p t r u"))
+                nc.scalar.copy(out=xgw[:, h], in_=live["xt", b, h][:].rearrange("p t u r -> p t r u"))
 
         def qk_transpose(b):
             if there(b):
@@ -118,7 +116,7 @@ def tile_model_pa_t_kernel(tc, q, k, x3, Wv, bv, inv_scale, dropout_mask, out):
         def qk_drain(b):
             if there(b):
                 live["qkT", b] = work3.tile([P, 8, P], BF16, name="qkT")
-                copy_on(b == 0, live["qkT", b][:], live["qk_ps", b][:])
+                nc.scalar.copy(out=live["qkT", b][:], in_=live["qk_ps", b][:])
 
         def quant_x(b):
             if there(b):
@@ -157,14 +155,16 @@ def tile_model_pa_t_kernel(tc, q, k, x3, Wv, bv, inv_scale, dropout_mask, out):
                     op=ALU.add,
                 )
 
-        def quant_v(b):
+        def quant_v(b, h):
             if there(b):
-                live["vc", b] = work2.tile([P, DV], U32, name="vc", align_bytes=64)
-                live["vs", b] = work2.tile([P, DV], U8, name="vs", align_bytes=64)
+                if h == 0:
+                    live["vc", b] = work2.tile([P, DV], U32, name="vc", align_bytes=64)
+                    live["vs", b] = work2.tile([P, DV], U8, name="vs", align_bytes=64)
+                cols = slice(512 * h, 512 * h + 512)
                 nc.vector.quantize_mx(
-                    out=live["vc", b][:].bitcast(FP8X4),
-                    scales=live["vs", b][:],
-                    in_=live["vg", b][:].rearrange("p c t -> p (c t)"),
+                    out=live["vc", b][:, cols].bitcast(FP8X4),
+                    scales=live["vs", b][:, cols],
+                    in_=live["vg", b][:, cols, :].rearrange("p c t -> p (c t)"),
                 )
 
         def score_pass(b, i):
@@ -179,13 +179,16 @@ def tile_model_pa_t_kernel(tc, q, k, x3, Wv, bv, inv_scale, dropout_mask, out):
                 )
                 live["sp", b, i] = sp
 
-        def score_scale_max(b, i):
+        def score_scale(b, i):
             if there(b):
                 z = work4.tile([P, S], F32, name="z")
                 nc.vector.tensor_tensor(out=z[:], in0=live["sp", b, i][:], in1=rinv[:, i, :], op=ALU.mult)
-                nm = work8.tile([P, 1], F32, name="nm")
-                nc.vector.tensor_reduce(out=nm[:], in_=z[:], axis=AX.X, op=ALU.min)
                 live["z", b, i] = z
+
+        def score_max(b, i):
+            if there(b):
+                nm = work8.tile([P, 1], F32, name="nm")
+                nc.vector.tensor_reduce(out=nm[:], in_=live["z", b, i][:], axis=AX.X, op=ALU.min)
                 live["nm", b, i] = nm
 
         def score_exp(b, i):
@@ -201,12 +204,8 @@ def tile_model_pa_t_kernel(tc, q, k, x3, Wv, bv, inv_scale, dropout_mask, out):
                     scale=-1.0,
                     accum_out=live["rs", b][:, i : i + 1],
                 )
-                live["e", b, i] = e
-
-        def score_mask(b, i):
-            if there(b):
                 pei = work8.tile([P, S], BF16, name="pei")
-                nc.gpsimd.tensor_tensor(out=pei[:], in0=live["e", b, i][:], in1=m_raw[b][:, i, :], op=ALU.mult)
+                nc.gpsimd.tensor_tensor(out=pei[:], in0=e[:], in1=m_raw[b][:, i, :], op=ALU.mult)
                 live["pe", b, i] = pei
 
         def recip_rowsum(b):
@@ -242,7 +241,7 @@ def tile_model_pa_t_kernel(tc, q, k, x3, Wv, bv, inv_scale, dropout_mask, out):
 
         def out_pass(b, j):
             if there(b):
-                i, h = divmod(j, 2)
+                h, i = divmod(j, 4)
                 rows = slice(P * i, P * i + P)
                 cols = slice(512 * h, 512 * h + 512)
                 op = ring_s.tile([P, 512], F32, name="op", tag="rs")
@@ -259,68 +258,174 @@ def tile_model_pa_t_kernel(tc, q, k, x3, Wv, bv, inv_scale, dropout_mask, out):
 
         def out_drain(b, j):
             if there(b):
-                i, h = divmod(j, 2)
+                h, i = divmod(j, 4)
                 if j == 0:
                     live["o", b] = big.tile([P, 4, DV], F32, name="o", tag="big", align_bytes=64)
                 dst = live["o", b][:, i, 512 * h : 512 * h + 512]
                 scale = live["rr", b][:, i : i + 1]
-                if b + 2 >= B and h == 1:
+                if b == B - 1 and j in (5, 7):
                     nc.vector.tensor_scalar_mul(out=dst, in0=live["op", b, j][:], scalar1=scale)
                 else:
                     nc.scalar.activation(out=dst, in_=live["op", b, j][:], func=ACT.Copy, scale=scale)
                 rows_of = out[b].rearrange("(p i) n -> p i n", i=4)
-                if h == 1:
+                if b >= B - 2:
+                    nc.sync.dma_start(out=rows_of[:, i, 512 * h : 512 * h + 512], in_=dst)
+                elif h == 1:
                     nc.sync.dma_start(out=rows_of[:, i, :], in_=live["o", b][:, i, :])
 
-        def period(n):
-            x_drain(n + 4, 0)
-            x_drain(n + 4, 1)
-            qk_drain(n + 4)
-            p_transpose(n + 1, 0)
-            p_transpose(n + 1, 1)
-            p_drain(n + 1, 0)
-            p_drain(n + 1, 1)
-            quant_v(n + 1)
-            quant_x(n + 3)
-            quant_p(n)
-            recip_rowsum(n)
-            for j in range(8):
-                out_pass(n, j)
-                if j < 4:
-                    score_scale_max(n + 2, j)
-                    score_exp(n + 2, j)
-                    score_mask(n + 2, j)
-                else:
-                    v_drain(n + 2, j - 4)
-                v_pass(n + 2, j)
-                out_drain(n, j)
-            for c in range(4, 8):
-                v_drain(n + 2, c)
-                score_pass(n + 3, c - 4)
-                if c < 6:
-                    x_transpose(n + 5, c - 4)
-                elif c == 6:
-                    qk_transpose(n + 5)
+        users = []
+        for n in range(-1, B):
+            for kind, at in (("s", 0), ("s", 1), ("v", 0), ("s", 2), ("v", 1), ("s", 3)):
+                users.append((kind, n + 1 if kind == "s" else n, at))
+            for c in range(2, 8):
+                users.append(("v", n, c))
+        users = [u for u in users if there(u[1])]
 
-        wg = big.tile([P, 4 * DV], BF16, name="wg", tag="big", align_bytes=64)
-        wgw = wg[:].bitcast(F32).rearrange("p (h t r u) -> p h t r u", h=4, t=2, u=2)
-        for h in range(4):
-            wt = word_transposes(w_raw, h)
-            nc.vector.tensor_copy(out=wgw[:, h], in_=wt[:].rearrange("p t u r -> p t r u"))
-        nc.vector.quantize_mx(out=wc[:].bitcast(FP8X4), scales=ws[:], in_=wg[:])
-        for i in range(4):
+        def fill(count):
+            for u in range(count):
+                if users:
+                    kind, b, at = users.pop(0)
+                    if kind == "s":
+                        score_pass(b, at)
+                    else:
+                        v_pass(b, at)
+
+        def outs(b, first, last):
+            for j in range(first, last):
+                out_pass(b, j)
+                out_drain(b, j)
+
+        def period(n):
+            s, v, o = n + 1, n, n - 1
+            outs(o, 4, 6)
+            score_scale(s, 0)
+            fill(1)
+            score_scale(s, 1)
+            fill(1)
+            recip_rowsum(v)
+            quant_p(v)
+            score_max(s, 0)
+            score_exp(s, 0)
+            outs(o, 6, 8)
+            v_drain(v, 0)
+            fill(1)
+            score_scale(s, 2)
+            fill(1)
+            score_max(s, 1)
+            score_exp(s, 1)
+            x_transpose(n + 3, 0)
+            x_drain(n + 3, 0)
+            v_drain(v, 1)
+            fill(1)
+            score_scale(s, 3)
+            fill(1)
+            x_transpose(n + 3, 1)
+            x_drain(n + 3, 1)
+            score_max(s, 2)
+            score_exp(s, 2)
+            v_drain(v, 2)
+            fill(1)
+            qk_transpose(n + 3)
+            qk_drain(n + 3)
+            score_max(s, 3)
+            score_exp(s, 3)
+            v_drain(v, 3)
+            fill(1)
+            p_transpose(s, 0)
+            p_drain(s, 0)
+            if v == B - 1:
+                quant_v(v, 0)
+                outs(v, 0, 4)
+            for c in range(4, 8):
+                v_drain(v, c)
+                fill(1)
+            p_transpose(s, 1)
+            p_drain(s, 1)
+            if v < B - 1:
+                quant_v(v, 0)
+                outs(v, 0, 4)
+            quant_v(v, 1)
+            quant_x(n + 2)
+
+        def table_seed(i):
             x = inv_raw[:, i, :]
             r0 = work4.tile([P, S], F32, name="r0", tag="e")
             nc.scalar.activation(out=r0[:], in_=x, func=ACT.Abs_reciprocal_sqrt)
             nc.scalar.activation(out=r0[:], in_=r0[:], func=ACT.Square)
             t0 = work4.tile([P, S], F32, name="t0", tag="z")
-            nc.gpsimd.tensor_tensor(out=t0[:], in0=r0[:], in1=x, op=ALU.mult)
+            nc.vector.tensor_tensor(out=t0[:], in0=r0[:], in1=x, op=ALU.mult)
+            live["r0", i] = r0
+            live["t0", i] = t0
+
+        def table_step(i):
             nc.vector.scalar_tensor_tensor(
-                out=rinv[:, i, :], in0=t0[:], scalar=2.0, in1=r0[:], op0=ALU.subtract, op1=ALU.mult
+                out=rinv[:, i, :], in0=live["t0", i][:], scalar=2.0, in1=live["r0", i][:], op0=ALU.subtract, op1=ALU.mult
             )
+
+        wg = big.tile([P, 4 * DV], BF16, name="wg", tag="big", align_bytes=64)
+        wgw = wg[:].bitcast(F32).rearrange("p (h t r u) -> p h t r u", h=4, t=2, u=2)
+
+        def w_step(h):
+            wt = word_transposes(w_raw, h)
+            if h < 2:
+                nc.vector.tensor_copy(out=wgw[:, h], in_=wt[:].rearrange("p t u r -> p t r u"))
+            else:
+                nc.scalar.copy(out=wgw[:, h], in_=wt[:].rearrange("p t u r -> p t r u"))
+
+        table_seed(0)
+        qk_transpose(0)
+        qk_drain(0)
+        w_step(0)
+        table_seed(1)
+        fill(4)
+        table_step(0)
+        table_step(1)
+        score_scale(0, 0)
+        table_seed(2)
+        score_scale(0, 1)
+        w_step(1)
+        score_max(0, 0)
+        table_seed(3)
+        table_step(2)
+        score_max(0, 1)
+        table_step(3)
+        warm = const.tile([P, 1], F32, name="warm")
+        nc.scalar.activation(out=warm[:], in_=ones[:, 0:1], func=ACT.Exp)
+        w_step(2)
+        w_step(3)
+        x_transpose(0, 0)
+        x_drain(0, 0)
+        score_scale(0, 2)
+        score_exp(0, 0)
+        x_transpose(0, 1)
+        x_drain(0, 1)
+        score_scale(0, 3)
+        score_exp(0, 1)
+        qk_transpose(1)
+        qk_drain(1)
+        score_max(0, 2)
+        score_exp(0, 2)
+        nc.vector.quantize_mx(out=wc[:].bitcast(FP8X4), scales=ws[:], in_=wg[:])
+        for h in range(2):
+            x_transpose(1, h)
+            x_drain(1, h)
+        score_max(0, 3)
+        score_exp(0, 3)
+        quant_x(0)
+        fill(4)
         for h in range(2):
             bp = ring_s.tile([P, 512], F32, name="bp", tag="rs")
             nc.tensor.matmul(out=bp[:], lhsT=ones[:], rhs=brow[:, 512 * h : 512 * h + 512], start=True, stop=True)
             nc.scalar.copy(out=bias[:, 512 * h : 512 * h + 512], in_=bp[:])
-        for n in range(-5, B):
+        quant_x(1)
+        for h in range(2):
+            p_transpose(0, h)
+            p_drain(0, h)
+        qk_transpose(2)
+        qk_drain(2)
+        for h in range(2):
+            x_transpose(2, h)
+            x_drain(2, h)
+        for n in range(0, B):
             period(n)
+        outs(B - 1, 4, 8)

@@ -45,7 +45,10 @@ def tile_model_pa_t_kernel(tc, q, k, x3, Wv, bv, inv_scale, dropout_mask, out):
         nc.vector.memset(ones[:], 1.0)
 
         def load_x(b):
-            nc.sync.dma_start(out=x_raw[b][:], in_=x3[b].rearrange("(t p) d -> p t d", p=P))
+            nc.sync.dma_start(
+                out=x_raw[b][:].rearrange("p (u e) d -> p u e d", u=2),
+                in_=x3[b].rearrange("(u p e) d -> p u e d", u=2, e=2),
+            )
 
         def load_m(b):
             nc.sync.dma_start(out=m_raw[b][:], in_=dropout_mask[b].rearrange("(p i) k -> p i k", i=4))
@@ -215,19 +218,20 @@ def tile_model_pa_t_kernel(tc, q, k, x3, Wv, bv, inv_scale, dropout_mask, out):
 
         def p_transpose(b, h):
             if there(b):
-                pt = ring_s.tile([P, 2, 4, P], BF16, name="pt", tag="rs")
+                pt = ring_s.tile([P, 2, 2, P], F32, name="pt", tag="rs")
                 for ii in range(2):
-                    for t in range(4):
+                    for u in range(2):
                         nc.tensor.transpose(
-                            pt[:, ii, t, :], live["pe", b, 2 * h + ii][:, P * t : P * t + P], id_b[:]
+                            pt[:, ii, u, :], live["pe", b, 2 * h + ii][:].bitcast(F32)[:, P * u : P * u + P], id_f[:]
                         )
                 live["pt", b, h] = pt
 
         def p_drain(b, h):
             if there(b):
                 if h == 0:
-                    live["pg", b] = work2.tile([P, 2, 2, P, 4], BF16, name="pg", align_bytes=64)
-                nc.scalar.copy(out=live["pg", b][:, h], in_=live["pt", b, h][:].rearrange("p i t r -> p i r t"))
+                    live["pg", b] = work2.tile([P, 4 * S], BF16, name="pg", align_bytes=64)
+                pgw = live["pg", b][:].bitcast(F32).rearrange("p (h i r u) -> p h i r u", h=2, i=2, u=2)
+                nc.scalar.copy(out=pgw[:, h], in_=live["pt", b, h][:].rearrange("p i u r -> p i r u"))
 
         def quant_p(b):
             if there(b):
@@ -236,7 +240,7 @@ def tile_model_pa_t_kernel(tc, q, k, x3, Wv, bv, inv_scale, dropout_mask, out):
                 nc.vector.quantize_mx(
                     out=live["pc", b][:].bitcast(FP8X4),
                     scales=live["ps", b][:],
-                    in_=live["pg", b][:].rearrange("p h i r t -> p (h i r t)"),
+                    in_=live["pg", b][:],
                 )
 
         def out_pass(b, j):
@@ -291,69 +295,90 @@ def tile_model_pa_t_kernel(tc, q, k, x3, Wv, bv, inv_scale, dropout_mask, out):
                         v_pass(b, at)
 
         def outs(b, first, last):
-            for j in range(first, last):
+            for j in range(first, last) if there(b) else ():
                 out_pass(b, j)
                 out_drain(b, j)
 
         def period(n):
             s, v, o = n + 1, n, n - 1
-            outs(o, 4, 6)
+            outs(o, 3, 4)
             score_scale(s, 0)
             fill(1)
             score_scale(s, 1)
             fill(1)
-            recip_rowsum(v)
-            quant_p(v)
+            if v > 0:
+                recip_rowsum(v)
+                quant_p(v)
             score_max(s, 0)
             score_exp(s, 0)
-            outs(o, 6, 8)
+            outs(o, 4, 5)
+            if v == 0:
+                p_transpose(0, 0)
+                p_drain(0, 0)
+                p_transpose(0, 1)
+                p_drain(0, 1)
+                x_transpose(2, 0)
+                x_drain(2, 0)
+                x_transpose(2, 1)
+                x_drain(2, 1)
+            x_transpose(n + 3, 0)
+            x_drain(n + 3, 0)
             v_drain(v, 0)
             fill(1)
             score_scale(s, 2)
             fill(1)
             score_max(s, 1)
             score_exp(s, 1)
-            x_transpose(n + 3, 0)
-            x_drain(n + 3, 0)
+            outs(o, 5, 6)
+            x_transpose(n + 3, 1)
+            x_drain(n + 3, 1)
             v_drain(v, 1)
             fill(1)
             score_scale(s, 3)
             fill(1)
-            x_transpose(n + 3, 1)
-            x_drain(n + 3, 1)
             score_max(s, 2)
             score_exp(s, 2)
+            outs(o, 6, 7)
             v_drain(v, 2)
             fill(1)
-            qk_transpose(n + 3)
-            qk_drain(n + 3)
             score_max(s, 3)
             score_exp(s, 3)
             v_drain(v, 3)
             fill(1)
-            p_transpose(s, 0)
-            p_drain(s, 0)
+            outs(o, 7, 8)
+            qk_transpose(n + 3)
+            qk_drain(n + 3)
             if v == B - 1:
                 quant_v(v, 0)
                 outs(v, 0, 4)
-            for c in range(4, 8):
-                v_drain(v, c)
-                fill(1)
+            v_drain(v, 4)
+            fill(1)
+            v_drain(v, 5)
+            fill(1)
+            p_transpose(s, 0)
+            p_drain(s, 0)
+            v_drain(v, 6)
+            fill(1)
+            v_drain(v, 7)
+            fill(1)
             p_transpose(s, 1)
             p_drain(s, 1)
+            if v == 0:
+                recip_rowsum(0)
+                quant_p(0)
             if v < B - 1:
                 quant_v(v, 0)
-                outs(v, 0, 4)
+                outs(v, 0, 3)
             quant_v(v, 1)
             quant_x(n + 2)
 
-        def table_seed(i):
+        def table_seed(i, product_on):
             x = inv_raw[:, i, :]
             r0 = work4.tile([P, S], F32, name="r0", tag="e")
             nc.scalar.activation(out=r0[:], in_=x, func=ACT.Abs_reciprocal_sqrt)
             nc.scalar.activation(out=r0[:], in_=r0[:], func=ACT.Square)
             t0 = work4.tile([P, S], F32, name="t0", tag="z")
-            nc.vector.tensor_tensor(out=t0[:], in0=r0[:], in1=x, op=ALU.mult)
+            product_on.tensor_tensor(out=t0[:], in0=r0[:], in1=x, op=ALU.mult)
             live["r0", i] = r0
             live["t0", i] = t0
 
@@ -372,60 +397,50 @@ def tile_model_pa_t_kernel(tc, q, k, x3, Wv, bv, inv_scale, dropout_mask, out):
             else:
                 nc.scalar.copy(out=wgw[:, h], in_=wt[:].rearrange("p t u r -> p t r u"))
 
-        table_seed(0)
+        table_seed(0, nc.vector)
         qk_transpose(0)
         qk_drain(0)
         w_step(0)
-        table_seed(1)
         fill(4)
         table_step(0)
-        table_step(1)
+        table_seed(1, nc.gpsimd)
         score_scale(0, 0)
-        table_seed(2)
-        score_scale(0, 1)
         w_step(1)
+        table_step(1)
+        score_scale(0, 1)
+        table_seed(2, nc.gpsimd)
+        table_seed(3, nc.gpsimd)
         score_max(0, 0)
-        table_seed(3)
-        table_step(2)
         score_max(0, 1)
-        table_step(3)
-        warm = const.tile([P, 1], F32, name="warm")
-        nc.scalar.activation(out=warm[:], in_=ones[:, 0:1], func=ACT.Exp)
         w_step(2)
         w_step(3)
+        table_step(2)
+        table_step(3)
+        score_scale(0, 2)
+        score_scale(0, 3)
         x_transpose(0, 0)
         x_drain(0, 0)
-        score_scale(0, 2)
-        score_exp(0, 0)
         x_transpose(0, 1)
         x_drain(0, 1)
-        score_scale(0, 3)
-        score_exp(0, 1)
         qk_transpose(1)
         qk_drain(1)
-        score_max(0, 2)
-        score_exp(0, 2)
-        nc.vector.quantize_mx(out=wc[:].bitcast(FP8X4), scales=ws[:], in_=wg[:])
         for h in range(2):
             x_transpose(1, h)
             x_drain(1, h)
-        score_max(0, 3)
-        score_exp(0, 3)
+        nc.vector.quantize_mx(out=wc[:].bitcast(FP8X4), scales=ws[:], in_=wg[:])
+        score_max(0, 2)
         quant_x(0)
-        fill(4)
+        score_max(0, 3)
+        quant_x(1)
         for h in range(2):
             bp = ring_s.tile([P, 512], F32, name="bp", tag="rs")
             nc.tensor.matmul(out=bp[:], lhsT=ones[:], rhs=brow[:, 512 * h : 512 * h + 512], start=True, stop=True)
             nc.scalar.copy(out=bias[:, 512 * h : 512 * h + 512], in_=bp[:])
-        quant_x(1)
-        for h in range(2):
-            p_transpose(0, h)
-            p_drain(0, h)
+        fill(4)
+        for i in range(4):
+            score_exp(0, i)
         qk_transpose(2)
         qk_drain(2)
-        for h in range(2):
-            x_transpose(2, h)
-            x_drain(2, h)
         for n in range(0, B):
             period(n)
         outs(B - 1, 4, 8)

@@ -129,10 +129,10 @@ def tile_model_pa_t_kernel(tc, q, k, x3, Wv, bv, inv_scale, dropout_mask, out):
                     out=live["xc", b][:].bitcast(FP8X4), scales=live["xs", b][:], in_=live["xg", b][:]
                 )
 
-        def v_pass(b, c):
+        def v_pass(b, c, ring, tag):
             if there(b):
                 cols = slice(P * c, P * c + P)
-                vp = ring_v.tile([P, 4, P], F32, name="vp", tag="rv")
+                vp = ring.tile([P, 4, P], F32, name="vp", tag=tag)
                 for t in range(4):
                     keys = slice(P * t, P * t + P)
                     nc.tensor.matmul_mx(
@@ -148,13 +148,24 @@ def tile_model_pa_t_kernel(tc, q, k, x3, Wv, bv, inv_scale, dropout_mask, out):
 
         def v_drain(b, c):
             if there(b):
-                if c == 0:
-                    live["vg", b] = work2.tile([P, DV, 4], BF16, name="vg", align_bytes=64)
                 cols = slice(P * c, P * c + P)
                 nc.vector.tensor_tensor(
                     out=live["vg", b][:, cols, :],
                     in0=live["vp", b, c][:].rearrange("p t c -> p c t"),
                     in1=bias[:, cols].unsqueeze(2).to_broadcast([P, P, 4]),
+                    op=ALU.add,
+                )
+
+        def v_side(b):
+            if there(b):
+                v_pass(b, 0, ring_s, "rs")
+                live["vg", b] = work2.tile([P, DV, 4], BF16, name="vg", align_bytes=64)
+                vf = work2.tile([P, P, 4], F32, name="vf")
+                nc.scalar.copy(out=vf[:], in_=live["vp", b, 0][:].rearrange("p t c -> p c t"))
+                nc.gpsimd.tensor_tensor(
+                    out=live["vg", b][:, 0:P, :],
+                    in0=vf[:],
+                    in1=bias[:, 0:P].unsqueeze(2).to_broadcast([P, P, 4]),
                     op=ALU.add,
                 )
 
@@ -279,9 +290,9 @@ def tile_model_pa_t_kernel(tc, q, k, x3, Wv, bv, inv_scale, dropout_mask, out):
 
         users = []
         for n in range(-1, B):
-            for kind, at in (("s", 0), ("s", 1), ("v", 0), ("s", 2), ("v", 1), ("s", 3)):
+            for kind, at in (("s", 0), ("s", 1), ("v", 1), ("s", 2), ("v", 2), ("s", 3)):
                 users.append((kind, n + 1 if kind == "s" else n, at))
-            for c in range(2, 8):
+            for c in range(3, 8):
                 users.append(("v", n, c))
         users = [u for u in users if there(u[1])]
 
@@ -292,7 +303,7 @@ def tile_model_pa_t_kernel(tc, q, k, x3, Wv, bv, inv_scale, dropout_mask, out):
                     if kind == "s":
                         score_pass(b, at)
                     else:
-                        v_pass(b, at)
+                        v_pass(b, at, ring_v, "rv")
 
         def outs(b, first, last):
             for j in range(first, last) if there(b) else ():
@@ -313,17 +324,13 @@ def tile_model_pa_t_kernel(tc, q, k, x3, Wv, bv, inv_scale, dropout_mask, out):
             score_exp(s, 0)
             outs(o, 4, 5)
             if v == 0:
-                p_transpose(0, 0)
-                p_drain(0, 0)
-                p_transpose(0, 1)
-                p_drain(0, 1)
                 x_transpose(2, 0)
                 x_drain(2, 0)
                 x_transpose(2, 1)
                 x_drain(2, 1)
             x_transpose(n + 3, 0)
             x_drain(n + 3, 0)
-            v_drain(v, 0)
+            v_drain(v, 1)
             fill(1)
             score_scale(s, 2)
             fill(1)
@@ -332,19 +339,17 @@ def tile_model_pa_t_kernel(tc, q, k, x3, Wv, bv, inv_scale, dropout_mask, out):
             outs(o, 5, 6)
             x_transpose(n + 3, 1)
             x_drain(n + 3, 1)
-            v_drain(v, 1)
+            v_drain(v, 2)
             fill(1)
             score_scale(s, 3)
             fill(1)
             score_max(s, 2)
             score_exp(s, 2)
             outs(o, 6, 7)
-            v_drain(v, 2)
+            v_drain(v, 3)
             fill(1)
             score_max(s, 3)
             score_exp(s, 3)
-            v_drain(v, 3)
-            fill(1)
             outs(o, 7, 8)
             qk_transpose(n + 3)
             qk_drain(n + 3)
@@ -355,6 +360,11 @@ def tile_model_pa_t_kernel(tc, q, k, x3, Wv, bv, inv_scale, dropout_mask, out):
             fill(1)
             v_drain(v, 5)
             fill(1)
+            if v == 0:
+                p_transpose(0, 0)
+                p_drain(0, 0)
+                p_transpose(0, 1)
+                p_drain(0, 1)
             p_transpose(s, 0)
             p_drain(s, 0)
             v_drain(v, 6)
@@ -368,7 +378,9 @@ def tile_model_pa_t_kernel(tc, q, k, x3, Wv, bv, inv_scale, dropout_mask, out):
                 quant_p(0)
             if v < B - 1:
                 quant_v(v, 0)
-                outs(v, 0, 3)
+                outs(v, 0, 2)
+                v_side(v + 1)
+                outs(v, 2, 3)
             quant_v(v, 1)
             quant_x(n + 2)
 
@@ -439,6 +451,7 @@ def tile_model_pa_t_kernel(tc, q, k, x3, Wv, bv, inv_scale, dropout_mask, out):
         fill(4)
         for i in range(4):
             score_exp(0, i)
+        v_side(0)
         qk_transpose(2)
         qk_drain(2)
         for n in range(0, B):

@@ -148,6 +148,8 @@ def tile_model_pa_t_kernel(tc, q, k, x3, Wv, bv, inv_scale, dropout_mask, out):
 
         def v_drain(b, c):
             if there(b):
+                if c == 0:
+                    live["vg", b] = const.tile([P, DV, 4], BF16, name="vg", align_bytes=64)
                 cols = slice(P * c, P * c + P)
                 nc.vector.tensor_tensor(
                     out=live["vg", b][:, cols, :],
@@ -156,15 +158,18 @@ def tile_model_pa_t_kernel(tc, q, k, x3, Wv, bv, inv_scale, dropout_mask, out):
                     op=ALU.add,
                 )
 
-        def v_side(b):
+        def v_side_copy(b):
             if there(b):
                 v_pass(b, 0, ring_s, "rs")
-                live["vg", b] = work2.tile([P, DV, 4], BF16, name="vg", align_bytes=64)
-                vf = work2.tile([P, P, 4], F32, name="vf")
-                nc.scalar.copy(out=vf[:], in_=live["vp", b, 0][:].rearrange("p t c -> p c t"))
+                live["vf", b] = work2.tile([P, P, 4], F32, name="vf")
+                nc.scalar.copy(out=live["vf", b][:], in_=live["vp", b, 0][:].rearrange("p t c -> p c t"))
+
+        def v_side_add(b):
+            if there(b):
+                live["vg", b] = const.tile([P, DV, 4], BF16, name="vg", align_bytes=64)
                 nc.gpsimd.tensor_tensor(
                     out=live["vg", b][:, 0:P, :],
-                    in0=vf[:],
+                    in0=live["vf", b][:],
                     in1=bias[:, 0:P].unsqueeze(2).to_broadcast([P, P, 4]),
                     op=ALU.add,
                 )
@@ -278,7 +283,7 @@ def tile_model_pa_t_kernel(tc, q, k, x3, Wv, bv, inv_scale, dropout_mask, out):
                     live["o", b] = big.tile([P, 4, DV], F32, name="o", tag="big", align_bytes=64)
                 dst = live["o", b][:, i, 512 * h : 512 * h + 512]
                 scale = live["rr", b][:, i : i + 1]
-                if b == B - 1 and j in (5, 7):
+                if b == B - 1 and j in (4, 5):
                     nc.vector.tensor_scalar_mul(out=dst, in0=live["op", b, j][:], scalar1=scale)
                 else:
                     nc.scalar.activation(out=dst, in_=live["op", b, j][:], func=ACT.Copy, scale=scale)
@@ -290,9 +295,9 @@ def tile_model_pa_t_kernel(tc, q, k, x3, Wv, bv, inv_scale, dropout_mask, out):
 
         users = []
         for n in range(-1, B):
-            for kind, at in (("s", 0), ("s", 1), ("v", 1), ("s", 2), ("v", 2), ("s", 3)):
-                users.append((kind, n + 1 if kind == "s" else n, at))
-            for c in range(3, 8):
+            for i in range(4):
+                users.append(("s", n + 1, i))
+            for c in range(0 if n == 0 else 1, 8):
                 users.append(("v", n, c))
         users = [u for u in users if there(u[1])]
 
@@ -312,86 +317,91 @@ def tile_model_pa_t_kernel(tc, q, k, x3, Wv, bv, inv_scale, dropout_mask, out):
 
         def period(n):
             s, v, o = n + 1, n, n - 1
-            outs(o, 3, 4)
+            outs(o, 0, 3)
             score_scale(s, 0)
             fill(1)
             score_scale(s, 1)
             fill(1)
-            if v > 0:
-                recip_rowsum(v)
-                quant_p(v)
             score_max(s, 0)
             score_exp(s, 0)
-            outs(o, 4, 5)
-            if v == 0:
-                x_transpose(2, 0)
-                x_drain(2, 0)
-                x_transpose(2, 1)
-                x_drain(2, 1)
+            if 0 < v < B - 1:
+                recip_rowsum(v)
+                quant_p(v)
+            outs(o, 3, 4)
             x_transpose(n + 3, 0)
             x_drain(n + 3, 0)
-            v_drain(v, 1)
-            fill(1)
             score_scale(s, 2)
             fill(1)
             score_max(s, 1)
             score_exp(s, 1)
-            outs(o, 5, 6)
-            x_transpose(n + 3, 1)
-            x_drain(n + 3, 1)
-            v_drain(v, 2)
-            fill(1)
+            outs(o, 4, 5)
             score_scale(s, 3)
             fill(1)
             score_max(s, 2)
             score_exp(s, 2)
-            outs(o, 6, 7)
-            v_drain(v, 3)
+            x_transpose(n + 3, 1)
+            x_drain(n + 3, 1)
+            if v == 0:
+                v_drain(0, 0)
+                fill(1)
+            v_drain(v, 1)
             fill(1)
             score_max(s, 3)
             score_exp(s, 3)
+            outs(o, 5, 6)
+            v_drain(v, 2)
+            fill(1)
+            outs(o, 6, 7)
+            if v == 0:
+                for h in range(2):
+                    x_transpose(2, h)
+                    x_drain(2, h)
+            v_drain(v, 3)
+            fill(1)
             outs(o, 7, 8)
             qk_transpose(n + 3)
             qk_drain(n + 3)
+            if v == 0:
+                for h in range(2):
+                    p_transpose(0, h)
+                    p_drain(0, h)
             if v == B - 1:
+                recip_rowsum(v)
+                quant_p(v)
                 quant_v(v, 0)
                 outs(v, 0, 4)
             v_drain(v, 4)
             fill(1)
-            v_drain(v, 5)
-            fill(1)
-            if v == 0:
-                p_transpose(0, 0)
-                p_drain(0, 0)
-                p_transpose(0, 1)
-                p_drain(0, 1)
             p_transpose(s, 0)
             p_drain(s, 0)
+            v_drain(v, 5)
+            fill(1)
+            v_side_copy(v + 1)
             v_drain(v, 6)
             fill(1)
             v_drain(v, 7)
             fill(1)
             p_transpose(s, 1)
             p_drain(s, 1)
+            quant_x(n + 2)
             if v == 0:
                 recip_rowsum(0)
                 quant_p(0)
             if v < B - 1:
                 quant_v(v, 0)
-                outs(v, 0, 2)
-                v_side(v + 1)
-                outs(v, 2, 3)
             quant_v(v, 1)
-            quant_x(n + 2)
+            v_side_add(v + 1)
 
-        def table_seed(i, product_on):
+        def table_seed(i):
             x = inv_raw[:, i, :]
             r0 = work4.tile([P, S], F32, name="r0", tag="e")
             nc.scalar.activation(out=r0[:], in_=x, func=ACT.Abs_reciprocal_sqrt)
             nc.scalar.activation(out=r0[:], in_=r0[:], func=ACT.Square)
-            t0 = work4.tile([P, S], F32, name="t0", tag="z")
-            product_on.tensor_tensor(out=t0[:], in0=r0[:], in1=x, op=ALU.mult)
             live["r0", i] = r0
+
+        def table_product(i):
+            t0 = work4.tile([P, S], F32, name="t0", tag="z")
+            nc.vector.tensor_tensor(out=t0[:], in0=live["r0", i][:], in1=inv_raw[:, i, :], op=ALU.mult)
             live["t0", i] = t0
 
         def table_step(i):
@@ -409,49 +419,53 @@ def tile_model_pa_t_kernel(tc, q, k, x3, Wv, bv, inv_scale, dropout_mask, out):
             else:
                 nc.scalar.copy(out=wgw[:, h], in_=wt[:].rearrange("p t u r -> p t r u"))
 
-        table_seed(0, nc.vector)
+        table_seed(0)
+        table_product(0)
         qk_transpose(0)
         qk_drain(0)
         w_step(0)
         fill(4)
         table_step(0)
-        table_seed(1, nc.gpsimd)
+        table_seed(1)
+        table_product(1)
         score_scale(0, 0)
-        w_step(1)
         table_step(1)
+        w_step(1)
         score_scale(0, 1)
-        table_seed(2, nc.gpsimd)
-        table_seed(3, nc.gpsimd)
         score_max(0, 0)
         score_max(0, 1)
+        table_seed(2)
+        table_seed(3)
+        table_product(2)
         w_step(2)
         w_step(3)
+        for h in range(2):
+            x_transpose(0, h)
+            x_drain(0, h)
+        nc.vector.quantize_mx(out=wc[:].bitcast(FP8X4), scales=ws[:], in_=wg[:])
+        table_product(3)
+        quant_x(0)
         table_step(2)
         table_step(3)
-        score_scale(0, 2)
-        score_scale(0, 3)
-        x_transpose(0, 0)
-        x_drain(0, 0)
-        x_transpose(0, 1)
-        x_drain(0, 1)
         qk_transpose(1)
         qk_drain(1)
         for h in range(2):
             x_transpose(1, h)
             x_drain(1, h)
-        nc.vector.quantize_mx(out=wc[:].bitcast(FP8X4), scales=ws[:], in_=wg[:])
-        score_max(0, 2)
-        quant_x(0)
-        score_max(0, 3)
+        score_exp(0, 0)
+        score_exp(0, 1)
         quant_x(1)
+        score_scale(0, 2)
+        score_scale(0, 3)
+        score_max(0, 2)
+        score_exp(0, 2)
+        score_max(0, 3)
+        score_exp(0, 3)
         for h in range(2):
             bp = ring_s.tile([P, 512], F32, name="bp", tag="rs")
             nc.tensor.matmul(out=bp[:], lhsT=ones[:], rhs=brow[:, 512 * h : 512 * h + 512], start=True, stop=True)
             nc.scalar.copy(out=bias[:, 512 * h : 512 * h + 512], in_=bp[:])
         fill(4)
-        for i in range(4):
-            score_exp(0, i)
-        v_side(0)
         qk_transpose(2)
         qk_drain(2)
         for n in range(0, B):

@@ -57,10 +57,12 @@ def tile_model_pa_t_kernel(tc, q, k, x3, Wv, bv, inv_scale, dropout_mask, out):
             nc.sync.dma_start(out=q_raw[:, b], in_=q[b].rearrange("(p i) d -> p i d", i=4))
             nc.sync.dma_start(out=k_raw[:, b], in_=k[b].rearrange("(t p) d -> p t d", p=P))
 
-        nc.sync.dma_start(out=inv_raw[:], in_=inv_scale.rearrange("(p i) k -> p i k", i=4))
-        load_qk(0)
+        inv_view = inv_scale.rearrange("(p i) k -> p i k", i=4)
+        nc.sync.dma_start(out=inv_raw[:, 0:1], in_=inv_view[:, 0:1])
         w_view = Wv.rearrange("(j p) d -> p j d", p=P)
         nc.sync.dma_start(out=w_raw[:, 0:4], in_=w_view[:, 0:4])
+        nc.sync.dma_start(out=inv_raw[:, 1:4], in_=inv_view[:, 1:4])
+        load_qk(0)
         nc.sync.dma_start(out=w_raw[:, 4:8], in_=w_view[:, 4:8])
         nc.sync.dma_start(out=brow[0:1, :], in_=bv.rearrange("(o n) -> o n", o=1))
         load_x(0)
@@ -100,11 +102,19 @@ def tile_model_pa_t_kernel(tc, q, k, x3, Wv, bv, inv_scale, dropout_mask, out):
             if there(b):
                 live["xt", b, h] = word_transposes(x_raw[b], h)
 
+        def stage(b):
+            if ("xp", b) not in live:
+                live["xp", b] = work2.tile([P, 8 * S], BF16, name="xp", align_bytes=64)
+            return live["xp", b]
+
         def x_drain(b, h):
             if there(b):
-                if h == 0:
-                    live["xg", b] = work2.tile([P, 4 * S], BF16, name="xg", align_bytes=64)
-                xgw = live["xg", b][:].bitcast(F32).rearrange("p (h t r u) -> p h t r u", h=2, t=2, u=2)
+                if h == 0 and b < 2:
+                    xg = work2.tile([P, 4 * S], BF16, name="xg", tag="xp", align_bytes=64)
+                    live["xg", b] = xg[:]
+                elif h == 0:
+                    live["xg", b] = stage(b - 2)[:, 0 : 4 * S]
+                xgw = live["xg", b].bitcast(F32).rearrange("p (h t r u) -> p h t r u", h=2, t=2, u=2)
                 nc.scalar.copy(out=xgw[:, h], in_=live["xt", b, h][:].rearrange("p t u r -> p t r u"))
 
         def qk_transpose(b):
@@ -123,10 +133,11 @@ def tile_model_pa_t_kernel(tc, q, k, x3, Wv, bv, inv_scale, dropout_mask, out):
 
         def quant_x(b):
             if there(b):
-                live["xc", b] = work3.tile([P, S], U32, name="xc", align_bytes=64)
-                live["xs", b] = work3.tile([P, S], U8, name="xs", align_bytes=64)
+                xc = work3.tile([P, S], U32, name="xc", tag="xpc", align_bytes=64)
+                xs = work3.tile([P, S], U8, name="xs", tag="xps", align_bytes=64)
+                live["xc", b], live["xs", b] = xc[:], xs[:]
                 nc.vector.quantize_mx(
-                    out=live["xc", b][:].bitcast(FP8X4), scales=live["xs", b][:], in_=live["xg", b][:]
+                    out=live["xc", b].bitcast(FP8X4), scales=live["xs", b], in_=live["xg", b]
                 )
 
         def v_pass(b, c, ring, tag):
@@ -244,20 +255,21 @@ def tile_model_pa_t_kernel(tc, q, k, x3, Wv, bv, inv_scale, dropout_mask, out):
 
         def p_drain(b, h):
             if there(b):
-                if h == 0:
-                    live["pg", b] = work2.tile([P, 4 * S], BF16, name="pg", align_bytes=64)
-                pgw = live["pg", b][:].bitcast(F32).rearrange("p (h i r u) -> p h i r u", h=2, i=2, u=2)
+                pgw = stage(b)[:, 4 * S : 8 * S].bitcast(F32).rearrange("p (h i r u) -> p h i r u", h=2, i=2, u=2)
                 nc.scalar.copy(out=pgw[:, h], in_=live["pt", b, h][:].rearrange("p i u r -> p i r u"))
 
-        def quant_p(b):
+        def quant_xp(b):
             if there(b):
-                live["pc", b] = work2.tile([P, S], U32, name="pc", align_bytes=64)
-                live["ps", b] = work2.tile([P, S], U8, name="psc", align_bytes=64)
+                codes = work3.tile([P, 2 * S], U32, name="xpc", align_bytes=64)
+                scales = work3.tile([P, 2 * S], U8, name="xps", align_bytes=64)
+                first = 0 if there(b + 2) else S
                 nc.vector.quantize_mx(
-                    out=live["pc", b][:].bitcast(FP8X4),
-                    scales=live["ps", b][:],
-                    in_=live["pg", b][:],
+                    out=codes[:, first : 2 * S].bitcast(FP8X4),
+                    scales=scales[:, first : 2 * S],
+                    in_=stage(b)[:, 4 * first : 8 * S],
                 )
+                live["xc", b + 2], live["xs", b + 2] = codes[:, 0:S], scales[:, 0:S]
+                live["pc", b], live["ps", b] = codes[:, S : 2 * S], scales[:, S : 2 * S]
 
         def out_pass(b, j):
             if there(b):
@@ -283,15 +295,12 @@ def tile_model_pa_t_kernel(tc, q, k, x3, Wv, bv, inv_scale, dropout_mask, out):
                     live["o", b] = big.tile([P, 4, DV], F32, name="o", tag="big", align_bytes=64)
                 dst = live["o", b][:, i, 512 * h : 512 * h + 512]
                 scale = live["rr", b][:, i : i + 1]
-                if b == B - 1 and j in (4, 5):
+                if b == B - 1 and j in (3, 5, 7):
                     nc.vector.tensor_scalar_mul(out=dst, in0=live["op", b, j][:], scalar1=scale)
                 else:
                     nc.scalar.activation(out=dst, in_=live["op", b, j][:], func=ACT.Copy, scale=scale)
                 rows_of = out[b].rearrange("(p i) n -> p i n", i=4)
-                if b >= B - 2:
-                    nc.sync.dma_start(out=rows_of[:, i, 512 * h : 512 * h + 512], in_=dst)
-                elif h == 1:
-                    nc.sync.dma_start(out=rows_of[:, i, :], in_=live["o", b][:, i, :])
+                nc.sync.dma_start(out=rows_of[:, i, 512 * h : 512 * h + 512], in_=dst)
 
         users = []
         for n in range(-1, B):
@@ -324,17 +333,13 @@ def tile_model_pa_t_kernel(tc, q, k, x3, Wv, bv, inv_scale, dropout_mask, out):
             fill(1)
             score_max(s, 0)
             score_exp(s, 0)
-            if 0 < v < B - 1:
-                recip_rowsum(v)
-                quant_p(v)
-            outs(o, 3, 4)
             x_transpose(n + 3, 0)
             x_drain(n + 3, 0)
             score_scale(s, 2)
             fill(1)
             score_max(s, 1)
             score_exp(s, 1)
-            outs(o, 4, 5)
+            outs(o, 3, 4)
             score_scale(s, 3)
             fill(1)
             score_max(s, 2)
@@ -348,17 +353,15 @@ def tile_model_pa_t_kernel(tc, q, k, x3, Wv, bv, inv_scale, dropout_mask, out):
             fill(1)
             score_max(s, 3)
             score_exp(s, 3)
-            outs(o, 5, 6)
+            outs(o, 4, 5)
             v_drain(v, 2)
             fill(1)
-            outs(o, 6, 7)
             if v == 0:
                 for h in range(2):
                     x_transpose(2, h)
                     x_drain(2, h)
             v_drain(v, 3)
             fill(1)
-            outs(o, 7, 8)
             qk_transpose(n + 3)
             qk_drain(n + 3)
             if v == 0:
@@ -366,14 +369,17 @@ def tile_model_pa_t_kernel(tc, q, k, x3, Wv, bv, inv_scale, dropout_mask, out):
                     p_transpose(0, h)
                     p_drain(0, h)
             if v == B - 1:
+                outs(o, 5, 8)
                 recip_rowsum(v)
-                quant_p(v)
+                quant_xp(v)
                 quant_v(v, 0)
-                outs(v, 0, 4)
-            v_drain(v, 4)
-            fill(1)
+                outs(v, 0, 3)
             p_transpose(s, 0)
             p_drain(s, 0)
+            v_drain(v, 4)
+            fill(1)
+            if v < B - 1:
+                outs(o, 5, 6)
             v_drain(v, 5)
             fill(1)
             v_side_copy(v + 1)
@@ -383,24 +389,23 @@ def tile_model_pa_t_kernel(tc, q, k, x3, Wv, bv, inv_scale, dropout_mask, out):
             fill(1)
             p_transpose(s, 1)
             p_drain(s, 1)
-            quant_x(n + 2)
-            if v == 0:
-                recip_rowsum(0)
-                quant_p(0)
             if v < B - 1:
+                outs(o, 6, 8)
+                recip_rowsum(v)
+                quant_xp(v)
                 quant_v(v, 0)
             quant_v(v, 1)
             v_side_add(v + 1)
 
         def table_seed(i):
             x = inv_raw[:, i, :]
-            r0 = work4.tile([P, S], F32, name="r0", tag="e")
+            r0 = work3.tile([P, S], F32, name="r0")
             nc.scalar.activation(out=r0[:], in_=x, func=ACT.Abs_reciprocal_sqrt)
             nc.scalar.activation(out=r0[:], in_=r0[:], func=ACT.Square)
             live["r0", i] = r0
 
         def table_product(i):
-            t0 = work4.tile([P, S], F32, name="t0", tag="z")
+            t0 = work2.tile([P, S], F32, name="t0")
             nc.vector.tensor_tensor(out=t0[:], in0=live["r0", i][:], in1=inv_raw[:, i, :], op=ALU.mult)
             live["t0", i] = t0
 
@@ -421,22 +426,22 @@ def tile_model_pa_t_kernel(tc, q, k, x3, Wv, bv, inv_scale, dropout_mask, out):
 
         table_seed(0)
         table_product(0)
-        qk_transpose(0)
-        qk_drain(0)
         w_step(0)
-        fill(4)
+        w_step(1)
         table_step(0)
         table_seed(1)
+        qk_transpose(0)
+        qk_drain(0)
+        fill(4)
         table_product(1)
         score_scale(0, 0)
         table_step(1)
-        w_step(1)
+        table_seed(2)
         score_scale(0, 1)
         score_max(0, 0)
-        score_max(0, 1)
-        table_seed(2)
-        table_seed(3)
         table_product(2)
+        score_max(0, 1)
+        table_seed(3)
         w_step(2)
         w_step(3)
         for h in range(2):
@@ -470,4 +475,4 @@ def tile_model_pa_t_kernel(tc, q, k, x3, Wv, bv, inv_scale, dropout_mask, out):
         qk_drain(2)
         for n in range(0, B):
             period(n)
-        outs(B - 1, 4, 8)
+        outs(B - 1, 3, 8)

@@ -326,6 +326,7 @@ def tile_model_pa_t_kernel(tc, q, k, x3, Wv, bv, inv_scale, dropout_mask, out):
 
         def period(n):
             s, v, o = n + 1, n, n - 1
+            x = n + 3 if n > 0 else 2
             outs(o, 0, 3)
             score_scale(s, 0)
             fill(1)
@@ -333,8 +334,8 @@ def tile_model_pa_t_kernel(tc, q, k, x3, Wv, bv, inv_scale, dropout_mask, out):
             fill(1)
             score_max(s, 0)
             score_exp(s, 0)
-            x_transpose(n + 3, 0)
-            x_drain(n + 3, 0)
+            x_transpose(x, 0)
+            x_drain(x, 0)
             score_scale(s, 2)
             fill(1)
             score_max(s, 1)
@@ -344,8 +345,8 @@ def tile_model_pa_t_kernel(tc, q, k, x3, Wv, bv, inv_scale, dropout_mask, out):
             fill(1)
             score_max(s, 2)
             score_exp(s, 2)
-            x_transpose(n + 3, 1)
-            x_drain(n + 3, 1)
+            x_transpose(x, 1)
+            x_drain(x, 1)
             if v == 0:
                 v_drain(0, 0)
                 fill(1)
@@ -358,16 +359,12 @@ def tile_model_pa_t_kernel(tc, q, k, x3, Wv, bv, inv_scale, dropout_mask, out):
             fill(1)
             if v == 0:
                 for h in range(2):
-                    x_transpose(2, h)
-                    x_drain(2, h)
+                    p_transpose(0, h)
+                    p_drain(0, h)
             v_drain(v, 3)
             fill(1)
             qk_transpose(n + 3)
             qk_drain(n + 3)
-            if v == 0:
-                for h in range(2):
-                    p_transpose(0, h)
-                    p_drain(0, h)
             if v == B - 1:
                 outs(o, 5, 8)
                 recip_rowsum(v)
@@ -389,6 +386,10 @@ def tile_model_pa_t_kernel(tc, q, k, x3, Wv, bv, inv_scale, dropout_mask, out):
             fill(1)
             p_transpose(s, 1)
             p_drain(s, 1)
+            if v == 0:
+                for h in range(2):
+                    x_transpose(3, h)
+                    x_drain(3, h)
             if v < B - 1:
                 outs(o, 6, 8)
                 recip_rowsum(v)

@@ -405,9 +405,9 @@ def tile_model_pa_t_kernel(tc, q, k, x3, Wv, bv, inv_scale, dropout_mask, out):
             nc.scalar.activation(out=r0[:], in_=r0[:], func=ACT.Square)
             live["r0", i] = r0
 
-        def table_product(i):
+        def table_product(i, engine):
             t0 = work2.tile([P, S], F32, name="t0")
-            nc.vector.tensor_tensor(out=t0[:], in0=live["r0", i][:], in1=inv_raw[:, i, :], op=ALU.mult)
+            engine.tensor_tensor(out=t0[:], in0=live["r0", i][:], in1=inv_raw[:, i, :], op=ALU.mult)
             live["t0", i] = t0
 
         def table_step(i):
@@ -426,7 +426,7 @@ def tile_model_pa_t_kernel(tc, q, k, x3, Wv, bv, inv_scale, dropout_mask, out):
                 nc.scalar.copy(out=wgw[:, h], in_=wt[:].rearrange("p t u r -> p t r u"))
 
         table_seed(0)
-        table_product(0)
+        table_product(0, nc.vector)
         w_step(0)
         w_step(1)
         table_step(0)
@@ -434,13 +434,13 @@ def tile_model_pa_t_kernel(tc, q, k, x3, Wv, bv, inv_scale, dropout_mask, out):
         qk_transpose(0)
         qk_drain(0)
         fill(4)
-        table_product(1)
+        table_product(1, nc.vector)
         score_scale(0, 0)
         table_step(1)
         table_seed(2)
         score_scale(0, 1)
         score_max(0, 0)
-        table_product(2)
+        table_product(2, nc.gpsimd)
         score_max(0, 1)
         table_seed(3)
         w_step(2)
@@ -449,7 +449,7 @@ def tile_model_pa_t_kernel(tc, q, k, x3, Wv, bv, inv_scale, dropout_mask, out):
             x_transpose(0, h)
             x_drain(0, h)
         nc.vector.quantize_mx(out=wc[:].bitcast(FP8X4), scales=ws[:], in_=wg[:])
-        table_product(3)
+        table_product(3, nc.gpsimd)
         quant_x(0)
         table_step(2)
         table_step(3)

@@ -14,6 +14,8 @@ AX = mybir.AxisListType
 
 B, S, D, DV, DK = 8, 512, 512, 1024, 128
 P = 128
+W_ON_VECTOR = 4
+X_ON_VECTOR = 1
 FLOPS = 2 * B * (S * D * DV + S * S * DK + S * S * DV)
 
 
@@ -39,10 +41,14 @@ def tile_model_pa_t_kernel(tc, q, k, x3, Wv, bv, inv_scale, dropout_mask, out):
         q_raw = const.tile([P, B, 4, DK], BF16, name="q_raw")
         inv_raw = const.tile([P, 4, S], BF16, name="inv_raw")
         w_raw = big.tile([P, 8, D], BF16, name="w_raw", tag="big", align_bytes=64)
+        one = const.tile([P, 1], F32, name="one")
+        nc.vector.memset(one[:], 1.0)
         brow = const.tile([P, DV], BF16, name="brow")
-        nc.vector.memset(brow[:], 0.0)
         ones = const.tile([P, P], BF16, name="ones")
         nc.vector.memset(ones[:], 1.0)
+        nc.vector.memset(brow[:], 0.0)
+        warm = const.tile([P, 1], F32, name="warm")
+        nc.scalar.activation(out=warm[:], in_=one[:], func=ACT.Ln)
 
         def load_x(b):
             nc.sync.dma_start(
@@ -58,17 +64,17 @@ def tile_model_pa_t_kernel(tc, q, k, x3, Wv, bv, inv_scale, dropout_mask, out):
             nc.sync.dma_start(out=k_raw[:, b], in_=k[b].rearrange("(t p) d -> p t d", p=P))
 
         inv_view = inv_scale.rearrange("(p i) k -> p i k", i=4)
-        nc.sync.dma_start(out=inv_raw[:, 0:1], in_=inv_view[:, 0:1])
         w_view = Wv.rearrange("(j p) d -> p j d", p=P)
-        nc.sync.dma_start(out=w_raw[:, 0:4], in_=w_view[:, 0:4])
+        nc.sync.dma_start(out=inv_raw[:, 0:1], in_=inv_view[:, 0:1])
         nc.sync.dma_start(out=inv_raw[:, 1:4], in_=inv_view[:, 1:4])
-        load_qk(0)
+        nc.sync.dma_start(out=w_raw[:, 0:4], in_=w_view[:, 0:4])
         nc.sync.dma_start(out=w_raw[:, 4:8], in_=w_view[:, 4:8])
-        nc.sync.dma_start(out=brow[0:1, :], in_=bv.rearrange("(o n) -> o n", o=1))
         load_x(0)
-        load_m(0)
-        load_qk(1)
+        load_qk(0)
         load_x(1)
+        load_qk(1)
+        nc.sync.dma_start(out=brow[0:1, :], in_=bv.rearrange("(o n) -> o n", o=1))
+        load_m(0)
         load_m(1)
         for b in range(2, B):
             load_qk(b)
@@ -115,7 +121,11 @@ def tile_model_pa_t_kernel(tc, q, k, x3, Wv, bv, inv_scale, dropout_mask, out):
                 elif h == 0:
                     live["xg", b] = stage(b - 2)[:, 0 : 4 * S]
                 xgw = live["xg", b].bitcast(F32).rearrange("p (h t r u) -> p h t r u", h=2, t=2, u=2)
-                nc.scalar.copy(out=xgw[:, h], in_=live["xt", b, h][:].rearrange("p t u r -> p t r u"))
+                words = live["xt", b, h][:].rearrange("p t u r -> p t r u")
+                if b < X_ON_VECTOR:
+                    nc.vector.tensor_copy(out=xgw[:, h], in_=words)
+                else:
+                    nc.scalar.copy(out=xgw[:, h], in_=words)
 
         def qk_transpose(b):
             if there(b):
@@ -157,31 +167,34 @@ def tile_model_pa_t_kernel(tc, q, k, x3, Wv, bv, inv_scale, dropout_mask, out):
                     )
                 live["vp", b, c] = vp
 
+        def values(b):
+            if ("vg", b) not in live:
+                live["vg", b] = const.tile([P, DV, 4], BF16, name="vg", align_bytes=64)
+            return live["vg", b]
+
         def v_drain(b, c):
             if there(b):
-                if c == 0:
-                    live["vg", b] = const.tile([P, DV, 4], BF16, name="vg", align_bytes=64)
                 cols = slice(P * c, P * c + P)
                 nc.vector.tensor_tensor(
-                    out=live["vg", b][:, cols, :],
+                    out=values(b)[:, cols, :],
                     in0=live["vp", b, c][:].rearrange("p t c -> p c t"),
                     in1=bias[:, cols].unsqueeze(2).to_broadcast([P, P, 4]),
                     op=ALU.add,
                 )
 
-        def v_side_copy(b):
+        def v_side_copy(b, c):
             if there(b):
-                v_pass(b, 0, ring_s, "rs")
-                live["vf", b] = work2.tile([P, P, 4], F32, name="vf")
-                nc.scalar.copy(out=live["vf", b][:], in_=live["vp", b, 0][:].rearrange("p t c -> p c t"))
+                v_pass(b, c, ring_s, "rs")
+                live["vf", b, c] = work2.tile([P, P, 4], F32, name="vf")
+                nc.scalar.copy(out=live["vf", b, c][:], in_=live["vp", b, c][:].rearrange("p t c -> p c t"))
 
-        def v_side_add(b):
+        def v_side_add(b, c):
             if there(b):
-                live["vg", b] = const.tile([P, DV, 4], BF16, name="vg", align_bytes=64)
+                cols = slice(P * c, P * c + P)
                 nc.gpsimd.tensor_tensor(
-                    out=live["vg", b][:, 0:P, :],
-                    in0=live["vf", b][:],
-                    in1=bias[:, 0:P].unsqueeze(2).to_broadcast([P, P, 4]),
+                    out=values(b)[:, cols, :],
+                    in0=live["vf", b, c][:],
+                    in1=bias[:, cols].unsqueeze(2).to_broadcast([P, P, 4]),
                     op=ALU.add,
                 )
 
@@ -218,7 +231,7 @@ def tile_model_pa_t_kernel(tc, q, k, x3, Wv, bv, inv_scale, dropout_mask, out):
         def score_max(b, i):
             if there(b):
                 nm = work8.tile([P, 1], F32, name="nm")
-                nc.vector.tensor_reduce(out=nm[:], in_=live["z", b, i][:], axis=AX.X, op=ALU.min)
+                nc.vector.tensor_reduce(out=nm[:], in_=live["z", b, i][:], axis=AX.X, op=ALU.max, negate=True)
                 live["nm", b, i] = nm
 
         def score_exp(b, i):
@@ -231,7 +244,7 @@ def tile_model_pa_t_kernel(tc, q, k, x3, Wv, bv, inv_scale, dropout_mask, out):
                     in_=live["z", b, i][:],
                     func=ACT.Exp,
                     bias=live["nm", b, i][:],
-                    scale=-1.0,
+                    scale=1.0,
                     accum_out=live["rs", b][:, i : i + 1],
                 )
                 pei = work8.tile([P, S], BF16, name="pei")
@@ -379,7 +392,7 @@ def tile_model_pa_t_kernel(tc, q, k, x3, Wv, bv, inv_scale, dropout_mask, out):
                 outs(o, 5, 6)
             v_drain(v, 5)
             fill(1)
-            v_side_copy(v + 1)
+            v_side_copy(v + 1, 0)
             v_drain(v, 6)
             fill(1)
             v_drain(v, 7)
@@ -396,81 +409,64 @@ def tile_model_pa_t_kernel(tc, q, k, x3, Wv, bv, inv_scale, dropout_mask, out):
                 quant_xp(v)
                 quant_v(v, 0)
             quant_v(v, 1)
-            v_side_add(v + 1)
+            v_side_add(v + 1, 0)
 
-        def table_seed(i):
-            x = inv_raw[:, i, :]
-            r0 = work3.tile([P, S], F32, name="r0")
-            nc.scalar.activation(out=r0[:], in_=x, func=ACT.Abs_reciprocal_sqrt)
-            nc.scalar.activation(out=r0[:], in_=r0[:], func=ACT.Square)
-            live["r0", i] = r0
+        def table_ln(i):
+            nc.scalar.activation(out=rinv[:, i, :], in_=inv_raw[:, i, :], func=ACT.Ln)
 
-        def table_product(i, engine):
-            t0 = work2.tile([P, S], F32, name="t0")
-            engine.tensor_tensor(out=t0[:], in0=live["r0", i][:], in1=inv_raw[:, i, :], op=ALU.mult)
-            live["t0", i] = t0
+        def table_exp(i):
+            nc.scalar.activation(out=rinv[:, i, :], in_=rinv[:, i, :], func=ACT.Exp, scale=-1.0)
 
-        def table_step(i):
-            nc.vector.scalar_tensor_tensor(
-                out=rinv[:, i, :], in0=live["t0", i][:], scalar=2.0, in1=live["r0", i][:], op0=ALU.subtract, op1=ALU.mult
-            )
+        def bias_fill():
+            for h in range(2):
+                bp = ring_s.tile([P, 512], F32, name="bp", tag="rs")
+                nc.tensor.matmul(out=bp[:], lhsT=ones[:], rhs=brow[:, 512 * h : 512 * h + 512], start=True, stop=True)
+                nc.scalar.copy(out=bias[:, 512 * h : 512 * h + 512], in_=bp[:])
 
         wg = big.tile([P, 4 * DV], BF16, name="wg", tag="big", align_bytes=64)
         wgw = wg[:].bitcast(F32).rearrange("p (h t r u) -> p h t r u", h=4, t=2, u=2)
 
         def w_step(h):
             wt = word_transposes(w_raw, h)
-            if h < 2:
+            if h < W_ON_VECTOR:
                 nc.vector.tensor_copy(out=wgw[:, h], in_=wt[:].rearrange("p t u r -> p t r u"))
             else:
                 nc.scalar.copy(out=wgw[:, h], in_=wt[:].rearrange("p t u r -> p t r u"))
 
-        table_seed(0)
-        table_product(0, nc.vector)
-        w_step(0)
-        w_step(1)
-        table_step(0)
-        table_seed(1)
-        qk_transpose(0)
-        qk_drain(0)
-        fill(4)
-        table_product(1, nc.vector)
-        score_scale(0, 0)
-        table_step(1)
-        table_seed(2)
-        score_scale(0, 1)
-        score_max(0, 0)
-        table_product(2, nc.gpsimd)
-        score_max(0, 1)
-        table_seed(3)
-        w_step(2)
-        w_step(3)
+        for i in range(4):
+            table_ln(i)
+        for h in range(4):
+            w_step(h)
+        for i in range(4):
+            table_exp(i)
         for h in range(2):
             x_transpose(0, h)
             x_drain(0, h)
-        nc.vector.quantize_mx(out=wc[:].bitcast(FP8X4), scales=ws[:], in_=wg[:])
-        table_product(3, nc.gpsimd)
-        quant_x(0)
-        table_step(2)
-        table_step(3)
-        qk_transpose(1)
-        qk_drain(1)
+        qk_transpose(0)
+        qk_drain(0)
         for h in range(2):
             x_transpose(1, h)
+        fill(4)
+        for h in range(2):
             x_drain(1, h)
-        score_exp(0, 0)
-        score_exp(0, 1)
+        nc.vector.quantize_mx(out=wc[:].bitcast(FP8X4), scales=ws[:], in_=wg[:])
+        quant_x(0)
+        qk_transpose(1)
+        qk_drain(1)
+        score_scale(0, 0)
+        score_scale(0, 1)
         quant_x(1)
+        score_max(0, 0)
+        score_exp(0, 0)
+        score_max(0, 1)
+        score_exp(0, 1)
         score_scale(0, 2)
+        bias_fill()
         score_scale(0, 3)
         score_max(0, 2)
         score_exp(0, 2)
         score_max(0, 3)
         score_exp(0, 3)
-        for h in range(2):
-            bp = ring_s.tile([P, 512], F32, name="bp", tag="rs")
-            nc.tensor.matmul(out=bp[:], lhsT=ones[:], rhs=brow[:, 512 * h : 512 * h + 512], start=True, stop=True)
-            nc.scalar.copy(out=bias[:, 512 * h : 512 * h + 512], in_=bp[:])
         fill(4)
         qk_transpose(2)
         qk_drain(2)

@@ -14,9 +14,8 @@ AX = mybir.AxisListType
 
 B, S, D, DV, DK = 8, 512, 512, 1024, 128
 P = 128
-W_ON_VECTOR = 4
-X_ON_VECTOR = 1
 FLOPS = 2 * B * (S * D * DV + S * S * DK + S * S * DV)
+SIDE = {1: (0, 1), 2: (0,), 3: (0, 1), 4: (0,), 5: (0, 1), 6: (0,), 7: (0,)}
 
 
 def tile_model_pa_t_kernel(tc, q, k, x3, Wv, bv, inv_scale, dropout_mask, out):
@@ -41,12 +40,10 @@ def tile_model_pa_t_kernel(tc, q, k, x3, Wv, bv, inv_scale, dropout_mask, out):
         q_raw = const.tile([P, B, 4, DK], BF16, name="q_raw")
         inv_raw = const.tile([P, 4, S], BF16, name="inv_raw")
         w_raw = big.tile([P, 8, D], BF16, name="w_raw", tag="big", align_bytes=64)
+        bias = const.tile([P, DV], BF16, name="bias")
+
         one = const.tile([P, 1], F32, name="one")
         nc.vector.memset(one[:], 1.0)
-        brow = const.tile([P, DV], BF16, name="brow")
-        ones = const.tile([P, P], BF16, name="ones")
-        nc.vector.memset(ones[:], 1.0)
-        nc.vector.memset(brow[:], 0.0)
         warm = const.tile([P, 1], F32, name="warm")
         nc.scalar.activation(out=warm[:], in_=one[:], func=ACT.Ln)
 
@@ -65,16 +62,28 @@ def tile_model_pa_t_kernel(tc, q, k, x3, Wv, bv, inv_scale, dropout_mask, out):
 
         inv_view = inv_scale.rearrange("(p i) k -> p i k", i=4)
         w_view = Wv.rearrange("(j p) d -> p j d", p=P)
-        nc.sync.dma_start(out=inv_raw[:, 0:1], in_=inv_view[:, 0:1])
-        nc.sync.dma_start(out=inv_raw[:, 1:4], in_=inv_view[:, 1:4])
-        nc.sync.dma_start(out=w_raw[:, 0:4], in_=w_view[:, 0:4])
-        nc.sync.dma_start(out=w_raw[:, 4:8], in_=w_view[:, 4:8])
-        load_x(0)
+
+        def load_inv(first, last):
+            nc.sync.dma_start(out=inv_raw[:, first:last], in_=inv_view[:, first:last])
+
+        def load_w(first, last):
+            nc.sync.dma_start(out=w_raw[:, first:last], in_=w_view[:, first:last])
+
+        def load_bias():
+            nc.sync.dma_start(out=bias[:], in_=bv.partition_broadcast(P))
+
+        load_inv(0, 2)
+        load_inv(2, 4)
+        load_w(0, 2)
+        load_w(2, 4)
+        load_w(4, 6)
+        load_w(6, 8)
         load_qk(0)
+        load_x(0)
+        load_bias()
         load_x(1)
-        load_qk(1)
-        nc.sync.dma_start(out=brow[0:1, :], in_=bv.rearrange("(o n) -> o n", o=1))
         load_m(0)
+        load_qk(1)
         load_m(1)
         for b in range(2, B):
             load_qk(b)
@@ -82,82 +91,61 @@ def tile_model_pa_t_kernel(tc, q, k, x3, Wv, bv, inv_scale, dropout_mask, out):
             load_m(b)
 
         id_b = const.tile([P, P], BF16, name="id_b")
-        make_identity(nc, id_b[:])
         id_f = const.tile([P, P], F32, name="id_f")
         make_identity(nc, id_f[:])
+        make_identity(nc, id_b[:])
         rinv = const.tile([P, 4, S], F32, name="rinv")
-        bias = const.tile([P, DV], F32, name="bias")
         wc = const.tile([P, DV], U32, name="wc", align_bytes=64)
         ws = const.tile([P, DV], U8, name="ws", align_bytes=64)
-
         live = {}
 
         def there(b):
             return 0 <= b < B
 
-        def word_transposes(src, h):
-            xt = ring_s.tile([P, 2, 2, P], F32, name="xt", tag="rs")
+        def bank(engine, shape, dtype, name):
+            pool, tag = (ring_v, "rv") if engine == "V" else (ring_s, "rs")
+            return pool.tile(shape, dtype, name=name, tag=tag)
+
+        def fill_words(engine, sources):
+            words = bank(engine, [P, 2, 2, P], F32, "words")
             for t in range(2):
                 for u in range(2):
                     nc.tensor.transpose(
-                        xt[:, t, u, :], src[:, 2 * h + t, :].bitcast(F32)[:, P * u : P * u + P], id_f[:]
+                        words[:, t, u, :], sources[t].bitcast(F32)[:, P * u : P * u + P], id_f[:]
                     )
-            return xt
+            return words
 
-        def x_transpose(b, h):
-            if there(b):
-                live["xt", b, h] = word_transposes(x_raw[b], h)
-
-        def stage(b):
-            if ("xp", b) not in live:
-                live["xp", b] = work2.tile([P, 8 * S], BF16, name="xp", align_bytes=64)
-            return live["xp", b]
-
-        def x_drain(b, h):
-            if there(b):
-                if h == 0 and b < 2:
-                    xg = work2.tile([P, 4 * S], BF16, name="xg", tag="xp", align_bytes=64)
-                    live["xg", b] = xg[:]
-                elif h == 0:
-                    live["xg", b] = stage(b - 2)[:, 0 : 4 * S]
-                xgw = live["xg", b].bitcast(F32).rearrange("p (h t r u) -> p h t r u", h=2, t=2, u=2)
-                words = live["xt", b, h][:].rearrange("p t u r -> p t r u")
-                if b < X_ON_VECTOR:
-                    nc.vector.tensor_copy(out=xgw[:, h], in_=words)
-                else:
-                    nc.scalar.copy(out=xgw[:, h], in_=words)
-
-        def qk_transpose(b):
-            if there(b):
-                qk_ps = ring_s.tile([P, 8, P], BF16, name="qk_ps", tag="rs")
-                for i in range(4):
-                    nc.tensor.transpose(qk_ps[:, i, :], q_raw[:, b, i, :], id_b[:])
-                for t in range(4):
-                    nc.tensor.transpose(qk_ps[:, 4 + t, :], k_raw[:, b, t, :], id_b[:])
-                live["qk_ps", b] = qk_ps
-
-        def qk_drain(b):
-            if there(b):
-                live["qkT", b] = work3.tile([P, 8, P], BF16, name="qkT")
-                nc.scalar.copy(out=live["qkT", b][:], in_=live["qk_ps", b][:])
-
-        def quant_x(b):
-            if there(b):
-                xc = work3.tile([P, S], U32, name="xc", tag="xpc", align_bytes=64)
-                xs = work3.tile([P, S], U8, name="xs", tag="xps", align_bytes=64)
-                live["xc", b], live["xs", b] = xc[:], xs[:]
-                nc.vector.quantize_mx(
-                    out=live["xc", b].bitcast(FP8X4), scales=live["xs", b], in_=live["xg", b]
+        def fill(step):
+            kind, engine, b, i = step
+            if kind == "w":
+                live[step] = fill_words(engine, [w_raw[:, 2 * i + t, :] for t in range(2)])
+            elif kind == "x":
+                live[step] = fill_words(engine, [x_raw[b][:, 2 * i + t, :] for t in range(2)])
+            elif kind == "p":
+                live[step] = fill_words(engine, [live["pe", b, 2 * i + t][:] for t in range(2)])
+            elif kind == "qk":
+                heads = bank(engine, [P, 8, P], BF16, "heads")
+                for t in range(8):
+                    src = q_raw[:, b, t, :] if t < 4 else k_raw[:, b, t - 4, :]
+                    nc.tensor.transpose(heads[:, t, :], src, id_b[:])
+                live[step] = heads
+            elif kind == "scale":
+                scores = bank(engine, [P, S], F32, "scores")
+                nc.tensor.matmul(
+                    out=scores[:],
+                    lhsT=live["qkT", b][:, i, :],
+                    rhs=live["qkT", b][:, 4:8, :].rearrange("p t c -> p (t c)"),
+                    start=True,
+                    stop=True,
                 )
-
-        def v_pass(b, c, ring, tag):
-            if there(b):
-                cols = slice(P * c, P * c + P)
-                vp = ring.tile([P, 4, P], F32, name="vp", tag=tag)
+                live[step] = scores
+            elif kind in ("value", "side"):
+                cols = slice(P * i, P * i + P)
+                sums = bank(engine, [P, 4, P], F32, "sums")
                 for t in range(4):
                     keys = slice(P * t, P * t + P)
                     nc.tensor.matmul_mx(
-                        out=vp[:, t, :],
+                        out=sums[:, t, :],
                         lhsT=live["xc", b][:, keys].bitcast(FP8X4),
                         lhsT_scale=live["xs", b][:, keys],
                         rhs=wc[:, cols].bitcast(FP8X4),
@@ -165,77 +153,101 @@ def tile_model_pa_t_kernel(tc, q, k, x3, Wv, bv, inv_scale, dropout_mask, out):
                         start=True,
                         stop=True,
                     )
-                live["vp", b, c] = vp
-
-        def values(b):
-            if ("vg", b) not in live:
-                live["vg", b] = const.tile([P, DV, 4], BF16, name="vg", align_bytes=64)
-            return live["vg", b]
-
-        def v_drain(b, c):
-            if there(b):
-                cols = slice(P * c, P * c + P)
-                nc.vector.tensor_tensor(
-                    out=values(b)[:, cols, :],
-                    in0=live["vp", b, c][:].rearrange("p t c -> p c t"),
-                    in1=bias[:, cols].unsqueeze(2).to_broadcast([P, P, 4]),
-                    op=ALU.add,
-                )
-
-        def v_side_copy(b, c):
-            if there(b):
-                v_pass(b, c, ring_s, "rs")
-                live["vf", b, c] = work2.tile([P, P, 4], F32, name="vf")
-                nc.scalar.copy(out=live["vf", b, c][:], in_=live["vp", b, c][:].rearrange("p t c -> p c t"))
-
-        def v_side_add(b, c):
-            if there(b):
-                cols = slice(P * c, P * c + P)
-                nc.gpsimd.tensor_tensor(
-                    out=values(b)[:, cols, :],
-                    in0=live["vf", b, c][:],
-                    in1=bias[:, cols].unsqueeze(2).to_broadcast([P, P, 4]),
-                    op=ALU.add,
-                )
-
-        def quant_v(b, h):
-            if there(b):
-                if h == 0:
-                    live["vc", b] = work2.tile([P, DV], U32, name="vc", align_bytes=64)
-                    live["vs", b] = work2.tile([P, DV], U8, name="vs", align_bytes=64)
+                live[step] = sums
+            elif kind == "out":
+                h, t = divmod(i, 4)
+                rows = slice(P * t, P * t + P)
                 cols = slice(512 * h, 512 * h + 512)
-                nc.vector.quantize_mx(
-                    out=live["vc", b][:, cols].bitcast(FP8X4),
-                    scales=live["vs", b][:, cols],
-                    in_=live["vg", b][:, cols, :].rearrange("p c t -> p (c t)"),
-                )
-
-        def score_pass(b, i):
-            if there(b):
-                sp = ring_v.tile([P, S], F32, name="sp", tag="rv")
-                nc.tensor.matmul(
-                    out=sp[:],
-                    lhsT=live["qkT", b][:, i, :],
-                    rhs=live["qkT", b][:, 4:8, :].rearrange("p t c -> p (t c)"),
+                sums = bank(engine, [P, 512], F32, "out_sums")
+                nc.tensor.matmul_mx(
+                    out=sums[:],
+                    lhsT=live["pc", b][:, rows].bitcast(FP8X4),
+                    lhsT_scale=live["ps", b][:, rows],
+                    rhs=live["vc", b][:, cols].bitcast(FP8X4),
+                    rhs_scale=live["vs", b][:, cols],
                     start=True,
                     stop=True,
                 )
-                live["sp", b, i] = sp
+                live[step] = sums
 
-        def score_scale(b, i):
-            if there(b):
+        def ready(step):
+            kind, engine, b, i = step
+            needs = {
+                "p": [("pe", b, 2 * i + 1)],
+                "scale": [("qkT", b)],
+                "value": [("xc", b), "wc"],
+                "side": [("xc", b), "wc"],
+                "out": [("pc", b), ("vq", b, i // 4)],
+            }
+            return all(n in live for n in needs.get(kind, []))
+
+        has_bank = ("w", "x", "p", "qk", "scale", "value", "side", "out")
+
+        def copy(engine, out, in_):
+            if engine == "V":
+                nc.vector.tensor_copy(out=out, in_=in_)
+            else:
+                nc.scalar.copy(out=out, in_=in_)
+
+        def stage(b):
+            if ("xp", b) not in live:
+                live["xp", b] = work2.tile([P, 8 * S], BF16, name="xp", align_bytes=64)
+            return live["xp", b]
+
+        def x_stage(b):
+            if b >= 2:
+                return stage(b - 2)[:, 0 : 4 * S]
+            if ("xg", b) not in live:
+                xg = work2.tile([P, 4 * S], BF16, name="xg", tag="xp", align_bytes=64)
+                live["xg", b] = xg[:]
+            return live["xg", b]
+
+        def values(b):
+            if ("vg", b) not in live:
+                live["vg", b] = work2.tile([P, DV, 4], BF16, name="vg", align_bytes=64)
+            return live["vg", b]
+
+        def side_tiles(b):
+            return SIDE.get(b, ())
+
+        wg = big.tile([P, 4 * DV], BF16, name="wg", tag="big", align_bytes=64)
+
+        def words_to(target, engine, step, i):
+            words = target.bitcast(F32).rearrange("p (h t r u) -> p h t r u", t=2, u=2, r=P)
+            copy(engine, words[:, i], live[step][:].rearrange("p t u r -> p t r u"))
+
+        def work(step):
+            kind, engine, b, i = step
+            if kind == "w":
+                words_to(wg[:], engine, step, i)
+            elif kind == "x":
+                words_to(x_stage(b), engine, step, i)
+            elif kind == "p":
+                words_to(stage(b)[:, 4 * S : 8 * S], engine, step, i)
+            elif kind == "qk":
+                live["qkT", b] = work3.tile([P, 8, P], BF16, name="qkT")
+                copy(engine, live["qkT", b][:], live[step][:])
+            elif kind == "ln":
+                nc.scalar.activation(out=rinv[:, i, :], in_=inv_raw[:, i, :], func=ACT.Ln)
+            elif kind == "recip":
+                nc.scalar.activation(out=rinv[:, i, :], in_=rinv[:, i, :], func=ACT.Exp, scale=-1.0)
+            elif kind == "quant_w":
+                nc.vector.quantize_mx(out=wc[:].bitcast(FP8X4), scales=ws[:], in_=wg[:])
+                live["wc"] = True
+            elif kind == "quant_x":
+                xc = work3.tile([P, S], U32, name="xc", tag="xpc", align_bytes=64)
+                xs = work3.tile([P, S], U8, name="xs", tag="xps", align_bytes=64)
+                live["xc", b], live["xs", b] = xc[:], xs[:]
+                nc.vector.quantize_mx(out=live["xc", b].bitcast(FP8X4), scales=live["xs", b], in_=x_stage(b))
+            elif kind == "scale":
                 z = work4.tile([P, S], F32, name="z")
-                nc.vector.tensor_tensor(out=z[:], in0=live["sp", b, i][:], in1=rinv[:, i, :], op=ALU.mult)
+                nc.vector.tensor_tensor(out=z[:], in0=live[step][:], in1=rinv[:, i, :], op=ALU.mult)
                 live["z", b, i] = z
-
-        def score_max(b, i):
-            if there(b):
+            elif kind == "max":
                 nm = work8.tile([P, 1], F32, name="nm")
                 nc.vector.tensor_reduce(out=nm[:], in_=live["z", b, i][:], axis=AX.X, op=ALU.max, negate=True)
                 live["nm", b, i] = nm
-
-        def score_exp(b, i):
-            if there(b):
+            elif kind == "exp":
                 if i == 0:
                     live["rs", b] = work4.tile([P, 4], F32, name="rs")
                 e = work4.tile([P, S], F32, name="e")
@@ -250,32 +262,47 @@ def tile_model_pa_t_kernel(tc, q, k, x3, Wv, bv, inv_scale, dropout_mask, out):
                 pei = work8.tile([P, S], BF16, name="pei")
                 nc.gpsimd.tensor_tensor(out=pei[:], in0=e[:], in1=m_raw[b][:, i, :], op=ALU.mult)
                 live["pe", b, i] = pei
-
-        def recip_rowsum(b):
-            if there(b):
+            elif kind == "value":
+                cols = slice(P * i, P * i + P)
+                nc.vector.tensor_tensor(
+                    out=values(b)[:, cols, :],
+                    in0=live[step][:].rearrange("p t c -> p c t"),
+                    in1=bias[:, cols].unsqueeze(2).to_broadcast([P, P, 4]),
+                    op=ALU.add,
+                )
+            elif kind == "side":
+                if ("vf", b) not in live:
+                    live["vf", b] = work2.tile([P, P * len(side_tiles(b)), 4], F32, name="vf")
+                at = side_tiles(b).index(i)
+                nc.scalar.copy(
+                    out=live["vf", b][:, P * at : P * at + P, :], in_=live[step][:].rearrange("p t c -> p c t")
+                )
+            elif kind == "side_add":
+                n = len(side_tiles(b))
+                cols = slice(P * side_tiles(b)[0], P * side_tiles(b)[0] + P * n)
+                nc.gpsimd.tensor_tensor(
+                    out=values(b)[:, cols, :],
+                    in0=live["vf", b][:],
+                    in1=bias[:, cols].unsqueeze(2).to_broadcast([P, P * n, 4]),
+                    op=ALU.add,
+                )
+            elif kind == "quant_v":
+                if ("vc", b) not in live:
+                    live["vc", b] = work2.tile([P, DV], U32, name="vc", align_bytes=64)
+                    live["vs", b] = work2.tile([P, DV], U8, name="vs", align_bytes=64)
+                cols = slice(512 * i, 512 * i + 512)
+                nc.vector.quantize_mx(
+                    out=live["vc", b][:, cols].bitcast(FP8X4),
+                    scales=live["vs", b][:, cols],
+                    in_=live["vg", b][:, cols, :].rearrange("p c t -> p (c t)"),
+                )
+                live["vq", b, i] = True
+            elif kind == "quant_xp":
                 live["rr", b] = work4.tile([P, 4], F32, name="rr")
                 nc.vector.reciprocal(out=live["rr", b][:], in_=live["rs", b][:])
-
-        def p_transpose(b, h):
-            if there(b):
-                pt = ring_s.tile([P, 2, 2, P], F32, name="pt", tag="rs")
-                for ii in range(2):
-                    for u in range(2):
-                        nc.tensor.transpose(
-                            pt[:, ii, u, :], live["pe", b, 2 * h + ii][:].bitcast(F32)[:, P * u : P * u + P], id_f[:]
-                        )
-                live["pt", b, h] = pt
-
-        def p_drain(b, h):
-            if there(b):
-                pgw = stage(b)[:, 4 * S : 8 * S].bitcast(F32).rearrange("p (h i r u) -> p h i r u", h=2, i=2, u=2)
-                nc.scalar.copy(out=pgw[:, h], in_=live["pt", b, h][:].rearrange("p i u r -> p i r u"))
-
-        def quant_xp(b):
-            if there(b):
                 codes = work3.tile([P, 2 * S], U32, name="xpc", align_bytes=64)
                 scales = work3.tile([P, 2 * S], U8, name="xps", align_bytes=64)
-                first = 0 if there(b + 2) else S
+                first = 0 if b + 2 < B else S
                 nc.vector.quantize_mx(
                     out=codes[:, first : 2 * S].bitcast(FP8X4),
                     scales=scales[:, first : 2 * S],
@@ -283,193 +310,176 @@ def tile_model_pa_t_kernel(tc, q, k, x3, Wv, bv, inv_scale, dropout_mask, out):
                 )
                 live["xc", b + 2], live["xs", b + 2] = codes[:, 0:S], scales[:, 0:S]
                 live["pc", b], live["ps", b] = codes[:, S : 2 * S], scales[:, S : 2 * S]
-
-        def out_pass(b, j):
-            if there(b):
-                h, i = divmod(j, 4)
-                rows = slice(P * i, P * i + P)
-                cols = slice(512 * h, 512 * h + 512)
-                op = ring_s.tile([P, 512], F32, name="op", tag="rs")
-                nc.tensor.matmul_mx(
-                    out=op[:],
-                    lhsT=live["pc", b][:, rows].bitcast(FP8X4),
-                    lhsT_scale=live["ps", b][:, rows],
-                    rhs=live["vc", b][:, cols].bitcast(FP8X4),
-                    rhs_scale=live["vs", b][:, cols],
-                    start=True,
-                    stop=True,
-                )
-                live["op", b, j] = op
-
-        def out_drain(b, j):
-            if there(b):
-                h, i = divmod(j, 4)
-                if j == 0:
+            elif kind == "out":
+                h, t = divmod(i, 4)
+                if ("o", b) not in live:
                     live["o", b] = big.tile([P, 4, DV], F32, name="o", tag="big", align_bytes=64)
-                dst = live["o", b][:, i, 512 * h : 512 * h + 512]
-                scale = live["rr", b][:, i : i + 1]
-                if b == B - 1 and j in (3, 5, 7):
-                    nc.vector.tensor_scalar_mul(out=dst, in0=live["op", b, j][:], scalar1=scale)
+                dst = live["o", b][:, t, 512 * h : 512 * h + 512]
+                scale = live["rr", b][:, t : t + 1]
+                if engine == "V":
+                    nc.vector.tensor_scalar_mul(out=dst, in0=live[step][:], scalar1=scale)
                 else:
-                    nc.scalar.activation(out=dst, in_=live["op", b, j][:], func=ACT.Copy, scale=scale)
+                    nc.scalar.activation(out=dst, in_=live[step][:], func=ACT.Copy, scale=scale)
                 rows_of = out[b].rearrange("(p i) n -> p i n", i=4)
-                nc.sync.dma_start(out=rows_of[:, i, 512 * h : 512 * h + 512], in_=dst)
+                nc.sync.dma_start(out=rows_of[:, t, 512 * h : 512 * h + 512], in_=dst)
 
-        users = []
-        for n in range(-1, B):
-            for i in range(4):
-                users.append(("s", n + 1, i))
-            for c in range(0 if n == 0 else 1, 8):
-                users.append(("v", n, c))
-        users = [u for u in users if there(u[1])]
+        plan = []
 
-        def fill(count):
-            for u in range(count):
-                if users:
-                    kind, b, at = users.pop(0)
-                    if kind == "s":
-                        score_pass(b, at)
-                    else:
-                        v_pass(b, at, ring_v, "rv")
+        def add(kind, b, *indices, on=None):
+            engine = on or ("S" if kind in ("x", "p", "qk", "ln", "recip", "exp", "side", "out") else "G" if kind == "side_add" else "V")
+            for i in indices or (0,):
+                if 0 <= b < B and not (kind == "value" and i in side_tiles(b)):
+                    plan.append((kind, engine, b, i))
 
-        def outs(b, first, last):
-            for j in range(first, last) if there(b) else ():
-                out_pass(b, j)
-                out_drain(b, j)
+        EARLY_V = 0
+        add("w", 0, 0, on="V")
+        add("ln", 0, 0, 1)
+        add("w", 0, 1, on="V")
+        add("ln", 0, 2, 3)
+        add("w", 0, 2, on="V")
+        add("w", 0, 3, on="V")
+        add("recip", 0, 0)
+        add("qk", 0, on="V")
+        add("recip", 0, 1, 2, 3)
+        add("quant_w", 0)
+        add("scale", 0, 0, 1)
+        add("x", 0, 0, on="S")
+        add("max", 0, 0)
+        add("x", 0, 1, on="S")
+        add("max", 0, 1)
+        add("exp", 0, 0, 1)
+        add("quant_x", 0)
+        add("scale", 0, 2, 3)
+        add("qk", 1)
+        add("max", 0, 2)
+        add("exp", 0, 2)
+        add("max", 0, 3)
+        add("exp", 0, 3)
+        add("x", 1, 0, 1)
+        add("qk", 2)
+        for c in side_tiles(0):
+            add("side", 0, c)
+        if side_tiles(0):
+            add("side_add", 0)
+        def val(b, *tiles):
+            add("value", b, *[c for c in tiles if b > 0 or c >= EARLY_V])
 
-        def period(n):
+        for n in range(B - 2):
             s, v, o = n + 1, n, n - 1
-            x = n + 3 if n > 0 else 2
-            outs(o, 0, 3)
-            score_scale(s, 0)
-            fill(1)
-            score_scale(s, 1)
-            fill(1)
-            score_max(s, 0)
-            score_exp(s, 0)
-            x_transpose(x, 0)
-            x_drain(x, 0)
-            score_scale(s, 2)
-            fill(1)
-            score_max(s, 1)
-            score_exp(s, 1)
-            outs(o, 3, 4)
-            score_scale(s, 3)
-            fill(1)
-            score_max(s, 2)
-            score_exp(s, 2)
-            x_transpose(x, 1)
-            x_drain(x, 1)
-            if v == 0:
-                v_drain(0, 0)
-                fill(1)
-            v_drain(v, 1)
-            fill(1)
-            score_max(s, 3)
-            score_exp(s, 3)
-            outs(o, 4, 5)
-            v_drain(v, 2)
-            fill(1)
-            if v == 0:
-                for h in range(2):
-                    p_transpose(0, h)
-                    p_drain(0, h)
-            v_drain(v, 3)
-            fill(1)
-            qk_transpose(n + 3)
-            qk_drain(n + 3)
-            if v == B - 1:
-                outs(o, 5, 8)
-                recip_rowsum(v)
-                quant_xp(v)
-                quant_v(v, 0)
-                outs(v, 0, 3)
-            p_transpose(s, 0)
-            p_drain(s, 0)
-            v_drain(v, 4)
-            fill(1)
-            if v < B - 1:
-                outs(o, 5, 6)
-            v_drain(v, 5)
-            fill(1)
-            v_side_copy(v + 1, 0)
-            v_drain(v, 6)
-            fill(1)
-            v_drain(v, 7)
-            fill(1)
-            p_transpose(s, 1)
-            p_drain(s, 1)
-            if v == 0:
-                for h in range(2):
-                    x_transpose(3, h)
-                    x_drain(3, h)
-            if v < B - 1:
-                outs(o, 6, 8)
-                recip_rowsum(v)
-                quant_xp(v)
-                quant_v(v, 0)
-            quant_v(v, 1)
-            v_side_add(v + 1, 0)
+            add("out", o, 0, 1)
+            add("scale", s, 0, 1)
+            add("max", s, 0)
+            add("exp", s, 0)
+            add("out", o, 2)
+            add("scale", s, 2)
+            add("max", s, 1)
+            add("exp", s, 1)
+            add("p", v, 0)
+            add("scale", s, 3)
+            add("max", s, 2)
+            add("exp", s, 2)
+            add("p", v, 1)
+            val(v, 0, 1)
+            add("x", v + 2, 0)
+            val(v, 2)
+            add("max", s, 3)
+            add("exp", s, 3)
+            add("x", v + 2, 1)
+            val(v, 3)
+            add("out", o, 3, 4)
+            val(v, 4)
+            add("out", o, 5)
+            val(v, 5)
+            add("qk", n + 3)
+            val(v, 6)
+            val(v, 7)
+            if n == 0:
+                add("quant_x", 1)
+            add("side", v + 1, *side_tiles(v + 1))
+            add("out", o, 6, 7)
+            add("quant_xp", v)
+            add("quant_v", v, 0, 1)
+            if v + 1 < B and side_tiles(v + 1):
+                add("side_add", v + 1)
+        a, b = B - 2, B - 1
+        add("out", a - 1, 0)
+        add("scale", b, 0, 1)
+        add("p", a, 0)
+        add("max", b, 0)
+        add("exp", b, 0)
+        add("scale", b, 2)
+        add("out", a - 1, 1)
+        add("max", b, 1)
+        add("exp", b, 1)
+        add("p", a, 1)
+        add("scale", b, 3)
+        add("max", b, 2)
+        add("exp", b, 2)
+        add("value", a, 0, 1)
+        add("out", a - 1, 2)
+        add("max", b, 3)
+        add("exp", b, 3)
+        add("value", a, 2, 3)
+        add("out", a - 1, 3, 4)
+        add("side", b, *side_tiles(b))
+        if side_tiles(b):
+            add("side_add", b)
+        add("value", a, 4)
+        add("out", a - 1, 5)
+        add("value", a, 5)
+        add("quant_xp", a)
+        add("quant_v", a, 0)
+        add("out", a - 1, 6)
+        add("value", a, 6)
+        add("out", a - 1, 7)
+        add("value", a, 7)
+        add("p", b, 0)
+        add("out", a, 0)
+        add("value", b, 0, 1)
+        add("quant_v", a, 1)
+        add("out", a, 1)
+        add("p", b, 1)
+        add("value", b, 2)
+        add("out", a, 2)
+        add("value", b, 3)
+        add("out", a, 3)
+        add("quant_xp", b)
+        add("quant_v", b, 0)
+        add("out", a, 4)
+        add("value", b, 4)
+        add("out", a, 5)
+        add("value", b, 5)
+        add("out", a, 6)
+        add("value", b, 6)
+        add("out", a, 7)
+        add("value", b, 7)
+        add("out", b, 0)
+        add("out", b, 1)
+        add("quant_v", b, 1)
+        add("out", b, 2)
+        add("out", b, 3, on="V")
+        add("out", b, 4)
+        add("out", b, 5, on="V")
+        add("out", b, 6)
+        add("out", b, 7, on="V")
 
-        def table_ln(i):
-            nc.scalar.activation(out=rinv[:, i, :], in_=inv_raw[:, i, :], func=ACT.Ln)
 
-        def table_exp(i):
-            nc.scalar.activation(out=rinv[:, i, :], in_=rinv[:, i, :], func=ACT.Exp, scale=-1.0)
-
-        def bias_fill():
-            for h in range(2):
-                bp = ring_s.tile([P, 512], F32, name="bp", tag="rs")
-                nc.tensor.matmul(out=bp[:], lhsT=ones[:], rhs=brow[:, 512 * h : 512 * h + 512], start=True, stop=True)
-                nc.scalar.copy(out=bias[:, 512 * h : 512 * h + 512], in_=bp[:])
-
-        wg = big.tile([P, 4 * DV], BF16, name="wg", tag="big", align_bytes=64)
-        wgw = wg[:].bitcast(F32).rearrange("p (h t r u) -> p h t r u", h=4, t=2, u=2)
-
-        def w_step(h):
-            wt = word_transposes(w_raw, h)
-            if h < W_ON_VECTOR:
-                nc.vector.tensor_copy(out=wgw[:, h], in_=wt[:].rearrange("p t u r -> p t r u"))
-            else:
-                nc.scalar.copy(out=wgw[:, h], in_=wt[:].rearrange("p t u r -> p t r u"))
-
-        for i in range(4):
-            table_ln(i)
-        for h in range(4):
-            w_step(h)
-        for i in range(4):
-            table_exp(i)
-        for h in range(2):
-            x_transpose(0, h)
-            x_drain(0, h)
-        qk_transpose(0)
-        qk_drain(0)
-        for h in range(2):
-            x_transpose(1, h)
-        fill(4)
-        for h in range(2):
-            x_drain(1, h)
-        nc.vector.quantize_mx(out=wc[:].bitcast(FP8X4), scales=ws[:], in_=wg[:])
-        quant_x(0)
-        qk_transpose(1)
-        qk_drain(1)
-        score_scale(0, 0)
-        score_scale(0, 1)
-        quant_x(1)
-        score_max(0, 0)
-        score_exp(0, 0)
-        score_max(0, 1)
-        score_exp(0, 1)
-        score_scale(0, 2)
-        bias_fill()
-        score_scale(0, 3)
-        score_max(0, 2)
-        score_exp(0, 2)
-        score_max(0, 3)
-        score_exp(0, 3)
-        fill(4)
-        qk_transpose(2)
-        qk_drain(2)
-        for n in range(0, B):
-            period(n)
-        outs(B - 1, 3, 8)
+        waiting = {e: [(at, s) for at, s in enumerate(plan) if s[0] in has_bank and s[1] == e] for e in ("V", "S")}
+        free = {"V": 5, "S": 3}
+        reach = {"V": 20, "S": 8}
+        for now, step in enumerate(plan):
+            while True:
+                heads = [
+                    (*waiting[e][0], e)
+                    for e in ("V", "S")
+                    if waiting[e] and free[e] and waiting[e][0][0] <= now + reach[e] and ready(waiting[e][0][1])
+                ]
+                if not heads:
+                    break
+                at, next_step, e = min(heads)
+                waiting[e].pop(0)
+                fill(next_step)
+                free[e] -= 1
+            work(step)
+            if step[0] in has_bank:
+                free[step[1]] += 1

@@ -40,10 +40,14 @@ def tile_model_pa_t_kernel(tc, q, k, x3, Wv, bv, inv_scale, dropout_mask, out):
         q_raw = const.tile([P, B, 4, DK], BF16, name="q_raw")
         inv_raw = const.tile([P, 4, S], BF16, name="inv_raw")
         w_raw = big.tile([P, 8, D], BF16, name="w_raw", tag="big", align_bytes=64)
-        bias = const.tile([P, DV], BF16, name="bias")
+        bias = const.tile([P, DV], F32, name="bias")
+        brow = const.tile([P, DV], BF16, name="brow")
+        ones = const.tile([P, P], BF16, name="ones")
 
         one = const.tile([P, 1], F32, name="one")
         nc.vector.memset(one[:], 1.0)
+        nc.vector.memset(brow[:], 0.0)
+        nc.vector.memset(ones[:], 1.0)
         warm = const.tile([P, 1], F32, name="warm")
         nc.scalar.activation(out=warm[:], in_=one[:], func=ACT.Ln)
 
@@ -70,7 +74,7 @@ def tile_model_pa_t_kernel(tc, q, k, x3, Wv, bv, inv_scale, dropout_mask, out):
             nc.sync.dma_start(out=w_raw[:, first:last], in_=w_view[:, first:last])
 
         def load_bias():
-            nc.sync.dma_start(out=bias[:], in_=bv.partition_broadcast(P))
+            nc.sync.dma_start(out=brow[0:1, :], in_=bv.rearrange("(o n) -> o n", o=1))
 
         load_inv(0, 2)
         load_inv(2, 4)
@@ -79,8 +83,8 @@ def tile_model_pa_t_kernel(tc, q, k, x3, Wv, bv, inv_scale, dropout_mask, out):
         load_w(4, 6)
         load_w(6, 8)
         load_qk(0)
-        load_x(0)
         load_bias()
+        load_x(0)
         load_x(1)
         load_m(0)
         load_qk(1)
@@ -117,7 +121,13 @@ def tile_model_pa_t_kernel(tc, q, k, x3, Wv, bv, inv_scale, dropout_mask, out):
 
         def fill(step):
             kind, engine, b, i = step
-            if kind == "w":
+            if kind == "bias":
+                sums = bank(engine, [P, 512], F32, "bias_sums")
+                nc.tensor.matmul(
+                    out=sums[:], lhsT=ones[:], rhs=brow[:, 512 * i : 512 * i + 512], start=True, stop=True
+                )
+                live[step] = sums
+            elif kind == "w":
                 live[step] = fill_words(engine, [w_raw[:, 2 * i + t, :] for t in range(2)])
             elif kind == "x":
                 live[step] = fill_words(engine, [x_raw[b][:, 2 * i + t, :] for t in range(2)])
@@ -181,7 +191,7 @@ def tile_model_pa_t_kernel(tc, q, k, x3, Wv, bv, inv_scale, dropout_mask, out):
             }
             return all(n in live for n in needs.get(kind, []))
 
-        has_bank = ("w", "x", "p", "qk", "scale", "value", "side", "out")
+        has_bank = ("bias", "w", "x", "p", "qk", "scale", "value", "side", "out")
 
         def copy(engine, out, in_):
             if engine == "V":
@@ -218,7 +228,9 @@ def tile_model_pa_t_kernel(tc, q, k, x3, Wv, bv, inv_scale, dropout_mask, out):
 
         def work(step):
             kind, engine, b, i = step
-            if kind == "w":
+            if kind == "bias":
+                copy(engine, bias[:, 512 * i : 512 * i + 512], live[step][:])
+            elif kind == "w":
                 words_to(wg[:], engine, step, i)
             elif kind == "x":
                 words_to(x_stage(b), engine, step, i)
@@ -326,7 +338,7 @@ def tile_model_pa_t_kernel(tc, q, k, x3, Wv, bv, inv_scale, dropout_mask, out):
         plan = []
 
         def add(kind, b, *indices, on=None):
-            engine = on or ("S" if kind in ("x", "p", "qk", "ln", "recip", "exp", "side", "out") else "G" if kind == "side_add" else "V")
+            engine = on or ("S" if kind in ("bias", "x", "p", "qk", "ln", "recip", "exp", "side", "out") else "G" if kind == "side_add" else "V")
             for i in indices or (0,):
                 if 0 <= b < B and not (kind == "value" and i in side_tiles(b)):
                     plan.append((kind, engine, b, i))
@@ -347,6 +359,7 @@ def tile_model_pa_t_kernel(tc, q, k, x3, Wv, bv, inv_scale, dropout_mask, out):
         add("max", 0, 0)
         add("x", 0, 1, on="S")
         add("max", 0, 1)
+        add("bias", 0, 0, 1)
         add("exp", 0, 0, 1)
         add("quant_x", 0)
         add("scale", 0, 2, 3)

@@ -16,6 +16,7 @@ B, S, D, DV, DK = 8, 512, 512, 1024, 128
 P = 128
 FLOPS = 2 * B * (S * D * DV + S * S * DK + S * S * DV)
 SIDE = {1: (0, 1), 2: (0,), 3: (0, 1), 4: (0,), 5: (0, 1), 6: (0,), 7: (0,)}
+GROUPS = {}
 
 
 def tile_model_pa_t_kernel(tc, q, k, x3, Wv, bv, inv_scale, dropout_mask, out):
@@ -41,13 +42,10 @@ def tile_model_pa_t_kernel(tc, q, k, x3, Wv, bv, inv_scale, dropout_mask, out):
         inv_raw = const.tile([P, 4, S], BF16, name="inv_raw")
         w_raw = big.tile([P, 8, D], BF16, name="w_raw", tag="big", align_bytes=64)
         bias = const.tile([P, DV], F32, name="bias")
-        brow = const.tile([P, DV], BF16, name="brow")
-        ones = const.tile([P, P], BF16, name="ones")
+        brow = const.tile([P, 8], BF16, name="brow")
 
         one = const.tile([P, 1], F32, name="one")
         nc.vector.memset(one[:], 1.0)
-        nc.vector.memset(brow[:], 0.0)
-        nc.vector.memset(ones[:], 1.0)
         warm = const.tile([P, 1], F32, name="warm")
         nc.scalar.activation(out=warm[:], in_=one[:], func=ACT.Ln)
 
@@ -65,7 +63,7 @@ def tile_model_pa_t_kernel(tc, q, k, x3, Wv, bv, inv_scale, dropout_mask, out):
             nc.sync.dma_start(out=k_raw[:, b], in_=k[b].rearrange("(t p) d -> p t d", p=P))
 
         inv_view = inv_scale.rearrange("(p i) k -> p i k", i=4)
-        w_view = Wv.rearrange("(j p) d -> p j d", p=P)
+        w_view = Wv.rearrange("(p j) d -> p j d", j=8)
 
         def load_inv(first, last):
             nc.sync.dma_start(out=inv_raw[:, first:last], in_=inv_view[:, first:last])
@@ -74,16 +72,16 @@ def tile_model_pa_t_kernel(tc, q, k, x3, Wv, bv, inv_scale, dropout_mask, out):
             nc.sync.dma_start(out=w_raw[:, first:last], in_=w_view[:, first:last])
 
         def load_bias():
-            nc.sync.dma_start(out=brow[0:1, :], in_=bv.rearrange("(o n) -> o n", o=1))
+            nc.sync.dma_start(out=brow[:], in_=bv.rearrange("(p n) -> p n", n=8))
 
+        load_bias()
         load_inv(0, 2)
         load_inv(2, 4)
         load_w(0, 2)
         load_w(2, 4)
         load_w(4, 6)
-        load_w(6, 8)
         load_qk(0)
-        load_bias()
+        load_w(6, 8)
         load_x(0)
         load_x(1)
         load_m(0)
@@ -96,8 +94,8 @@ def tile_model_pa_t_kernel(tc, q, k, x3, Wv, bv, inv_scale, dropout_mask, out):
 
         id_b = const.tile([P, P], BF16, name="id_b")
         id_f = const.tile([P, P], F32, name="id_f")
-        make_identity(nc, id_f[:])
         make_identity(nc, id_b[:])
+        make_identity(nc, id_f[:])
         rinv = const.tile([P, 4, S], F32, name="rinv")
         wc = const.tile([P, DV], U32, name="wc", align_bytes=64)
         ws = const.tile([P, DV], U8, name="ws", align_bytes=64)
@@ -119,14 +117,24 @@ def tile_model_pa_t_kernel(tc, q, k, x3, Wv, bv, inv_scale, dropout_mask, out):
                     )
             return words
 
+        def group_cols(b, g):
+            first, last = GROUPS.get(b, ((0, 4), (4, 8)))[g]
+            return slice(P * first, P * last)
+
         def fill(step):
             kind, engine, b, i = step
             if kind == "bias":
-                sums = bank(engine, [P, 512], F32, "bias_sums")
-                nc.tensor.matmul(
-                    out=sums[:], lhsT=ones[:], rhs=brow[:, 512 * i : 512 * i + 512], start=True, stop=True
-                )
-                live[step] = sums
+                spread = bank(engine, [P, 4, P], F32, "spread")
+                for t in range(4):
+                    n = 4 * i + t
+                    nc.tensor.matmul(
+                        out=spread[:, t, :],
+                        lhsT=brow[:, n : n + 1].to_broadcast([P, P]),
+                        rhs=id_b[:],
+                        start=True,
+                        stop=True,
+                    )
+                live[step] = spread
             elif kind == "w":
                 live[step] = fill_words(engine, [w_raw[:, 2 * i + t, :] for t in range(2)])
             elif kind == "x":
@@ -165,10 +173,10 @@ def tile_model_pa_t_kernel(tc, q, k, x3, Wv, bv, inv_scale, dropout_mask, out):
                     )
                 live[step] = sums
             elif kind == "out":
-                h, t = divmod(i, 4)
+                g, t = divmod(i, 4)
                 rows = slice(P * t, P * t + P)
-                cols = slice(512 * h, 512 * h + 512)
-                sums = bank(engine, [P, 512], F32, "out_sums")
+                cols = group_cols(b, g)
+                sums = bank(engine, [P, cols.stop - cols.start], F32, "out_sums")
                 nc.tensor.matmul_mx(
                     out=sums[:],
                     lhsT=live["pc", b][:, rows].bitcast(FP8X4),
@@ -229,9 +237,11 @@ def tile_model_pa_t_kernel(tc, q, k, x3, Wv, bv, inv_scale, dropout_mask, out):
         def work(step):
             kind, engine, b, i = step
             if kind == "bias":
-                copy(engine, bias[:, 512 * i : 512 * i + 512], live[step][:])
+                by_eight = bias[:].rearrange("p (c n) -> p c n", n=8)
+                copy(engine, by_eight[:, :, 4 * i : 4 * i + 4], live[step][:].rearrange("p t c -> p c t"))
             elif kind == "w":
-                words_to(wg[:], engine, step, i)
+                words = wg[:].bitcast(F32).rearrange("p (r j u) -> p r j u", j=8, u=2)
+                copy(engine, words[:, :, 2 * i : 2 * i + 2, :], live[step][:].rearrange("p t u r -> p r t u"))
             elif kind == "x":
                 words_to(x_stage(b), engine, step, i)
             elif kind == "p":
@@ -253,11 +263,13 @@ def tile_model_pa_t_kernel(tc, q, k, x3, Wv, bv, inv_scale, dropout_mask, out):
                 nc.vector.quantize_mx(out=live["xc", b].bitcast(FP8X4), scales=live["xs", b], in_=x_stage(b))
             elif kind == "scale":
                 z = work4.tile([P, S], F32, name="z")
-                nc.vector.tensor_tensor(out=z[:], in0=live[step][:], in1=rinv[:, i, :], op=ALU.mult)
+                nc.vector.scalar_tensor_tensor(
+                    out=z[:], in0=live[step][:], scalar=-1.0, in1=rinv[:, i, :], op0=ALU.mult, op1=ALU.mult
+                )
                 live["z", b, i] = z
             elif kind == "max":
                 nm = work8.tile([P, 1], F32, name="nm")
-                nc.vector.tensor_reduce(out=nm[:], in_=live["z", b, i][:], axis=AX.X, op=ALU.max, negate=True)
+                nc.vector.tensor_reduce(out=nm[:], in_=live["z", b, i][:], axis=AX.X, op=ALU.min)
                 live["nm", b, i] = nm
             elif kind == "exp":
                 if i == 0:
@@ -268,7 +280,7 @@ def tile_model_pa_t_kernel(tc, q, k, x3, Wv, bv, inv_scale, dropout_mask, out):
                     in_=live["z", b, i][:],
                     func=ACT.Exp,
                     bias=live["nm", b, i][:],
-                    scale=1.0,
+                    scale=-1.0,
                     accum_out=live["rs", b][:, i : i + 1],
                 )
                 pei = work8.tile([P, S], BF16, name="pei")
@@ -302,7 +314,7 @@ def tile_model_pa_t_kernel(tc, q, k, x3, Wv, bv, inv_scale, dropout_mask, out):
                 if ("vc", b) not in live:
                     live["vc", b] = work2.tile([P, DV], U32, name="vc", align_bytes=64)
                     live["vs", b] = work2.tile([P, DV], U8, name="vs", align_bytes=64)
-                cols = slice(512 * i, 512 * i + 512)
+                cols = group_cols(b, i)
                 nc.vector.quantize_mx(
                     out=live["vc", b][:, cols].bitcast(FP8X4),
                     scales=live["vs", b][:, cols],
@@ -323,35 +335,36 @@ def tile_model_pa_t_kernel(tc, q, k, x3, Wv, bv, inv_scale, dropout_mask, out):
                 live["xc", b + 2], live["xs", b + 2] = codes[:, 0:S], scales[:, 0:S]
                 live["pc", b], live["ps", b] = codes[:, S : 2 * S], scales[:, S : 2 * S]
             elif kind == "out":
-                h, t = divmod(i, 4)
+                g, t = divmod(i, 4)
                 if ("o", b) not in live:
                     live["o", b] = big.tile([P, 4, DV], F32, name="o", tag="big", align_bytes=64)
-                dst = live["o", b][:, t, 512 * h : 512 * h + 512]
+                dst = live["o", b][:, t, group_cols(b, g)]
                 scale = live["rr", b][:, t : t + 1]
                 if engine == "V":
                     nc.vector.tensor_scalar_mul(out=dst, in0=live[step][:], scalar1=scale)
                 else:
                     nc.scalar.activation(out=dst, in_=live[step][:], func=ACT.Copy, scale=scale)
                 rows_of = out[b].rearrange("(p i) n -> p i n", i=4)
-                nc.sync.dma_start(out=rows_of[:, t, 512 * h : 512 * h + 512], in_=dst)
+                nc.sync.dma_start(out=rows_of[:, t, group_cols(b, g)], in_=dst)
 
         plan = []
 
         def add(kind, b, *indices, on=None):
             engine = on or ("S" if kind in ("bias", "x", "p", "qk", "ln", "recip", "exp", "side", "out") else "G" if kind == "side_add" else "V")
-            for i in indices or (0,):
+            for i in indices or (() if kind == "side" else (0,)):
                 if 0 <= b < B and not (kind == "value" and i in side_tiles(b)):
                     plan.append((kind, engine, b, i))
 
         EARLY_V = 0
+        add("bias", 0, 0, 1, on="V")
         add("w", 0, 0, on="V")
         add("ln", 0, 0, 1)
         add("w", 0, 1, on="V")
         add("ln", 0, 2, 3)
         add("w", 0, 2, on="V")
-        add("w", 0, 3, on="V")
         add("recip", 0, 0)
         add("qk", 0, on="V")
+        add("w", 0, 3, on="V")
         add("recip", 0, 1, 2, 3)
         add("quant_w", 0)
         add("scale", 0, 0, 1)
@@ -359,7 +372,6 @@ def tile_model_pa_t_kernel(tc, q, k, x3, Wv, bv, inv_scale, dropout_mask, out):
         add("max", 0, 0)
         add("x", 0, 1, on="S")
         add("max", 0, 1)
-        add("bias", 0, 0, 1)
         add("exp", 0, 0, 1)
         add("quant_x", 0)
         add("scale", 0, 2, 3)

@@ -491,7 +491,7 @@ def tile_model_pa_t_kernel(tc, q, k, x3, Wv, bv, inv_scale, dropout_mask, out):
 
         waiting = {e: [(at, s) for at, s in enumerate(plan) if s[0] in has_bank and s[1] == e] for e in ("V", "S")}
         free = {"V": 5, "S": 3}
-        reach = {"V": 20, "S": 8}
+        reach = {"V": 12, "S": 5}
         for now, step in enumerate(plan):
             while True:
                 heads = [

@@ -17,6 +17,7 @@ P = 128
 FLOPS = 2 * B * (S * D * DV + S * S * DK + S * S * DV)
 SIDE = {1: (0, 1), 2: (0,), 3: (0, 1), 4: (0,), 5: (0, 1), 6: (0,), 7: (0,)}
 GROUPS = {}
+TURN = {0: (0,)}
 
 
 def tile_model_pa_t_kernel(tc, q, k, x3, Wv, bv, inv_scale, dropout_mask, out):
@@ -135,6 +136,36 @@ def tile_model_pa_t_kernel(tc, q, k, x3, Wv, bv, inv_scale, dropout_mask, out):
                         stop=True,
                     )
                 live[step] = spread
+            elif kind == "bias_col":
+                cols = bank(engine, [P, 8], F32, "cols")
+                for c in range(8):
+                    nc.tensor.matmul(
+                        out=cols[:, c : c + 1],
+                        lhsT=bias[:, P * c : P * c + P],
+                        rhs=id_f[:, 0:1],
+                        start=True,
+                        stop=True,
+                    )
+                live[step] = cols
+            elif kind == "turn":
+                sums = bank(engine, [P, S], F32, "turned_sums")
+                nc.tensor.matmul_mx(
+                    out=sums[:],
+                    lhsT=wc[:, P * i : P * i + P].bitcast(FP8X4),
+                    lhsT_scale=ws[:, P * i : P * i + P],
+                    rhs=live["xc", b][:, 0:S].bitcast(FP8X4),
+                    rhs_scale=live["xs", b][:, 0:S],
+                    start=True,
+                    stop=True,
+                )
+                live[step] = sums
+            elif kind == "turn_back":
+                words = bank(engine, [P, 2, P], F32, "back")
+                for u in range(2):
+                    nc.tensor.transpose(
+                        words[:, u, :], live["vt", b, i][:].bitcast(F32)[:, P * u : P * u + P], id_f[:]
+                    )
+                live[step] = words
             elif kind == "w":
                 live[step] = fill_words(engine, [w_raw[:, 2 * i + t, :] for t in range(2)])
             elif kind == "x":
@@ -195,11 +226,14 @@ def tile_model_pa_t_kernel(tc, q, k, x3, Wv, bv, inv_scale, dropout_mask, out):
                 "scale": [("qkT", b)],
                 "value": [("xc", b), "wc"],
                 "side": [("xc", b), "wc"],
+                "turn": [("xc", b), "wc"],
+                "turn_back": [("vt", b, i)],
+                "bias_col": ["bias"],
                 "out": [("pc", b), ("vq", b, i // 4)],
             }
             return all(n in live for n in needs.get(kind, []))
 
-        has_bank = ("bias", "w", "x", "p", "qk", "scale", "value", "side", "out")
+        has_bank = ("bias", "bias_col", "turn", "turn_back", "w", "x", "p", "qk", "scale", "value", "side", "out")
 
         def copy(engine, out, in_):
             if engine == "V":
@@ -239,6 +273,24 @@ def tile_model_pa_t_kernel(tc, q, k, x3, Wv, bv, inv_scale, dropout_mask, out):
             if kind == "bias":
                 by_eight = bias[:].rearrange("p (c n) -> p c n", n=8)
                 copy(engine, by_eight[:, :, 4 * i : 4 * i + 4], live[step][:].rearrange("p t c -> p c t"))
+                if i == 1:
+                    live["bias"] = True
+            elif kind == "bias_col":
+                live["bias_col"] = const.tile([P, 8], F32, name="bias_col")
+                copy(engine, live["bias_col"][:], live[step][:])
+            elif kind == "turn":
+                vt = work2.tile([P, S], BF16, name="vt")
+                nc.scalar.activation(
+                    out=vt[:].rearrange("p (u r e) -> p u r e", u=2, e=2),
+                    in_=live[step][:].rearrange("p (u e r) -> p u r e", u=2, e=2),
+                    func=ACT.Identity,
+                    bias=live["bias_col"][:, i : i + 1],
+                    scale=1.0,
+                )
+                live["vt", b, i] = vt
+            elif kind == "turn_back":
+                back = values(b)[:, P * i : P * i + P, :].rearrange("p c t -> p (c t)").bitcast(F32)
+                copy(engine, back.rearrange("p (c u) -> p c u", u=2), live[step][:].rearrange("p u c -> p c u"))
             elif kind == "w":
                 words = wg[:].bitcast(F32).rearrange("p (r j u) -> p r j u", j=8, u=2)
                 copy(engine, words[:, :, 2 * i : 2 * i + 2, :], live[step][:].rearrange("p t u r -> p r t u"))
@@ -350,9 +402,9 @@ def tile_model_pa_t_kernel(tc, q, k, x3, Wv, bv, inv_scale, dropout_mask, out):
         plan = []
 
         def add(kind, b, *indices, on=None):
-            engine = on or ("S" if kind in ("bias", "x", "p", "qk", "ln", "recip", "exp", "side", "out") else "G" if kind == "side_add" else "V")
-            for i in indices or (() if kind == "side" else (0,)):
-                if 0 <= b < B and not (kind == "value" and i in side_tiles(b)):
+            engine = on or ("S" if kind in ("turn", "turn_back", "bias", "x", "p", "qk", "ln", "recip", "exp", "side", "out") else "G" if kind == "side_add" else "V")
+            for i in indices or (() if kind in ("side", "turn", "turn_back") else (0,)):
+                if 0 <= b < B and not (kind == "value" and (i in side_tiles(b) or i in TURN.get(b, ()))):
                     plan.append((kind, engine, b, i))
 
         EARLY_V = 0
@@ -367,6 +419,7 @@ def tile_model_pa_t_kernel(tc, q, k, x3, Wv, bv, inv_scale, dropout_mask, out):
         add("w", 0, 3, on="V")
         add("recip", 0, 1, 2, 3)
         add("quant_w", 0)
+        add("bias_col", 0, on="V")
         add("scale", 0, 0, 1)
         add("x", 0, 0, on="S")
         add("max", 0, 0)
@@ -410,10 +463,12 @@ def tile_model_pa_t_kernel(tc, q, k, x3, Wv, bv, inv_scale, dropout_mask, out):
             add("max", s, 3)
             add("exp", s, 3)
             add("x", v + 2, 1)
+            add("turn", v, *TURN.get(v, ()))
             val(v, 3)
             add("out", o, 3, 4)
             val(v, 4)
             add("out", o, 5)
+            add("turn_back", v, *TURN.get(v, ()))
             val(v, 5)
             add("qk", n + 3)
             val(v, 6)

@@ -138,7 +138,7 @@ def tile_model_pa_t_kernel(tc, q, k, x3, Wv, bv, inv_scale, dropout_mask, out):
                 live[step] = spread
             elif kind == "bias_col":
                 cols = bank(engine, [P, 8], F32, "cols")
-                for c in range(8):
+                for c in TURN[0]:
                     nc.tensor.matmul(
                         out=cols[:, c : c + 1],
                         lhsT=bias[:, P * c : P * c + P],
@@ -277,7 +277,7 @@ def tile_model_pa_t_kernel(tc, q, k, x3, Wv, bv, inv_scale, dropout_mask, out):
                     live["bias"] = True
             elif kind == "bias_col":
                 live["bias_col"] = const.tile([P, 8], F32, name="bias_col")
-                copy(engine, live["bias_col"][:], live[step][:])
+                copy(engine, live["bias_col"][:, TURN[0][0] : TURN[0][-1] + 1], live[step][:, TURN[0][0] : TURN[0][-1] + 1])
             elif kind == "turn":
                 vt = work2.tile([P, S], BF16, name="vt")
                 nc.scalar.activation(
@@ -419,7 +419,6 @@ def tile_model_pa_t_kernel(tc, q, k, x3, Wv, bv, inv_scale, dropout_mask, out):
         add("w", 0, 3, on="V")
         add("recip", 0, 1, 2, 3)
         add("quant_w", 0)
-        add("bias_col", 0, on="V")
         add("scale", 0, 0, 1)
         add("x", 0, 0, on="S")
         add("max", 0, 0)
@@ -427,6 +426,7 @@ def tile_model_pa_t_kernel(tc, q, k, x3, Wv, bv, inv_scale, dropout_mask, out):
         add("max", 0, 1)
         add("exp", 0, 0, 1)
         add("quant_x", 0)
+        add("bias_col", 0, on="V")
         add("scale", 0, 2, 3)
         add("qk", 1)
         add("max", 0, 2)

from contextlib import ExitStack

import concourse.mybir as mybir
from concourse.masks import make_identity

F32 = mybir.dt.float32
BF16 = mybir.dt.bfloat16
U32 = mybir.dt.uint32
U8 = mybir.dt.uint8
FP8X4 = mybir.dt.float8_e4m3fn_x4
ALU = mybir.AluOpType
ACT = mybir.ActivationFunctionType
AX = mybir.AxisListType

B, S, D, DV, DK = 8, 512, 512, 1024, 128
P = 128
FLOPS = 2 * B * (S * D * DV + S * S * DK + S * S * DV)
SIDE = {1: (0, 1), 2: (0,), 3: (0, 1), 4: (0,), 5: (0, 1), 6: (0,), 7: (0,)}
GROUPS = {}
TURN = {0: (0,)}


def tile_model_pa_t_kernel(tc, q, k, x3, Wv, bv, inv_scale, dropout_mask, out):
    nc = tc.nc
    with ExitStack() as ctx:
        ctx.enter_context(tc.manual_schedule())
        const = ctx.enter_context(tc.tile_pool(name="const", bufs=1))
        big = ctx.enter_context(tc.tile_pool(name="big", bufs=2))
        work2 = ctx.enter_context(tc.tile_pool(name="work2", bufs=2))
        work3 = ctx.enter_context(tc.tile_pool(name="work3", bufs=3))
        work4 = ctx.enter_context(tc.tile_pool(name="work4", bufs=4))
        work8 = ctx.enter_context(tc.tile_pool(name="work8", bufs=8))
        ring_v = ctx.enter_context(tc.psum_pool(name="ring_v", bufs=5))
        ring_s = ctx.enter_context(tc.psum_pool(name="ring_s", bufs=3))

        x_raw = []
        m_raw = []
        for b in range(B):
            x_raw.append(const.tile([P, 4, D], BF16, name="x_raw%d" % b))
            m_raw.append(const.tile([P, 4, S], BF16, name="m_raw%d" % b))
        k_raw = const.tile([P, B, 4, DK], BF16, name="k_raw")
        q_raw = const.tile([P, B, 4, DK], BF16, name="q_raw")
        inv_raw = const.tile([P, 4, S], BF16, name="inv_raw")
        w_raw = big.tile([P, 8, D], BF16, name="w_raw", tag="big", align_bytes=64)
        bias = const.tile([P, DV], F32, name="bias")
        brow = const.tile([P, 8], BF16, name="brow")

        one = const.tile([P, 1], F32, name="one")
        nc.vector.memset(one[:], 1.0)
        warm = const.tile([P, 1], F32, name="warm")
        nc.scalar.activation(out=warm[:], in_=one[:], func=ACT.Ln)

        def load_x(b):
            nc.sync.dma_start(
                out=x_raw[b][:].rearrange("p (u e) d -> p u e d", u=2),
                in_=x3[b].rearrange("(u p e) d -> p u e d", u=2, e=2),
            )

        def load_m(b):
            nc.sync.dma_start(out=m_raw[b][:], in_=dropout_mask[b].rearrange("(p i) k -> p i k", i=4))

        def load_qk(b):
            nc.sync.dma_start(out=q_raw[:, b], in_=q[b].rearrange("(p i) d -> p i d", i=4))
            nc.sync.dma_start(out=k_raw[:, b], in_=k[b].rearrange("(t p) d -> p t d", p=P))

        inv_view = inv_scale.rearrange("(p i) k -> p i k", i=4)
        w_view = Wv.rearrange("(p j) d -> p j d", j=8)

        def load_inv(first, last):
            nc.sync.dma_start(out=inv_raw[:, first:last], in_=inv_view[:, first:last])

        def load_w(first, last):
            nc.sync.dma_start(out=w_raw[:, first:last], in_=w_view[:, first:last])

        def load_bias():
            nc.sync.dma_start(out=brow[:], in_=bv.rearrange("(p n) -> p n", n=8))

        load_bias()
        load_inv(0, 2)
        load_inv(2, 4)
        load_w(0, 2)
        load_w(2, 4)
        load_w(4, 6)
        load_qk(0)
        load_w(6, 8)
        load_x(0)
        load_x(1)
        load_m(0)
        load_qk(1)
        load_m(1)
        for b in range(2, B):
            load_qk(b)
            load_x(b)
            load_m(b)

        id_b = const.tile([P, P], BF16, name="id_b")
        id_f = const.tile([P, P], F32, name="id_f")
        make_identity(nc, id_b[:])
        make_identity(nc, id_f[:])
        rinv = const.tile([P, 4, S], F32, name="rinv")
        wc = const.tile([P, DV], U32, name="wc", align_bytes=64)
        ws = const.tile([P, DV], U8, name="ws", align_bytes=64)
        live = {}

        def there(b):
            return 0 <= b < B

        def bank(engine, shape, dtype, name):
            pool, tag = (ring_v, "rv") if engine == "V" else (ring_s, "rs")
            return pool.tile(shape, dtype, name=name, tag=tag)

        def fill_words(engine, sources):
            words = bank(engine, [P, 2, 2, P], F32, "words")
            for t in range(2):
                for u in range(2):
                    nc.tensor.transpose(
                        words[:, t, u, :], sources[t].bitcast(F32)[:, P * u : P * u + P], id_f[:]
                    )
            return words

        def group_cols(b, g):
            first, last = GROUPS.get(b, ((0, 4), (4, 8)))[g]
            return slice(P * first, P * last)

        def fill(step):
            kind, engine, b, i = step
            if kind == "bias":
                spread = bank(engine, [P, 4, P], F32, "spread")
                for t in range(4):
                    n = 4 * i + t
                    nc.tensor.matmul(
                        out=spread[:, t, :],
                        lhsT=brow[:, n : n + 1].to_broadcast([P, P]),
                        rhs=id_b[:],
                        start=True,
                        stop=True,
                    )
                live[step] = spread
            elif kind == "bias_col":
                cols = bank(engine, [P, 8], F32, "cols")
                for c in TURN[0]:
                    nc.tensor.matmul(
                        out=cols[:, c : c + 1],
                        lhsT=bias[:, P * c : P * c + P],
                        rhs=id_f[:, 0:1],
                        start=True,
                        stop=True,
                    )
                live[step] = cols
            elif kind == "turn":
                sums = bank(engine, [P, S], F32, "turned_sums")
                nc.tensor.matmul_mx(
                    out=sums[:],
                    lhsT=wc[:, P * i : P * i + P].bitcast(FP8X4),
                    lhsT_scale=ws[:, P * i : P * i + P],
                    rhs=live["xc", b][:, 0:S].bitcast(FP8X4),
                    rhs_scale=live["xs", b][:, 0:S],
                    start=True,
                    stop=True,
                )
                live[step] = sums
            elif kind == "turn_back":
                words = bank(engine, [P, 2, P], F32, "back")
                for u in range(2):
                    nc.tensor.transpose(
                        words[:, u, :], live["vt", b, i][:].bitcast(F32)[:, P * u : P * u + P], id_f[:]
                    )
                live[step] = words
            elif kind == "w":
                live[step] = fill_words(engine, [w_raw[:, 2 * i + t, :] for t in range(2)])
            elif kind == "x":
                live[step] = fill_words(engine, [x_raw[b][:, 2 * i + t, :] for t in range(2)])
            elif kind == "p":
                live[step] = fill_words(engine, [live["pe", b, 2 * i + t][:] for t in range(2)])
            elif kind == "qk":
                heads = bank(engine, [P, 8, P], BF16, "heads")
                for t in range(8):
                    src = q_raw[:, b, t, :] if t < 4 else k_raw[:, b, t - 4, :]
                    nc.tensor.transpose(heads[:, t, :], src, id_b[:])
                live[step] = heads
            elif kind == "scale":
                scores = bank(engine, [P, S], F32, "scores")
                nc.tensor.matmul(
                    out=scores[:],
                    lhsT=live["qkT", b][:, i, :],
                    rhs=live["qkT", b][:, 4:8, :].rearrange("p t c -> p (t c)"),
                    start=True,
                    stop=True,
                )
                live[step] = scores
            elif kind in ("value", "side"):
                cols = slice(P * i, P * i + P)
                sums = bank(engine, [P, 4, P], F32, "sums")
                for t in range(4):
                    keys = slice(P * t, P * t + P)
                    nc.tensor.matmul_mx(
                        out=sums[:, t, :],
                        lhsT=live["xc", b][:, keys].bitcast(FP8X4),
                        lhsT_scale=live["xs", b][:, keys],
                        rhs=wc[:, cols].bitcast(FP8X4),
                        rhs_scale=ws[:, cols],
                        start=True,
                        stop=True,
                    )
                live[step] = sums
            elif kind == "out":
                g, t = divmod(i, 4)
                rows = slice(P * t, P * t + P)
                cols = group_cols(b, g)
                sums = bank(engine, [P, cols.stop - cols.start], F32, "out_sums")
                nc.tensor.matmul_mx(
                    out=sums[:],
                    lhsT=live["pc", b][:, rows].bitcast(FP8X4),
                    lhsT_scale=live["ps", b][:, rows],
                    rhs=live["vc", b][:, cols].bitcast(FP8X4),
                    rhs_scale=live["vs", b][:, cols],
                    start=True,
                    stop=True,
                )
                live[step] = sums

        def ready(step):
            kind, engine, b, i = step
            needs = {
                "p": [("pe", b, 2 * i + 1)],
                "scale": [("qkT", b)],
                "value": [("xc", b), "wc"],
                "side": [("xc", b), "wc"],
                "turn": [("xc", b), "wc"],
                "turn_back": [("vt", b, i)],
                "bias_col": ["bias"],
                "out": [("pc", b), ("vq", b, i // 4)],
            }
            return all(n in live for n in needs.get(kind, []))

        has_bank = ("bias", "bias_col", "turn", "turn_back", "w", "x", "p", "qk", "scale", "value", "side", "out")

        def copy(engine, out, in_):
            if engine == "V":
                nc.vector.tensor_copy(out=out, in_=in_)
            else:
                nc.scalar.copy(out=out, in_=in_)

        def stage(b):
            if ("xp", b) not in live:
                live["xp", b] = work2.tile([P, 8 * S], BF16, name="xp", align_bytes=64)
            return live["xp", b]

        def x_stage(b):
            if b >= 2:
                return stage(b - 2)[:, 0 : 4 * S]
            if ("xg", b) not in live:
                xg = work2.tile([P, 4 * S], BF16, name="xg", tag="xp", align_bytes=64)
                live["xg", b] = xg[:]
            return live["xg", b]

        def values(b):
            if ("vg", b) not in live:
                live["vg", b] = work2.tile([P, DV, 4], BF16, name="vg", align_bytes=64)
            return live["vg", b]

        def side_tiles(b):
            return SIDE.get(b, ())

        wg = big.tile([P, 4 * DV], BF16, name="wg", tag="big", align_bytes=64)

        def words_to(target, engine, step, i):
            words = target.bitcast(F32).rearrange("p (h t r u) -> p h t r u", t=2, u=2, r=P)
            copy(engine, words[:, i], live[step][:].rearrange("p t u r -> p t r u"))

        def work(step):
            kind, engine, b, i = step
            if kind == "bias":
                by_eight = bias[:].rearrange("p (c n) -> p c n", n=8)
                copy(engine, by_eight[:, :, 4 * i : 4 * i + 4], live[step][:].rearrange("p t c -> p c t"))
                if i == 1:
                    live["bias"] = True
            elif kind == "bias_col":
                live["bias_col"] = const.tile([P, 8], F32, name="bias_col")
                copy(engine, live["bias_col"][:, TURN[0][0] : TURN[0][-1] + 1], live[step][:, TURN[0][0] : TURN[0][-1] + 1])
            elif kind == "turn":
                vt = work2.tile([P, S], BF16, name="vt")
                nc.scalar.activation(
                    out=vt[:].rearrange("p (u r e) -> p u r e", u=2, e=2),
                    in_=live[step][:].rearrange("p (u e r) -> p u r e", u=2, e=2),
                    func=ACT.Identity,
                    bias=live["bias_col"][:, i : i + 1],
                    scale=1.0,
                )
                live["vt", b, i] = vt
            elif kind == "turn_back":
                back = values(b)[:, P * i : P * i + P, :].rearrange("p c t -> p (c t)").bitcast(F32)
                copy(engine, back.rearrange("p (c u) -> p c u", u=2), live[step][:].rearrange("p u c -> p c u"))
            elif kind == "w":
                words = wg[:].bitcast(F32).rearrange("p (r j u) -> p r j u", j=8, u=2)
                copy(engine, words[:, :, 2 * i : 2 * i + 2, :], live[step][:].rearrange("p t u r -> p r t u"))
            elif kind == "x":
                words_to(x_stage(b), engine, step, i)
            elif kind == "p":
                words_to(stage(b)[:, 4 * S : 8 * S], engine, step, i)
            elif kind == "qk":
                live["qkT", b] = work3.tile([P, 8, P], BF16, name="qkT")
                copy(engine, live["qkT", b][:], live[step][:])
            elif kind == "ln":
                nc.scalar.activation(out=rinv[:, i, :], in_=inv_raw[:, i, :], func=ACT.Ln)
            elif kind == "recip":
                nc.scalar.activation(out=rinv[:, i, :], in_=rinv[:, i, :], func=ACT.Exp, scale=-1.0)
            elif kind == "quant_w":
                nc.vector.quantize_mx(out=wc[:].bitcast(FP8X4), scales=ws[:], in_=wg[:])
                live["wc"] = True
            elif kind == "quant_x":
                xc = work3.tile([P, S], U32, name="xc", tag="xpc", align_bytes=64)
                xs = work3.tile([P, S], U8, name="xs", tag="xps", align_bytes=64)
                live["xc", b], live["xs", b] = xc[:], xs[:]
                nc.vector.quantize_mx(out=live["xc", b].bitcast(FP8X4), scales=live["xs", b], in_=x_stage(b))
            elif kind == "scale":
                z = work4.tile([P, S], F32, name="z")
                nc.vector.scalar_tensor_tensor(
                    out=z[:], in0=live[step][:], scalar=-1.0, in1=rinv[:, i, :], op0=ALU.mult, op1=ALU.mult
                )
                live["z", b, i] = z
            elif kind == "max":
                nm = work8.tile([P, 1], F32, name="nm")
                nc.vector.tensor_reduce(out=nm[:], in_=live["z", b, i][:], axis=AX.X, op=ALU.min)
                live["nm", b, i] = nm
            elif kind == "exp":
                if i == 0:
                    live["rs", b] = work4.tile([P, 4], F32, name="rs")
                e = work4.tile([P, S], F32, name="e")
                nc.scalar.activation(
                    out=e[:],
                    in_=live["z", b, i][:],
                    func=ACT.Exp,
                    bias=live["nm", b, i][:],
                    scale=-1.0,
                    accum_out=live["rs", b][:, i : i + 1],
                )
                pei = work8.tile([P, S], BF16, name="pei")
                nc.gpsimd.tensor_tensor(out=pei[:], in0=e[:], in1=m_raw[b][:, i, :], op=ALU.mult)
                live["pe", b, i] = pei
            elif kind == "value":
                cols = slice(P * i, P * i + P)
                nc.vector.tensor_tensor(
                    out=values(b)[:, cols, :],
                    in0=live[step][:].rearrange("p t c -> p c t"),
                    in1=bias[:, cols].unsqueeze(2).to_broadcast([P, P, 4]),
                    op=ALU.add,
                )
            elif kind == "side":
                if ("vf", b) not in live:
                    live["vf", b] = work2.tile([P, P * len(side_tiles(b)), 4], F32, name="vf")
                at = side_tiles(b).index(i)
                nc.scalar.copy(
                    out=live["vf", b][:, P * at : P * at + P, :], in_=live[step][:].rearrange("p t c -> p c t")
                )
            elif kind == "side_add":
                n = len(side_tiles(b))
                cols = slice(P * side_tiles(b)[0], P * side_tiles(b)[0] + P * n)
                nc.gpsimd.tensor_tensor(
                    out=values(b)[:, cols, :],
                    in0=live["vf", b][:],
                    in1=bias[:, cols].unsqueeze(2).to_broadcast([P, P * n, 4]),
                    op=ALU.add,
                )
            elif kind == "quant_v":
                if ("vc", b) not in live:
                    live["vc", b] = work2.tile([P, DV], U32, name="vc", align_bytes=64)
                    live["vs", b] = work2.tile([P, DV], U8, name="vs", align_bytes=64)
                cols = group_cols(b, i)
                nc.vector.quantize_mx(
                    out=live["vc", b][:, cols].bitcast(FP8X4),
                    scales=live["vs", b][:, cols],
                    in_=live["vg", b][:, cols, :].rearrange("p c t -> p (c t)"),
                )
                live["vq", b, i] = True
            elif kind == "quant_xp":
                live["rr", b] = work4.tile([P, 4], F32, name="rr")
                nc.vector.reciprocal(out=live["rr", b][:], in_=live["rs", b][:])
                codes = work3.tile([P, 2 * S], U32, name="xpc", align_bytes=64)
                scales = work3.tile([P, 2 * S], U8, name="xps", align_bytes=64)
                first = 0 if b + 2 < B else S
                nc.vector.quantize_mx(
                    out=codes[:, first : 2 * S].bitcast(FP8X4),
                    scales=scales[:, first : 2 * S],
                    in_=stage(b)[:, 4 * first : 8 * S],
                )
                live["xc", b + 2], live["xs", b + 2] = codes[:, 0:S], scales[:, 0:S]
                live["pc", b], live["ps", b] = codes[:, S : 2 * S], scales[:, S : 2 * S]
            elif kind == "out":
                g, t = divmod(i, 4)
                if ("o", b) not in live:
                    live["o", b] = big.tile([P, 4, DV], F32, name="o", tag="big", align_bytes=64)
                dst = live["o", b][:, t, group_cols(b, g)]
                scale = live["rr", b][:, t : t + 1]
                if engine == "V":
                    nc.vector.tensor_scalar_mul(out=dst, in0=live[step][:], scalar1=scale)
                else:
                    nc.scalar.activation(out=dst, in_=live[step][:], func=ACT.Copy, scale=scale)
                rows_of = out[b].rearrange("(p i) n -> p i n", i=4)
                nc.sync.dma_start(out=rows_of[:, t, group_cols(b, g)], in_=dst)

        plan = []

        def add(kind, b, *indices, on=None):
            engine = on or ("S" if kind in ("turn", "turn_back", "bias", "x", "p", "qk", "ln", "recip", "exp", "side", "out") else "G" if kind == "side_add" else "V")
            for i in indices or (() if kind in ("side", "turn", "turn_back") else (0,)):
                if 0 <= b < B and not (kind == "value" and (i in side_tiles(b) or i in TURN.get(b, ()))):
                    plan.append((kind, engine, b, i))

        EARLY_V = 0
        add("bias", 0, 0, 1, on="V")
        add("w", 0, 0, on="V")
        add("ln", 0, 0, 1)
        add("w", 0, 1, on="V")
        add("ln", 0, 2, 3)
        add("w", 0, 2, on="V")
        add("recip", 0, 0)
        add("qk", 0, on="V")
        add("w", 0, 3, on="V")
        add("recip", 0, 1, 2, 3)
        add("quant_w", 0)
        add("scale", 0, 0, 1)
        add("x", 0, 0, on="S")
        add("max", 0, 0)
        add("x", 0, 1, on="S")
        add("max", 0, 1)
        add("exp", 0, 0, 1)
        add("quant_x", 0)
        add("bias_col", 0, on="V")
        add("scale", 0, 2, 3)
        add("qk", 1)
        add("max", 0, 2)
        add("exp", 0, 2)
        add("max", 0, 3)
        add("exp", 0, 3)
        add("x", 1, 0, 1)
        add("qk", 2)
        for c in side_tiles(0):
            add("side", 0, c)
        if side_tiles(0):
            add("side_add", 0)
        def val(b, *tiles):
            add("value", b, *[c for c in tiles if b > 0 or c >= EARLY_V])

        for n in range(B - 2):
            s, v, o = n + 1, n, n - 1
            add("out", o, 0, 1)
            add("scale", s, 0, 1)
            add("max", s, 0)
            add("exp", s, 0)
            add("out", o, 2)
            add("scale", s, 2)
            add("max", s, 1)
            add("exp", s, 1)
            add("p", v, 0)
            add("scale", s, 3)
            add("max", s, 2)
            add("exp", s, 2)
            add("p", v, 1)
            val(v, 0, 1)
            add("x", v + 2, 0)
            val(v, 2)
            add("max", s, 3)
            add("exp", s, 3)
            add("x", v + 2, 1)
            add("turn", v, *TURN.get(v, ()))
            val(v, 3)
            add("out", o, 3, 4)
            val(v, 4)
            add("out", o, 5)
            add("turn_back", v, *TURN.get(v, ()))
            val(v, 5)
            add("qk", n + 3)
            val(v, 6)
            val(v, 7)
            if n == 0:
                add("quant_x", 1)
            add("side", v + 1, *side_tiles(v + 1))
            add("out", o, 6, 7)
            add("quant_xp", v)
            add("quant_v", v, 0, 1)
            if v + 1 < B and side_tiles(v + 1):
                add("side_add", v + 1)
        a, b = B - 2, B - 1
        add("out", a - 1, 0)
        add("scale", b, 0, 1)
        add("p", a, 0)
        add("max", b, 0)
        add("exp", b, 0)
        add("scale", b, 2)
        add("out", a - 1, 1)
        add("max", b, 1)
        add("exp", b, 1)
        add("p", a, 1)
        add("scale", b, 3)
        add("max", b, 2)
        add("exp", b, 2)
        add("value", a, 0, 1)
        add("out", a - 1, 2)
        add("max", b, 3)
        add("exp", b, 3)
        add("value", a, 2, 3)
        add("out", a - 1, 3, 4)
        add("side", b, *side_tiles(b))
        if side_tiles(b):
            add("side_add", b)
        add("value", a, 4)
        add("out", a - 1, 5)
        add("value", a, 5)
        add("quant_xp", a)
        add("quant_v", a, 0)
        add("out", a - 1, 6)
        add("value", a, 6)
        add("out", a - 1, 7)
        add("value", a, 7)
        add("p", b, 0)
        add("out", a, 0)
        add("value", b, 0, 1)
        add("quant_v", a, 1)
        add("out", a, 1)
        add("p", b, 1)
        add("value", b, 2)
        add("out", a, 2)
        add("value", b, 3)
        add("out", a, 3)
        add("quant_xp", b)
        add("quant_v", b, 0)
        add("out", a, 4)
        add("value", b, 4)
        add("out", a, 5)
        add("value", b, 5)
        add("out", a, 6)
        add("value", b, 6)
        add("out", a, 7)
        add("value", b, 7)
        add("out", b, 0)
        add("out", b, 1)
        add("quant_v", b, 1)
        add("out", b, 2)
        add("out", b, 3, on="V")
        add("out", b, 4)
        add("out", b, 5, on="V")
        add("out", b, 6)
        add("out", b, 7, on="V")


        waiting = {e: [(at, s) for at, s in enumerate(plan) if s[0] in has_bank and s[1] == e] for e in ("V", "S")}
        free = {"V": 5, "S": 3}
        reach = {"V": 12, "S": 5}
        for now, step in enumerate(plan):
            while True:
                heads = [
                    (*waiting[e][0], e)
                    for e in ("V", "S")
                    if waiting[e] and free[e] and waiting[e][0][0] <= now + reach[e] and ready(waiting[e][0][1])
                ]
                if not heads:
                    break
                at, next_step, e = min(heads)
                waiting[e].pop(0)
                fill(next_step)
                free[e] -= 1
            work(step)
            if step[0] in has_bank:
                free[step[1]] += 1
